import numpy as np
import ml_dtypes


def mxq(x, axis, fmt="e4m3"):
    dtype, down = {"e4m3": (ml_dtypes.float8_e4m3fn, 7), "e5m2": (ml_dtypes.float8_e5m2, 14)}[fmt]
    v = np.moveaxis(np.asarray(x, np.float32).astype(ml_dtypes.bfloat16).astype(np.float64), axis, -1)
    blocks = v.reshape(v.shape[:-1] + (-1, 32))
    amax = np.abs(blocks).max(-1, keepdims=True)
    byte = np.maximum(np.where(amax > 0, np.frexp(amax)[1] - 1 + 127, 0) - down, 1)
    scale = np.exp2(byte - 127.0)
    codes = (blocks / scale).astype(np.float32).astype(dtype).astype(np.float64)
    return np.moveaxis((codes * scale).reshape(v.shape), -1, axis)


WIDE = False


def mx_kscale(k):
    if not WIDE:
        return np.ones(k)
    levels = np.array([10, -10, 5, -5, 0])
    a = np.random.permutation(np.resize(levels, k // 512 * 4)).reshape(k // 512, 4)
    idx = np.arange(k)
    return np.exp2(a[idx // 512, idx % 128 // 32])


BF16 = ml_dtypes.bfloat16


def bf(x):
    return np.asarray(x, np.float32).astype(BF16)


def f64(x):
    return np.asarray(x).astype(np.float64)


B, S, D, HD, DEPTH = 2, 1024, 2048, 128, 12
HD2 = 2 * HD
LAMBDA_INIT = 0.8 - 0.6 * np.exp(-0.3 * DEPTH)


def softmax(a):
    e = np.exp(a - a.max(-1, keepdims=True))
    return e / e.sum(-1, keepdims=True)


def setup_inputs():
    s = mx_kscale(D)
    ls = np.sqrt(0.5 / HD)

    def lam_vec(sign):
        return bf(sign * ls * (1.0 + 0.5 * np.random.standard_normal(HD)))

    return {"x": bf(np.random.standard_normal((B, S, D)) * s),
            "q": bf(np.random.standard_normal((B, S, HD2)) * 1.4),
            "k": bf(np.random.standard_normal((B, S, HD2)) * 1.4),
            "WV": bf(np.random.standard_normal((D, HD2)) / np.sqrt(D) / s[:, None]),
            "lambda_q1": lam_vec(1.0), "lambda_q2": lam_vec(1.0),
            "lambda_k1": lam_vec(1.0), "lambda_k2": lam_vec(-1.0)}


def reference(x, q, k, WV, lambda_q1, lambda_q2, lambda_k1, lambda_k2):
    scale = HD ** -0.5
    v = mxq(f64(x), 2, "e4m3") @ mxq(f64(WV), 0, "e4m3")
    a1 = f64(q)[..., :HD] @ f64(k)[..., :HD].transpose(0, 2, 1) * scale
    a2 = f64(q)[..., HD:] @ f64(k)[..., HD:].transpose(0, 2, 1) * scale
    lambda_1 = np.exp(np.sum(f64(lambda_q1) * f64(lambda_k1)))
    lambda_2 = np.exp(np.sum(f64(lambda_q2) * f64(lambda_k2)))
    lam = lambda_1 + lambda_2 + LAMBDA_INIT
    attn = softmax(a1) - lam * softmax(a2)
    return mxq(attn, 2, "e4m3") @ mxq(v, 1, "e4m3")

@@ -1,0 +1,301 @@
+import math
+from contextlib import ExitStack
+
+import concourse.mybir as mybir
+from concourse.masks import make_identity
+
+F32 = mybir.dt.float32
+BF16 = mybir.dt.bfloat16
+U32 = mybir.dt.uint32
+U8 = mybir.dt.uint8
+FP8X4 = mybir.dt.float8_e4m3fn_x4
+ALU = mybir.AluOpType
+ACT = mybir.ActivationFunctionType
+AXIS = mybir.AxisListType
+
+B, S, D, HD = 2, 1024, 2048, 128
+HD2 = 2 * HD
+DEPTH = 12
+LAMBDA_INIT = 0.8 - 0.6 * math.exp(-0.3 * DEPTH)
+SCALE = HD**-0.5
+
+P = 128
+PACK = 4
+K_PASS = P * PACK
+BANK = 512
+CHUNK = K_PASS
+CHUNKS_PER_BATCH = S // CHUNK
+CHUNKS = B * CHUNKS_PER_BATCH
+TILES_PER_BATCH = S // P
+QUERY_TILES = B * TILES_PER_BATCH
+D_PASSES = D // K_PASS
+KEY_BANKS = S // BANK
+
+FLOPS = 2 * B * S * D * HD2 + 2 * (2 * B * S * S * HD) + 2 * B * S * S * HD2
+
+
+def tile_differentialattention_pa_kernel(
+    tc, x, q, k, WV, lambda_q1, lambda_q2, lambda_k1, lambda_k2, out
+):
+    nc = tc.nc
+    with ExitStack() as ctx:
+        keep = ctx.enter_context(tc.tile_pool(name="keep", bufs=1))
+        work = ctx.enter_context(tc.tile_pool(name="work", bufs=3))
+        stats = ctx.enter_context(tc.tile_pool(name="stats", bufs=4))
+        score_banks = ctx.enter_context(tc.psum_pool(name="score_banks", bufs=4))
+        flip_banks = ctx.enter_context(tc.psum_pool(name="flip_banks", bufs=2))
+        mx_banks = ctx.enter_context(tc.psum_pool(name="mx_banks", bufs=2))
+
+        def load_tokens(name, source):
+            rows = keep.tile([P, CHUNKS_PER_BATCH, PACK * HD2], BF16, name=name)
+            nc.sync.dma_start(
+                out=rows[:], in_=source.rearrange("(g p j) h -> p g (j h)", g=CHUNKS_PER_BATCH, j=PACK)
+            )
+            return rows
+
+        k_rows = [None] * B
+        q_rows = [None] * B
+        k_rows[0] = load_tokens("k_rows0", k[0])
+        q_rows[0] = load_tokens("q_rows0", q[0])
+
+        wv_rows = keep.tile([P, D_PASSES, PACK, HD2], BF16)
+        nc.sync.dma_start(
+            out=wv_rows[:].rearrange("p c (u e) n -> p (c u) (e n)", e=2),
+            in_=WV.rearrange("(s p e) n -> p s (e n)", p=P, e=2),
+        )
+
+        x_flat = x.flatten_outer_dims()
+        x_rows = []
+        for g in range(CHUNKS):
+            rows = keep.tile([P, PACK * D], BF16, name="x_rows%d" % g)
+            nc.sync.dma_start(
+                out=rows[:],
+                in_=x_flat[g * CHUNK : (g + 1) * CHUNK, :].rearrange("(p j) d -> p (j d)", j=PACK),
+            )
+            x_rows.append(rows)
+        k_rows[1] = load_tokens("k_rows1", k[1])
+        q_rows[1] = load_tokens("q_rows1", q[1])
+
+        ident_bf16 = keep.tile([P, P], BF16)
+        make_identity(nc, ident_bf16[:])
+        ident_f32 = keep.tile([P, P], F32)
+        make_identity(nc, ident_f32[:])
+
+        lambda_q = keep.tile([P, 2, HD], BF16)
+        lambda_k = keep.tile([P, 2, HD], BF16)
+        nc.gpsimd.dma_start(out=lambda_q[:, 0, :], in_=lambda_q1.partition_broadcast(P))
+        nc.gpsimd.dma_start(out=lambda_k[:, 0, :], in_=lambda_k1.partition_broadcast(P))
+        nc.gpsimd.dma_start(out=lambda_q[:, 1, :], in_=lambda_q2.partition_broadcast(P))
+        nc.gpsimd.dma_start(out=lambda_k[:, 1, :], in_=lambda_k2.partition_broadcast(P))
+        lambda_products = keep.tile([P, 2, HD], F32)
+        nc.vector.tensor_tensor(out=lambda_products[:], in0=lambda_q[:], in1=lambda_k[:], op=ALU.mult)
+        lambda_dots = keep.tile([P, 2], F32)
+        nc.vector.tensor_reduce(out=lambda_dots[:], in_=lambda_products[:], axis=AXIS.X, op=ALU.add)
+        lambda_exps = keep.tile([P, 2], F32)
+        lambda_exp_sum = keep.tile([P, 1], F32)
+        nc.scalar.activation(
+            out=lambda_exps[:], in_=lambda_dots[:], func=ACT.Exp, accum_out=lambda_exp_sum[:]
+        )
+        lam = keep.tile([P, 1], F32)
+        nc.vector.tensor_scalar_add(out=lam[:], in0=lambda_exp_sum[:], scalar1=LAMBDA_INIT)
+
+        wv_grouped = keep.tile([P, D_PASSES, HD2, PACK], BF16, align_bytes=64)
+        nc.vector.tensor_copy(out=wv_grouped[:], in_=wv_rows[:].rearrange("p c t n -> p c n t"))
+        wv_codes = keep.tile([P, D_PASSES, HD2], U32, align_bytes=64)
+        wv_scales = keep.tile([P, D_PASSES, HD2], U8, align_bytes=64)
+        nc.vector.quantize_mx(
+            out=wv_codes[:].rearrange("p c n -> p (c n)").bitcast(FP8X4),
+            scales=wv_scales[:].rearrange("p c n -> p (c n)"),
+            in_=wv_grouped[:].rearrange("p c n t -> p (c n t)"),
+        )
+
+        def flip_tokens(name, rows):
+            flipped_sb = keep.tile([P, 2, S], BF16, name=name)
+            for half in range(2):
+                flipped = flip_banks.tile([P, TILES_PER_BATCH, P], BF16, tag="flip")
+                for g in range(CHUNKS_PER_BATCH):
+                    for j in range(PACK):
+                        first = j * HD2 + half * HD
+                        nc.tensor.transpose(
+                            flipped[:, g * PACK + j, :], rows[:, g, first : first + HD], ident_bf16[:]
+                        )
+                nc.scalar.copy(out=flipped_sb[:, half, :], in_=flipped[:].rearrange("p s r -> p (s r)"))
+            return flipped_sb
+
+        kT = [None] * B
+        qT = [None] * B
+
+        v_codes = [keep.tile([P, HD2], U32, name="v_codes%d" % g, align_bytes=64) for g in range(CHUNKS)]
+        v_scales = [keep.tile([P, HD2], U8, name="v_scales%d" % g, align_bytes=64) for g in range(CHUNKS)]
+
+        def project_values(g):
+            x_words = x_rows[g][:].bitcast(F32)
+            x_codes = work.tile([P, PACK, D_PASSES * P], U32, align_bytes=64, bufs=2)
+            x_scales = work.tile([P, PACK, D_PASSES * P], U8, align_bytes=64, bufs=2)
+            for j in range(PACK):
+                x_grouped = work.tile([P, D_PASSES * P * PACK], BF16, align_bytes=64)
+                grouped_words = x_grouped[:].bitcast(F32).rearrange("p (c r u) -> p c r u", c=D_PASSES, u=2)
+                for pair in range(D_PASSES // 2):
+                    flipped = flip_banks.tile([P, 2, 2, P], F32, tag="flip")
+                    for c in range(2):
+                        for u in range(2):
+                            first = j * (D // 2) + (2 * pair + c) * (K_PASS // 2) + u * P
+                            nc.tensor.transpose(
+                                flipped[:, c, u, :], x_words[:, first : first + P], ident_f32[:]
+                            )
+                    nc.scalar.copy(
+                        out=grouped_words[:, 2 * pair : 2 * pair + 2, :, :],
+                        in_=flipped[:].rearrange("p c u r -> p c r u"),
+                    )
+                nc.vector.quantize_mx(
+                    out=x_codes[:, j, :].bitcast(FP8X4), scales=x_scales[:, j, :], in_=x_grouped[:]
+                )
+            v_grouped = work.tile([P, HD2, PACK], BF16, align_bytes=64)
+            for half in range(2):
+                v_sums = mx_banks.tile([P, PACK, HD], F32, tag="mx")
+                for j in range(PACK):
+                    for c in range(D_PASSES):
+                        tokens = slice(c * P, (c + 1) * P)
+                        columns = slice(half * HD, (half + 1) * HD)
+                        nc.tensor.matmul_mx(
+                            out=v_sums[:, j, :],
+                            lhsT=x_codes[:, j, tokens].bitcast(FP8X4),
+                            lhsT_scale=x_scales[:, j, tokens],
+                            rhs=wv_codes[:, c, columns].bitcast(FP8X4),
+                            rhs_scale=wv_scales[:, c, columns],
+                            start=(c == 0),
+                            stop=(c == D_PASSES - 1),
+                        )
+                nc.scalar.copy(
+                    out=v_grouped[:, half * HD : (half + 1) * HD, :],
+                    in_=v_sums[:].rearrange("p j n -> p n j"),
+                )
+            nc.vector.quantize_mx(
+                out=v_codes[g][:].bitcast(FP8X4),
+                scales=v_scales[g][:],
+                in_=v_grouped[:].rearrange("p n j -> p (n j)"),
+            )
+
+        exponentials = {}
+        exp_sums = {}
+        attn_grouped = {}
+
+        def scores_and_exponentials(i):
+            b, tile_in_batch = divmod(i, TILES_PER_BATCH)
+            queries = slice(tile_in_batch * P, (tile_in_batch + 1) * P)
+            expo = work.tile([P, 2, S], F32)
+            sums = stats.tile([P, 2 * KEY_BANKS], F32)
+            peaks = stats.tile([P, 2 * KEY_BANKS], F32)
+            shift = stats.tile([P, 2], F32)
+            for half in range(2):
+                banks = []
+                for c in range(KEY_BANKS):
+                    scores = score_banks.tile([P, BANK], F32)
+                    nc.tensor.matmul(
+                        scores[:],
+                        lhsT=qT[b][:, half, queries],
+                        rhs=kT[b][:, half, c * BANK : (c + 1) * BANK],
+                        start=True,
+                        stop=True,
+                    )
+                    col = half * KEY_BANKS + c
+                    nc.vector.tensor_reduce(out=peaks[:, col : col + 1], in_=scores[:], axis=AXIS.X, op=ALU.max)
+                    banks.append(scores)
+                first = half * KEY_BANKS
+                nc.vector.tensor_scalar(
+                    out=shift[:, half : half + 1],
+                    in0=peaks[:, first : first + 1],
+                    scalar1=peaks[:, first + 1 : first + 2],
+                    scalar2=-SCALE,
+                    op0=ALU.max,
+                    op1=ALU.mult,
+                )
+                for c in range(KEY_BANKS):
+                    col = half * KEY_BANKS + c
+                    nc.scalar.activation(
+                        out=expo[:, half, c * BANK : (c + 1) * BANK],
+                        in_=banks[c][:],
+                        func=ACT.Exp,
+                        bias=shift[:, half : half + 1],
+                        scale=SCALE,
+                        accum_out=sums[:, col : col + 1],
+                    )
+            exponentials[i] = expo
+            exp_sums[i] = sums
+
+        def difference_and_flip(i):
+            expo = exponentials[i]
+            totals = stats.tile([P, 2], F32)
+            nc.vector.tensor_reduce(
+                out=totals[:],
+                in_=exp_sums[i][:].rearrange("p (h c) -> p h c", c=KEY_BANKS),
+                axis=AXIS.X,
+                op=ALU.add,
+            )
+            inverse = stats.tile([P, 2], F32)
+            nc.vector.reciprocal(out=inverse[:], in_=totals[:])
+            nc.vector.tensor_scalar(
+                out=expo[:, 1, :],
+                in0=expo[:, 1, :],
+                scalar1=inverse[:, 1:2],
+                scalar2=lam[:, 0:1],
+                op0=ALU.mult,
+                op1=ALU.mult,
+            )
+            attn = work.tile([P, S], BF16)
+            nc.vector.scalar_tensor_tensor(
+                out=attn[:],
+                in0=expo[:, 0, :],
+                scalar=inverse[:, 0:1],
+                in1=expo[:, 1, :],
+                op0=ALU.mult,
+                op1=ALU.subtract,
+            )
+            flipped = flip_banks.tile([P, TILES_PER_BATCH, P], BF16, tag="flip")
+            for s in range(TILES_PER_BATCH):
+                nc.tensor.transpose(flipped[:, s, :], attn[:, s * P : (s + 1) * P], ident_bf16[:])
+            grouped = work.tile([P, CHUNKS_PER_BATCH, P, PACK], BF16, align_bytes=64)
+            nc.scalar.copy(out=grouped[:], in_=flipped[:].rearrange("p (g j) r -> p g r j", j=PACK))
+            attn_grouped[i] = grouped
+
+        def quantise_and_multiply(i):
+            b, tile_in_batch = divmod(i, TILES_PER_BATCH)
+            attn_codes = work.tile([P, CHUNKS_PER_BATCH, P], U32, align_bytes=64)
+            attn_scales = work.tile([P, CHUNKS_PER_BATCH, P], U8, align_bytes=64)
+            nc.vector.quantize_mx(
+                out=attn_codes[:].rearrange("p g r -> p (g r)").bitcast(FP8X4),
+                scales=attn_scales[:].rearrange("p g r -> p (g r)"),
+                in_=attn_grouped[i][:].rearrange("p g r j -> p (g r j)"),
+            )
+            out_sums = mx_banks.tile([P, HD2], F32, tag="mx")
+            for g in range(CHUNKS_PER_BATCH):
+                nc.tensor.matmul_mx(
+                    out=out_sums[:],
+                    lhsT=attn_codes[:, g, :].bitcast(FP8X4),
+                    lhsT_scale=attn_scales[:, g, :],
+                    rhs=v_codes[b * CHUNKS_PER_BATCH + g][:].bitcast(FP8X4),
+                    rhs_scale=v_scales[b * CHUNKS_PER_BATCH + g][:],
+                    start=(g == 0),
+                    stop=(g == CHUNKS_PER_BATCH - 1),
+                )
+            out_rows = work.tile([P, HD2], F32)
+            nc.scalar.copy(out=out_rows[:], in_=out_sums[:])
+            g, j = divmod(tile_in_batch, PACK)
+            nc.sync.dma_start(
+                out=out[b].rearrange("(g p j) n -> g j p n", g=CHUNKS_PER_BATCH, j=PACK)[g, j], in_=out_rows[:]
+            )
+
+        kT[0] = flip_tokens("kT0", k_rows[0])
+        qT[0] = flip_tokens("qT0", q_rows[0])
+        for step in range(QUERY_TILES + 2):
+            if step < QUERY_TILES:
+                scores_and_exponentials(step)
+            if 1 <= step <= QUERY_TILES:
+                difference_and_flip(step - 1)
+            if step >= 2:
+                quantise_and_multiply(step - 2)
+            if step < CHUNKS:
+                project_values(step)
+            if step == CHUNKS:
+                kT[1] = flip_tokens("kT1", k_rows[1])
+                qT[1] = flip_tokens("qT1", q_rows[1])

@@ -28,8 +28,12 @@ CHUNKS_PER_BATCH = S // CHUNK
 CHUNKS = B * CHUNKS_PER_BATCH
 TILES_PER_BATCH = S // P
 QUERY_TILES = B * TILES_PER_BATCH
+X_TILES = CHUNKS * PACK
 D_PASSES = D // K_PASS
 KEY_BANKS = S // BANK
+
+X_TILES_PER_STEP = 2
+FINISHES_PER_STEP = 2
 
 FLOPS = 2 * B * S * D * HD2 + 2 * (2 * B * S * S * HD) + 2 * B * S * S * HD2
 
@@ -39,24 +43,30 @@ def tile_differentialattention_pa_kernel(
 ):
     nc = tc.nc
     with ExitStack() as ctx:
+        ctx.enter_context(tc.manual_schedule())
         keep = ctx.enter_context(tc.tile_pool(name="keep", bufs=1))
         work = ctx.enter_context(tc.tile_pool(name="work", bufs=3))
         stats = ctx.enter_context(tc.tile_pool(name="stats", bufs=4))
-        score_banks = ctx.enter_context(tc.psum_pool(name="score_banks", bufs=4))
+        score_banks = ctx.enter_context(tc.psum_pool(name="score_banks", bufs=2 * KEY_BANKS))
         flip_banks = ctx.enter_context(tc.psum_pool(name="flip_banks", bufs=2))
         mx_banks = ctx.enter_context(tc.psum_pool(name="mx_banks", bufs=2))
 
-        def load_tokens(name, source):
-            rows = keep.tile([P, CHUNKS_PER_BATCH, PACK * HD2], BF16, name=name)
-            nc.sync.dma_start(
-                out=rows[:], in_=source.rearrange("(g p j) h -> p g (j h)", g=CHUNKS_PER_BATCH, j=PACK)
-            )
+        lambda_q = keep.tile([P, 2, HD], BF16)
+        lambda_k = keep.tile([P, 2, HD], BF16)
+        nc.scalar.dma_start(out=lambda_q[:, 0, :], in_=lambda_q1.partition_broadcast(P))
+        nc.scalar.dma_start(out=lambda_k[:, 0, :], in_=lambda_k1.partition_broadcast(P))
+        nc.scalar.dma_start(out=lambda_q[:, 1, :], in_=lambda_q2.partition_broadcast(P))
+        nc.scalar.dma_start(out=lambda_k[:, 1, :], in_=lambda_k2.partition_broadcast(P))
+
+        def load_tokens(name, tiled_source):
+            rows = keep.tile([P, TILES_PER_BATCH, HD2], BF16, name=name)
+            nc.sync.dma_start(out=rows[:], in_=tiled_source)
             return rows
 
         k_rows = [None] * B
         q_rows = [None] * B
-        k_rows[0] = load_tokens("k_rows0", k[0])
-        q_rows[0] = load_tokens("q_rows0", q[0])
+        k_rows[0] = load_tokens("k_rows0", k[0].rearrange("(s p) h -> p s h", p=P))
+        q_rows[0] = load_tokens("q_rows0", q[0].rearrange("(p s) h -> p s h", p=P))
 
         wv_rows = keep.tile([P, D_PASSES, PACK, HD2], BF16)
         nc.sync.dma_start(
@@ -68,140 +78,168 @@ def tile_differentialattention_pa_kernel(
         x_rows = []
         for g in range(CHUNKS):
             rows = keep.tile([P, PACK * D], BF16, name="x_rows%d" % g)
-            nc.sync.dma_start(
-                out=rows[:],
-                in_=x_flat[g * CHUNK : (g + 1) * CHUNK, :].rearrange("(p j) d -> p (j d)", j=PACK),
-            )
+            for u in range(2):
+                first = g * CHUNK + u * (CHUNK // 2)
+                nc.sync.dma_start(
+                    out=rows[:, u * 2 * D : (u + 1) * 2 * D],
+                    in_=x_flat[first : first + CHUNK // 2, :].rearrange("(p e) d -> p (e d)", e=2),
+                )
             x_rows.append(rows)
-        k_rows[1] = load_tokens("k_rows1", k[1])
-        q_rows[1] = load_tokens("q_rows1", q[1])
+        k_rows[1] = load_tokens("k_rows1", k[1].rearrange("(s p) h -> p s h", p=P))
+        q_rows[1] = load_tokens("q_rows1", q[1].rearrange("(p s) h -> p s h", p=P))
 
         ident_bf16 = keep.tile([P, P], BF16)
         make_identity(nc, ident_bf16[:])
         ident_f32 = keep.tile([P, P], F32)
         make_identity(nc, ident_f32[:])
 
-        lambda_q = keep.tile([P, 2, HD], BF16)
-        lambda_k = keep.tile([P, 2, HD], BF16)
-        nc.gpsimd.dma_start(out=lambda_q[:, 0, :], in_=lambda_q1.partition_broadcast(P))
-        nc.gpsimd.dma_start(out=lambda_k[:, 0, :], in_=lambda_k1.partition_broadcast(P))
-        nc.gpsimd.dma_start(out=lambda_q[:, 1, :], in_=lambda_q2.partition_broadcast(P))
-        nc.gpsimd.dma_start(out=lambda_k[:, 1, :], in_=lambda_k2.partition_broadcast(P))
-        lambda_products = keep.tile([P, 2, HD], F32)
-        nc.vector.tensor_tensor(out=lambda_products[:], in0=lambda_q[:], in1=lambda_k[:], op=ALU.mult)
-        lambda_dots = keep.tile([P, 2], F32)
-        nc.vector.tensor_reduce(out=lambda_dots[:], in_=lambda_products[:], axis=AXIS.X, op=ALU.add)
-        lambda_exps = keep.tile([P, 2], F32)
-        lambda_exp_sum = keep.tile([P, 1], F32)
-        nc.scalar.activation(
-            out=lambda_exps[:], in_=lambda_dots[:], func=ACT.Exp, accum_out=lambda_exp_sum[:]
-        )
-        lam = keep.tile([P, 1], F32)
-        nc.vector.tensor_scalar_add(out=lam[:], in0=lambda_exp_sum[:], scalar1=LAMBDA_INIT)
-
-        wv_grouped = keep.tile([P, D_PASSES, HD2, PACK], BF16, align_bytes=64)
-        nc.vector.tensor_copy(out=wv_grouped[:], in_=wv_rows[:].rearrange("p c t n -> p c n t"))
-        wv_codes = keep.tile([P, D_PASSES, HD2], U32, align_bytes=64)
-        wv_scales = keep.tile([P, D_PASSES, HD2], U8, align_bytes=64)
-        nc.vector.quantize_mx(
-            out=wv_codes[:].rearrange("p c n -> p (c n)").bitcast(FP8X4),
-            scales=wv_scales[:].rearrange("p c n -> p (c n)"),
-            in_=wv_grouped[:].rearrange("p c n t -> p (c n t)"),
-        )
-
         def flip_tokens(name, rows):
             flipped_sb = keep.tile([P, 2, S], BF16, name=name)
             for half in range(2):
                 flipped = flip_banks.tile([P, TILES_PER_BATCH, P], BF16, tag="flip")
-                for g in range(CHUNKS_PER_BATCH):
-                    for j in range(PACK):
-                        first = j * HD2 + half * HD
-                        nc.tensor.transpose(
-                            flipped[:, g * PACK + j, :], rows[:, g, first : first + HD], ident_bf16[:]
-                        )
-                nc.scalar.copy(out=flipped_sb[:, half, :], in_=flipped[:].rearrange("p s r -> p (s r)"))
+                for s in range(TILES_PER_BATCH):
+                    nc.tensor.transpose(
+                        flipped[:, s, :], rows[:, s, half * HD : (half + 1) * HD], ident_bf16[:]
+                    )
+                copy = nc.vector.tensor_copy if half == 0 else nc.scalar.copy
+                copy(out=flipped_sb[:, half, :], in_=flipped[:].rearrange("p s r -> p (s r)"))
             return flipped_sb
 
         kT = [None] * B
         qT = [None] * B
 
+        lam = keep.tile([P, 1], F32)
+
+        def compute_lam():
+            products = keep.tile([P, 2, HD], F32)
+            nc.vector.tensor_tensor(out=products[:], in0=lambda_q[:], in1=lambda_k[:], op=ALU.mult)
+            dots = keep.tile([P, 2], F32)
+            nc.vector.tensor_reduce(out=dots[:], in_=products[:], axis=AXIS.X, op=ALU.add)
+            exps = keep.tile([P, 2], F32)
+            exp_sum = keep.tile([P, 1], F32)
+            nc.scalar.activation(out=exps[:], in_=dots[:], func=ACT.Exp, accum_out=exp_sum[:])
+            nc.vector.tensor_scalar_add(out=lam[:], in0=exp_sum[:], scalar1=LAMBDA_INIT)
+
+        wv_codes = keep.tile([P, D_PASSES, HD2], U32, align_bytes=64)
+        wv_scales = keep.tile([P, D_PASSES, HD2], U8, align_bytes=64)
+
+        def quantise_wv():
+            grouped = keep.tile([P, D_PASSES, HD2, PACK], BF16, align_bytes=64, name="wv_grouped")
+            nc.vector.tensor_copy(out=grouped[:], in_=wv_rows[:].rearrange("p c t n -> p c n t"))
+            nc.vector.quantize_mx(
+                out=wv_codes[:].rearrange("p c n -> p (c n)").bitcast(FP8X4),
+                scales=wv_scales[:].rearrange("p c n -> p (c n)"),
+                in_=grouped[:].rearrange("p c n t -> p (c n t)"),
+            )
+
+        x_flipped = {}
+        x_grouped = {}
+        x_codes = {}
+        x_scales = {}
+        v_sums = {}
         v_codes = [keep.tile([P, HD2], U32, name="v_codes%d" % g, align_bytes=64) for g in range(CHUNKS)]
         v_scales = [keep.tile([P, HD2], U8, name="v_scales%d" % g, align_bytes=64) for g in range(CHUNKS)]
 
-        def project_values(g):
-            x_words = x_rows[g][:].bitcast(F32)
-            x_codes = work.tile([P, PACK, D_PASSES * P], U32, align_bytes=64, bufs=2)
-            x_scales = work.tile([P, PACK, D_PASSES * P], U8, align_bytes=64, bufs=2)
-            for j in range(PACK):
-                x_grouped = work.tile([P, D_PASSES * P * PACK], BF16, align_bytes=64)
-                grouped_words = x_grouped[:].bitcast(F32).rearrange("p (c r u) -> p c r u", c=D_PASSES, u=2)
-                for pair in range(D_PASSES // 2):
-                    flipped = flip_banks.tile([P, 2, 2, P], F32, tag="flip")
-                    for c in range(2):
-                        for u in range(2):
-                            first = j * (D // 2) + (2 * pair + c) * (K_PASS // 2) + u * P
-                            nc.tensor.transpose(
-                                flipped[:, c, u, :], x_words[:, first : first + P], ident_f32[:]
-                            )
-                    nc.scalar.copy(
-                        out=grouped_words[:, 2 * pair : 2 * pair + 2, :, :],
-                        in_=flipped[:].rearrange("p c u r -> p c r u"),
-                    )
-                nc.vector.quantize_mx(
-                    out=x_codes[:, j, :].bitcast(FP8X4), scales=x_scales[:, j, :], in_=x_grouped[:]
+        def transpose_x(tile):
+            g, t = divmod(tile, PACK)
+            words = x_rows[g][:].bitcast(F32)
+            x_flipped[tile] = []
+            for pair in range(D_PASSES // 2):
+                flipped = flip_banks.tile([P, 2, 2, P], F32, tag="flip")
+                for c in range(2):
+                    for u in range(2):
+                        first = t * (D // 2) + (2 * pair + c) * (K_PASS // 2) + u * P
+                        nc.tensor.transpose(flipped[:, c, u, :], words[:, first : first + P], ident_f32[:])
+                x_flipped[tile].append(flipped)
+
+        def group_x(tile):
+            grouped = work.tile([P, D_PASSES * P * PACK], BF16, align_bytes=64, name="x_grouped")
+            grouped_words = grouped[:].bitcast(F32).rearrange("p (c r u) -> p c r u", c=D_PASSES, u=2)
+            for pair in range(D_PASSES // 2):
+                nc.scalar.copy(
+                    out=grouped_words[:, 2 * pair : 2 * pair + 2, :, :],
+                    in_=x_flipped[tile][pair][:].rearrange("p c u r -> p c r u"),
                 )
-            v_grouped = work.tile([P, HD2, PACK], BF16, align_bytes=64)
+            x_grouped[tile] = grouped
+
+        def quantise_x(tile):
+            g, t = divmod(tile, PACK)
+            if t == 0:
+                x_codes[g] = work.tile([P, PACK, D_PASSES * P], U32, align_bytes=64, bufs=2, name="x_codes")
+                x_scales[g] = work.tile([P, PACK, D_PASSES * P], U8, align_bytes=64, bufs=2, name="x_scales")
+            nc.vector.quantize_mx(
+                out=x_codes[g][:, t, :].bitcast(FP8X4), scales=x_scales[g][:, t, :], in_=x_grouped[tile][:]
+            )
+
+        def project_chunk(g):
+            v_sums[g] = []
             for half in range(2):
-                v_sums = mx_banks.tile([P, PACK, HD], F32, tag="mx")
-                for j in range(PACK):
+                sums = mx_banks.tile([P, PACK, HD], F32, tag="mx")
+                for t in range(PACK):
                     for c in range(D_PASSES):
                         tokens = slice(c * P, (c + 1) * P)
                         columns = slice(half * HD, (half + 1) * HD)
                         nc.tensor.matmul_mx(
-                            out=v_sums[:, j, :],
-                            lhsT=x_codes[:, j, tokens].bitcast(FP8X4),
-                            lhsT_scale=x_scales[:, j, tokens],
+                            out=sums[:, t, :],
+                            lhsT=x_codes[g][:, t, tokens].bitcast(FP8X4),
+                            lhsT_scale=x_scales[g][:, t, tokens],
                             rhs=wv_codes[:, c, columns].bitcast(FP8X4),
                             rhs_scale=wv_scales[:, c, columns],
                             start=(c == 0),
                             stop=(c == D_PASSES - 1),
                         )
+                v_sums[g].append(sums)
+
+        v_grouped = {}
+
+        def group_v(g):
+            grouped = work.tile([P, HD2, PACK], BF16, align_bytes=64, name="v_grouped")
+            for half in range(2):
                 nc.scalar.copy(
-                    out=v_grouped[:, half * HD : (half + 1) * HD, :],
-                    in_=v_sums[:].rearrange("p j n -> p n j"),
+                    out=grouped[:, half * HD : (half + 1) * HD, :],
+                    in_=v_sums[g][half][:].rearrange("p t n -> p n t"),
                 )
+            v_grouped[g] = grouped
+
+        def quantise_v(g):
             nc.vector.quantize_mx(
                 out=v_codes[g][:].bitcast(FP8X4),
                 scales=v_scales[g][:],
-                in_=v_grouped[:].rearrange("p n j -> p (n j)"),
+                in_=v_grouped[g][:].rearrange("p n t -> p (n t)"),
             )
 
+        scores = {}
         exponentials = {}
         exp_sums = {}
         attn_grouped = {}
+        attn_codes = {}
+        attn_scales = {}
 
-        def scores_and_exponentials(i):
+        def multiply_q_k(i):
             b, tile_in_batch = divmod(i, TILES_PER_BATCH)
             queries = slice(tile_in_batch * P, (tile_in_batch + 1) * P)
-            expo = work.tile([P, 2, S], F32)
-            sums = stats.tile([P, 2 * KEY_BANKS], F32)
-            peaks = stats.tile([P, 2 * KEY_BANKS], F32)
-            shift = stats.tile([P, 2], F32)
+            scores[i] = []
             for half in range(2):
-                banks = []
                 for c in range(KEY_BANKS):
-                    scores = score_banks.tile([P, BANK], F32)
+                    bank = score_banks.tile([P, BANK], F32, tag="scores")
                     nc.tensor.matmul(
-                        scores[:],
+                        bank[:],
                         lhsT=qT[b][:, half, queries],
                         rhs=kT[b][:, half, c * BANK : (c + 1) * BANK],
                         start=True,
                         stop=True,
                     )
-                    col = half * KEY_BANKS + c
-                    nc.vector.tensor_reduce(out=peaks[:, col : col + 1], in_=scores[:], axis=AXIS.X, op=ALU.max)
-                    banks.append(scores)
+                    scores[i].append(bank)
+
+        def exponentiate(i):
+            expo = work.tile([P, 2, S], F32)
+            sums = stats.tile([P, 2 * KEY_BANKS], F32)
+            peaks = stats.tile([P, 2 * KEY_BANKS], F32)
+            shift = stats.tile([P, 2], F32)
+            for half in range(2):
                 first = half * KEY_BANKS
+                for c in range(first, first + KEY_BANKS):
+                    nc.vector.tensor_reduce(out=peaks[:, c : c + 1], in_=scores[i][c][:], axis=AXIS.X, op=ALU.max)
                 nc.vector.tensor_scalar(
                     out=shift[:, half : half + 1],
                     in0=peaks[:, first : first + 1],
@@ -211,19 +249,18 @@ def tile_differentialattention_pa_kernel(
                     op1=ALU.mult,
                 )
                 for c in range(KEY_BANKS):
-                    col = half * KEY_BANKS + c
                     nc.scalar.activation(
                         out=expo[:, half, c * BANK : (c + 1) * BANK],
-                        in_=banks[c][:],
+                        in_=scores[i][first + c][:],
                         func=ACT.Exp,
                         bias=shift[:, half : half + 1],
                         scale=SCALE,
-                        accum_out=sums[:, col : col + 1],
+                        accum_out=sums[:, first + c : first + c + 1],
                     )
             exponentials[i] = expo
             exp_sums[i] = sums
 
-        def difference_and_flip(i):
+        def difference(i):
             expo = exponentials[i]
             totals = stats.tile([P, 2], F32)
             nc.vector.tensor_reduce(
@@ -251,28 +288,36 @@ def tile_differentialattention_pa_kernel(
                 op0=ALU.mult,
                 op1=ALU.subtract,
             )
-            flipped = flip_banks.tile([P, TILES_PER_BATCH, P], BF16, tag="flip")
-            for s in range(TILES_PER_BATCH):
-                nc.tensor.transpose(flipped[:, s, :], attn[:, s * P : (s + 1) * P], ident_bf16[:])
-            grouped = work.tile([P, CHUNKS_PER_BATCH, P, PACK], BF16, align_bytes=64)
-            nc.scalar.copy(out=grouped[:], in_=flipped[:].rearrange("p (g j) r -> p g r j", j=PACK))
+            attn_words = attn[:].bitcast(F32)
+            flipped = flip_banks.tile([P, CHUNKS_PER_BATCH, 2, P], F32, tag="flip")
+            for g in range(CHUNKS_PER_BATCH):
+                for u in range(2):
+                    first = (2 * g + u) * P
+                    nc.tensor.transpose(flipped[:, g, u, :], attn_words[:, first : first + P], ident_f32[:])
+            grouped = work.tile([P, S], BF16, align_bytes=64, name="attn_grouped")
+            nc.scalar.copy(
+                out=grouped[:].bitcast(F32).rearrange("p (g r u) -> p g r u", g=CHUNKS_PER_BATCH, u=2),
+                in_=flipped[:].rearrange("p g u r -> p g r u"),
+            )
             attn_grouped[i] = grouped
 
-        def quantise_and_multiply(i):
-            b, tile_in_batch = divmod(i, TILES_PER_BATCH)
-            attn_codes = work.tile([P, CHUNKS_PER_BATCH, P], U32, align_bytes=64)
-            attn_scales = work.tile([P, CHUNKS_PER_BATCH, P], U8, align_bytes=64)
+        def quantise_attn(i):
+            attn_codes[i] = work.tile([P, CHUNKS_PER_BATCH, P], U32, align_bytes=64, bufs=6, name="attn_codes")
+            attn_scales[i] = work.tile([P, CHUNKS_PER_BATCH, P], U8, align_bytes=64, bufs=6, name="attn_scales")
             nc.vector.quantize_mx(
-                out=attn_codes[:].rearrange("p g r -> p (g r)").bitcast(FP8X4),
-                scales=attn_scales[:].rearrange("p g r -> p (g r)"),
-                in_=attn_grouped[i][:].rearrange("p g r j -> p (g r j)"),
+                out=attn_codes[i][:].rearrange("p g r -> p (g r)").bitcast(FP8X4),
+                scales=attn_scales[i][:].rearrange("p g r -> p (g r)"),
+                in_=attn_grouped[i][:],
             )
+
+        def multiply_attn_v(i):
+            b, tile_in_batch = divmod(i, TILES_PER_BATCH)
             out_sums = mx_banks.tile([P, HD2], F32, tag="mx")
             for g in range(CHUNKS_PER_BATCH):
                 nc.tensor.matmul_mx(
                     out=out_sums[:],
-                    lhsT=attn_codes[:, g, :].bitcast(FP8X4),
-                    lhsT_scale=attn_scales[:, g, :],
+                    lhsT=attn_codes[i][:, g, :].bitcast(FP8X4),
+                    lhsT_scale=attn_scales[i][:, g, :],
                     rhs=v_codes[b * CHUNKS_PER_BATCH + g][:].bitcast(FP8X4),
                     rhs_scale=v_scales[b * CHUNKS_PER_BATCH + g][:],
                     start=(g == 0),
@@ -280,22 +325,51 @@ def tile_differentialattention_pa_kernel(
                 )
             out_rows = work.tile([P, HD2], F32)
             nc.scalar.copy(out=out_rows[:], in_=out_sums[:])
-            g, j = divmod(tile_in_batch, PACK)
-            nc.sync.dma_start(
-                out=out[b].rearrange("(g p j) n -> g j p n", g=CHUNKS_PER_BATCH, j=PACK)[g, j], in_=out_rows[:]
-            )
+            nc.sync.dma_start(out=out[b].rearrange("(p s) n -> s p n", p=P)[tile_in_batch], in_=out_rows[:])
 
         kT[0] = flip_tokens("kT0", k_rows[0])
         qT[0] = flip_tokens("qT0", q_rows[0])
+        compute_lam()
+        multiply_q_k(0)
+        chunks_ready = 0
+        finished = 0
         for step in range(QUERY_TILES + 2):
+            first_new = step * X_TILES_PER_STEP
+            new_x_tiles = [t for t in range(first_new, first_new + X_TILES_PER_STEP) if t < X_TILES]
+            grouped_x_tiles = [t for t in range(first_new - X_TILES_PER_STEP, first_new) if 0 <= t < X_TILES]
+            projected = [g for g in v_sums if g >= chunks_ready]
+
+            for t in new_x_tiles[:1]:
+                transpose_x(t)
+            if step + 1 < QUERY_TILES:
+                multiply_q_k(step + 1)
             if step < QUERY_TILES:
-                scores_and_exponentials(step)
+                exponentiate(step)
+            for g in projected:
+                group_v(g)
+            for t in new_x_tiles[:1]:
+                group_x(t)
+            for t in new_x_tiles[1:]:
+                transpose_x(t)
+                group_x(t)
             if 1 <= step <= QUERY_TILES:
-                difference_and_flip(step - 1)
-            if step >= 2:
-                quantise_and_multiply(step - 2)
-            if step < CHUNKS:
-                project_values(step)
-            if step == CHUNKS:
+                difference(step - 1)
+            if 2 <= step:
+                quantise_attn(step - 2)
+            if step == 0:
+                quantise_wv()
+            for t in grouped_x_tiles:
+                quantise_x(t)
+            for g in projected:
+                quantise_v(g)
+                chunks_ready += 1
+            for turn in range(FINISHES_PER_STEP):
+                if finished <= step - 2 and chunks_ready >= (finished // TILES_PER_BATCH + 1) * CHUNKS_PER_BATCH:
+                    multiply_attn_v(finished)
+                    finished += 1
+            for t in grouped_x_tiles:
+                if t % PACK == PACK - 1:
+                    project_chunk(t // PACK)
+            if step == TILES_PER_BATCH - 2:
                 kT[1] = flip_tokens("kT1", k_rows[1])
                 qT[1] = flip_tokens("qT1", q_rows[1])

@@ -48,8 +48,7 @@ def tile_differentialattention_pa_kernel(
         work = ctx.enter_context(tc.tile_pool(name="work", bufs=3))
         stats = ctx.enter_context(tc.tile_pool(name="stats", bufs=4))
         score_banks = ctx.enter_context(tc.psum_pool(name="score_banks", bufs=2 * KEY_BANKS))
-        flip_banks = ctx.enter_context(tc.psum_pool(name="flip_banks", bufs=2))
-        mx_banks = ctx.enter_context(tc.psum_pool(name="mx_banks", bufs=2))
+        spare_banks = ctx.enter_context(tc.psum_pool(name="spare_banks", bufs=4))
 
         lambda_q = keep.tile([P, 2, HD], BF16)
         lambda_k = keep.tile([P, 2, HD], BF16)
@@ -63,46 +62,52 @@ def tile_differentialattention_pa_kernel(
             nc.sync.dma_start(out=rows[:], in_=tiled_source)
             return rows
 
+        def load_x(rows, g, u):
+            first = g * CHUNK + u * (CHUNK // 2)
+            nc.sync.dma_start(
+                out=rows[:, u * 2 * D : (u + 1) * 2 * D],
+                in_=x_flat[first : first + CHUNK // 2, :].rearrange("(p e) d -> p (e d)", e=2),
+            )
+
+        x_flat = x.flatten_outer_dims()
+        x_rows = [keep.tile([P, PACK * D], BF16, name="x_rows%d" % g) for g in range(CHUNKS)]
+        wv_rows = keep.tile([P, D_PASSES, PACK, HD2], BF16)
         k_rows = [None] * B
         q_rows = [None] * B
         k_rows[0] = load_tokens("k_rows0", k[0].rearrange("(s p) h -> p s h", p=P))
         q_rows[0] = load_tokens("q_rows0", q[0].rearrange("(p s) h -> p s h", p=P))
-
-        wv_rows = keep.tile([P, D_PASSES, PACK, HD2], BF16)
+        load_x(x_rows[0], 0, 0)
+        k_rows[1] = load_tokens("k_rows1", k[1].rearrange("(s p) h -> p s h", p=P))
+        q_rows[1] = load_tokens("q_rows1", q[1].rearrange("(p s) h -> p s h", p=P))
         nc.sync.dma_start(
             out=wv_rows[:].rearrange("p c (u e) n -> p (c u) (e n)", e=2),
             in_=WV.rearrange("(s p e) n -> p s (e n)", p=P, e=2),
         )
-
-        x_flat = x.flatten_outer_dims()
-        x_rows = []
-        for g in range(CHUNKS):
-            rows = keep.tile([P, PACK * D], BF16, name="x_rows%d" % g)
+        load_x(x_rows[0], 0, 1)
+        for g in range(1, CHUNKS):
             for u in range(2):
-                first = g * CHUNK + u * (CHUNK // 2)
-                nc.sync.dma_start(
-                    out=rows[:, u * 2 * D : (u + 1) * 2 * D],
-                    in_=x_flat[first : first + CHUNK // 2, :].rearrange("(p e) d -> p (e d)", e=2),
-                )
-            x_rows.append(rows)
-        k_rows[1] = load_tokens("k_rows1", k[1].rearrange("(s p) h -> p s h", p=P))
-        q_rows[1] = load_tokens("q_rows1", q[1].rearrange("(p s) h -> p s h", p=P))
+                load_x(x_rows[g], g, u)
 
         ident_bf16 = keep.tile([P, P], BF16)
         make_identity(nc, ident_bf16[:])
         ident_f32 = keep.tile([P, P], F32)
         make_identity(nc, ident_f32[:])
 
-        def flip_tokens(name, rows):
-            flipped_sb = keep.tile([P, 2, S], BF16, name=name)
+        def transpose_tokens(rows):
+            banks = []
             for half in range(2):
-                flipped = flip_banks.tile([P, TILES_PER_BATCH, P], BF16, tag="flip")
+                flipped = spare_banks.tile([P, TILES_PER_BATCH, P], BF16, tag="spare")
                 for s in range(TILES_PER_BATCH):
                     nc.tensor.transpose(
                         flipped[:, s, :], rows[:, s, half * HD : (half + 1) * HD], ident_bf16[:]
                     )
-                copy = nc.vector.tensor_copy if half == 0 else nc.scalar.copy
-                copy(out=flipped_sb[:, half, :], in_=flipped[:].rearrange("p s r -> p (s r)"))
+                banks.append(flipped)
+            return banks
+
+        def keep_tokens(name, banks):
+            flipped_sb = keep.tile([P, 2, S], BF16, name=name)
+            nc.vector.tensor_copy(out=flipped_sb[:, 0, :], in_=banks[0][:].rearrange("p s r -> p (s r)"))
+            nc.scalar.copy(out=flipped_sb[:, 1, :], in_=banks[1][:].rearrange("p s r -> p (s r)"))
             return flipped_sb
 
         kT = [None] * B
@@ -118,18 +123,30 @@ def tile_differentialattention_pa_kernel(
             exps = keep.tile([P, 2], F32)
             exp_sum = keep.tile([P, 1], F32)
             nc.scalar.activation(out=exps[:], in_=dots[:], func=ACT.Exp, accum_out=exp_sum[:])
-            nc.vector.tensor_scalar_add(out=lam[:], in0=exp_sum[:], scalar1=LAMBDA_INIT)
+            nc.gpsimd.tensor_scalar(
+                out=lam[:], in0=exp_sum[:], scalar1=1.0, scalar2=LAMBDA_INIT, op0=ALU.mult, op1=ALU.add
+            )
 
         wv_codes = keep.tile([P, D_PASSES, HD2], U32, align_bytes=64)
         wv_scales = keep.tile([P, D_PASSES, HD2], U8, align_bytes=64)
 
+        wv_grouped = keep.tile([P, D_PASSES, HD2, PACK], BF16, align_bytes=64)
+
+        def group_wv():
+            nc.gpsimd.tensor_scalar(
+                out=wv_grouped[:],
+                in0=wv_rows[:].rearrange("p c t n -> p c n t"),
+                scalar1=1.0,
+                scalar2=0.0,
+                op0=ALU.mult,
+                op1=ALU.add,
+            )
+
         def quantise_wv():
-            grouped = keep.tile([P, D_PASSES, HD2, PACK], BF16, align_bytes=64, name="wv_grouped")
-            nc.vector.tensor_copy(out=grouped[:], in_=wv_rows[:].rearrange("p c t n -> p c n t"))
             nc.vector.quantize_mx(
                 out=wv_codes[:].rearrange("p c n -> p (c n)").bitcast(FP8X4),
                 scales=wv_scales[:].rearrange("p c n -> p (c n)"),
-                in_=grouped[:].rearrange("p c n t -> p (c n t)"),
+                in_=wv_grouped[:].rearrange("p c n t -> p (c n t)"),
             )
 
         x_flipped = {}
@@ -145,7 +162,7 @@ def tile_differentialattention_pa_kernel(
             words = x_rows[g][:].bitcast(F32)
             x_flipped[tile] = []
             for pair in range(D_PASSES // 2):
-                flipped = flip_banks.tile([P, 2, 2, P], F32, tag="flip")
+                flipped = spare_banks.tile([P, 2, 2, P], F32, tag="spare")
                 for c in range(2):
                     for u in range(2):
                         first = t * (D // 2) + (2 * pair + c) * (K_PASS // 2) + u * P
@@ -174,7 +191,7 @@ def tile_differentialattention_pa_kernel(
         def project_chunk(g):
             v_sums[g] = []
             for half in range(2):
-                sums = mx_banks.tile([P, PACK, HD], F32, tag="mx")
+                sums = spare_banks.tile([P, PACK, HD], F32, tag="spare")
                 for t in range(PACK):
                     for c in range(D_PASSES):
                         tokens = slice(c * P, (c + 1) * P)
@@ -195,7 +212,7 @@ def tile_differentialattention_pa_kernel(
         def group_v(g):
             grouped = work.tile([P, HD2, PACK], BF16, align_bytes=64, name="v_grouped")
             for half in range(2):
-                nc.scalar.copy(
+                nc.vector.tensor_copy(
                     out=grouped[:, half * HD : (half + 1) * HD, :],
                     in_=v_sums[g][half][:].rearrange("p t n -> p n t"),
                 )
@@ -211,56 +228,59 @@ def tile_differentialattention_pa_kernel(
         scores = {}
         exponentials = {}
         exp_sums = {}
+        attn_rows = {}
+        attn_flipped = {}
         attn_grouped = {}
+        out_sums = {}
         attn_codes = {}
         attn_scales = {}
 
-        def multiply_q_k(i):
+        def multiply_q_k(i, half):
             b, tile_in_batch = divmod(i, TILES_PER_BATCH)
             queries = slice(tile_in_batch * P, (tile_in_batch + 1) * P)
-            scores[i] = []
-            for half in range(2):
-                for c in range(KEY_BANKS):
-                    bank = score_banks.tile([P, BANK], F32, tag="scores")
-                    nc.tensor.matmul(
-                        bank[:],
-                        lhsT=qT[b][:, half, queries],
-                        rhs=kT[b][:, half, c * BANK : (c + 1) * BANK],
-                        start=True,
-                        stop=True,
-                    )
-                    scores[i].append(bank)
-
-        def exponentiate(i):
-            expo = work.tile([P, 2, S], F32)
-            sums = stats.tile([P, 2 * KEY_BANKS], F32)
-            peaks = stats.tile([P, 2 * KEY_BANKS], F32)
-            shift = stats.tile([P, 2], F32)
-            for half in range(2):
-                first = half * KEY_BANKS
-                for c in range(first, first + KEY_BANKS):
-                    nc.vector.tensor_reduce(out=peaks[:, c : c + 1], in_=scores[i][c][:], axis=AXIS.X, op=ALU.max)
-                nc.vector.tensor_scalar(
-                    out=shift[:, half : half + 1],
-                    in0=peaks[:, first : first + 1],
-                    scalar1=peaks[:, first + 1 : first + 2],
-                    scalar2=-SCALE,
-                    op0=ALU.max,
-                    op1=ALU.mult,
+            if half == 0:
+                scores[i] = []
+            for c in range(KEY_BANKS):
+                bank = score_banks.tile([P, BANK], F32, tag="scores")
+                nc.tensor.matmul(
+                    bank[:],
+                    lhsT=qT[b][:, half, queries],
+                    rhs=kT[b][:, half, c * BANK : (c + 1) * BANK],
+                    start=True,
+                    stop=True,
                 )
-                for c in range(KEY_BANKS):
-                    nc.scalar.activation(
-                        out=expo[:, half, c * BANK : (c + 1) * BANK],
-                        in_=scores[i][first + c][:],
-                        func=ACT.Exp,
-                        bias=shift[:, half : half + 1],
-                        scale=SCALE,
-                        accum_out=sums[:, first + c : first + c + 1],
-                    )
-            exponentials[i] = expo
-            exp_sums[i] = sums
+                scores[i].append(bank)
 
-        def difference(i):
+        def exponentiate(i, half):
+            if half == 0:
+                exponentials[i] = work.tile([P, 2, S], F32, name="expo", bufs=4)
+                exp_sums[i] = stats.tile([P, 2 * KEY_BANKS], F32, name="sums")
+            peaks = stats.tile([P, KEY_BANKS], F32)
+            shift = stats.tile([P, 1], F32)
+            first = half * KEY_BANKS
+            for c in range(KEY_BANKS):
+                nc.vector.tensor_reduce(out=peaks[:, c : c + 1], in_=scores[i][first + c][:], axis=AXIS.X, op=ALU.max)
+            nc.vector.tensor_scalar(
+                out=shift[:],
+                in0=peaks[:, 0:1],
+                scalar1=peaks[:, 1:2],
+                scalar2=-SCALE,
+                op0=ALU.max,
+                op1=ALU.mult,
+            )
+            for c in range(KEY_BANKS):
+                nc.scalar.activation(
+                    out=exponentials[i][:, half, c * BANK : (c + 1) * BANK],
+                    in_=scores[i][first + c][:],
+                    func=ACT.Exp,
+                    bias=shift[:],
+                    scale=SCALE,
+                    accum_out=exp_sums[i][:, first + c : first + c + 1],
+                )
+
+        inverses = {}
+
+        def scale_second_half(i):
             expo = exponentials[i]
             totals = stats.tile([P, 2], F32)
             nc.vector.tensor_reduce(
@@ -271,7 +291,7 @@ def tile_differentialattention_pa_kernel(
             )
             inverse = stats.tile([P, 2], F32)
             nc.vector.reciprocal(out=inverse[:], in_=totals[:])
-            nc.vector.tensor_scalar(
+            nc.gpsimd.tensor_scalar(
                 out=expo[:, 1, :],
                 in0=expo[:, 1, :],
                 scalar1=inverse[:, 1:2],
@@ -279,6 +299,11 @@ def tile_differentialattention_pa_kernel(
                 op0=ALU.mult,
                 op1=ALU.mult,
             )
+            inverses[i] = inverse
+
+        def difference(i):
+            expo = exponentials[i]
+            inverse = inverses[i]
             attn = work.tile([P, S], BF16)
             nc.vector.scalar_tensor_tensor(
                 out=attn[:],
@@ -288,16 +313,22 @@ def tile_differentialattention_pa_kernel(
                 op0=ALU.mult,
                 op1=ALU.subtract,
             )
-            attn_words = attn[:].bitcast(F32)
-            flipped = flip_banks.tile([P, CHUNKS_PER_BATCH, 2, P], F32, tag="flip")
+            attn_rows[i] = attn
+
+        def transpose_attn(i):
+            attn_words = attn_rows[i][:].bitcast(F32)
+            flipped = spare_banks.tile([P, CHUNKS_PER_BATCH, 2, P], F32, tag="spare")
             for g in range(CHUNKS_PER_BATCH):
                 for u in range(2):
                     first = (2 * g + u) * P
                     nc.tensor.transpose(flipped[:, g, u, :], attn_words[:, first : first + P], ident_f32[:])
+            attn_flipped[i] = flipped
+
+        def group_attn(i):
             grouped = work.tile([P, S], BF16, align_bytes=64, name="attn_grouped")
             nc.scalar.copy(
                 out=grouped[:].bitcast(F32).rearrange("p (g r u) -> p g r u", g=CHUNKS_PER_BATCH, u=2),
-                in_=flipped[:].rearrange("p g u r -> p g r u"),
+                in_=attn_flipped[i][:].rearrange("p g u r -> p g r u"),
             )
             attn_grouped[i] = grouped
 
@@ -312,10 +343,10 @@ def tile_differentialattention_pa_kernel(
 
         def multiply_attn_v(i):
             b, tile_in_batch = divmod(i, TILES_PER_BATCH)
-            out_sums = mx_banks.tile([P, HD2], F32, tag="mx")
+            sums = spare_banks.tile([P, HD2], F32, tag="spare")
             for g in range(CHUNKS_PER_BATCH):
                 nc.tensor.matmul_mx(
-                    out=out_sums[:],
+                    out=sums[:],
                     lhsT=attn_codes[i][:, g, :].bitcast(FP8X4),
                     lhsT_scale=attn_scales[i][:, g, :],
                     rhs=v_codes[b * CHUNKS_PER_BATCH + g][:].bitcast(FP8X4),
@@ -323,17 +354,23 @@ def tile_differentialattention_pa_kernel(
                     start=(g == 0),
                     stop=(g == CHUNKS_PER_BATCH - 1),
                 )
+            out_sums[i] = sums
+
+        def store_out(i):
+            b, tile_in_batch = divmod(i, TILES_PER_BATCH)
             out_rows = work.tile([P, HD2], F32)
-            nc.scalar.copy(out=out_rows[:], in_=out_sums[:])
+            nc.scalar.copy(out=out_rows[:], in_=out_sums[i][:])
             nc.sync.dma_start(out=out[b].rearrange("(p s) n -> s p n", p=P)[tile_in_batch], in_=out_rows[:])
 
-        kT[0] = flip_tokens("kT0", k_rows[0])
-        qT[0] = flip_tokens("qT0", q_rows[0])
+        kT[0] = keep_tokens("kT0", transpose_tokens(k_rows[0]))
+        qT[0] = keep_tokens("qT0", transpose_tokens(q_rows[0]))
         compute_lam()
-        multiply_q_k(0)
+        group_wv()
+        multiply_q_k(0, 0)
+        multiply_q_k(0, 1)
         chunks_ready = 0
         finished = 0
-        for step in range(QUERY_TILES + 2):
+        for step in range(QUERY_TILES + 3):
             first_new = step * X_TILES_PER_STEP
             new_x_tiles = [t for t in range(first_new, first_new + X_TILES_PER_STEP) if t < X_TILES]
             grouped_x_tiles = [t for t in range(first_new - X_TILES_PER_STEP, first_new) if 0 <= t < X_TILES]
@@ -341,35 +378,44 @@ def tile_differentialattention_pa_kernel(
 
             for t in new_x_tiles[:1]:
                 transpose_x(t)
-            if step + 1 < QUERY_TILES:
-                multiply_q_k(step + 1)
             if step < QUERY_TILES:
-                exponentiate(step)
-            for g in projected:
-                group_v(g)
+                exponentiate(step, 0)
+            if step + 1 < QUERY_TILES:
+                multiply_q_k(step + 1, 0)
+            if step < QUERY_TILES:
+                exponentiate(step, 1)
+            if step == 0:
+                kT[1] = keep_tokens("kT1", transpose_tokens(k_rows[1]))
+                qT[1] = keep_tokens("qT1", transpose_tokens(q_rows[1]))
+            if 0 <= step - 1 < QUERY_TILES:
+                scale_second_half(step - 1)
+            if 0 <= step - 2 < QUERY_TILES:
+                difference(step - 2)
+                transpose_attn(step - 2)
+            if step + 1 < QUERY_TILES:
+                multiply_q_k(step + 1, 1)
             for t in new_x_tiles[:1]:
                 group_x(t)
+            if 0 <= step - 2 < QUERY_TILES:
+                group_attn(step - 2)
+            if 0 <= step - 3 < QUERY_TILES:
+                quantise_attn(step - 3)
+            for turn in range(FINISHES_PER_STEP):
+                if finished <= step - 3 and chunks_ready >= (finished // TILES_PER_BATCH + 1) * CHUNKS_PER_BATCH:
+                    multiply_attn_v(finished)
+                    store_out(finished)
+                    finished += 1
             for t in new_x_tiles[1:]:
                 transpose_x(t)
                 group_x(t)
-            if 1 <= step <= QUERY_TILES:
-                difference(step - 1)
-            if 2 <= step:
-                quantise_attn(step - 2)
-            if step == 0:
+            if step == 1:
                 quantise_wv()
             for t in grouped_x_tiles:
                 quantise_x(t)
             for g in projected:
+                group_v(g)
                 quantise_v(g)
                 chunks_ready += 1
-            for turn in range(FINISHES_PER_STEP):
-                if finished <= step - 2 and chunks_ready >= (finished // TILES_PER_BATCH + 1) * CHUNKS_PER_BATCH:
-                    multiply_attn_v(finished)
-                    finished += 1
             for t in grouped_x_tiles:
                 if t % PACK == PACK - 1:
                     project_chunk(t // PACK)
-            if step == TILES_PER_BATCH - 2:
-                kT[1] = flip_tokens("kT1", k_rows[1])
-                qT[1] = flip_tokens("qT1", q_rows[1])

@@ -50,12 +50,10 @@ def tile_differentialattention_pa_kernel(
         score_banks = ctx.enter_context(tc.psum_pool(name="score_banks", bufs=2 * KEY_BANKS))
         spare_banks = ctx.enter_context(tc.psum_pool(name="spare_banks", bufs=4))
 
-        lambda_q = keep.tile([P, 2, HD], BF16)
-        lambda_k = keep.tile([P, 2, HD], BF16)
-        nc.scalar.dma_start(out=lambda_q[:, 0, :], in_=lambda_q1.partition_broadcast(P))
-        nc.scalar.dma_start(out=lambda_k[:, 0, :], in_=lambda_k1.partition_broadcast(P))
-        nc.scalar.dma_start(out=lambda_q[:, 1, :], in_=lambda_q2.partition_broadcast(P))
-        nc.scalar.dma_start(out=lambda_k[:, 1, :], in_=lambda_k2.partition_broadcast(P))
+        lambda_row = keep.tile([P, 4, HD], BF16)
+        nc.vector.memset(lambda_row[:], 0.0)
+        for n, vector in enumerate((lambda_q1, lambda_q2, lambda_k1, lambda_k2)):
+            nc.scalar.dma_start(out=lambda_row[0:1, n, :], in_=vector.unsqueeze(0))
 
         def load_tokens(name, tiled_source):
             rows = keep.tile([P, TILES_PER_BATCH, HD2], BF16, name=name)
@@ -114,10 +112,24 @@ def tile_differentialattention_pa_kernel(
         qT = [None] * B
 
         lam = keep.tile([P, 1], F32)
+        lambdas = keep.tile([P, 4, HD], F32)
+
+        def spread_lambdas():
+            ones = keep.tile([P, P], BF16)
+            nc.vector.memset(ones[:], 1.0)
+            spread = spare_banks.tile([P, 4, HD], F32, tag="spare")
+            nc.tensor.matmul(
+                spread[:].rearrange("p n h -> p (n h)"),
+                lhsT=ones[:],
+                rhs=lambda_row[:].rearrange("p n h -> p (n h)"),
+                start=True,
+                stop=True,
+            )
+            nc.scalar.copy(out=lambdas[:], in_=spread[:])
 
         def compute_lam():
             products = keep.tile([P, 2, HD], F32)
-            nc.vector.tensor_tensor(out=products[:], in0=lambda_q[:], in1=lambda_k[:], op=ALU.mult)
+            nc.vector.tensor_tensor(out=products[:], in0=lambdas[:, 0:2, :], in1=lambdas[:, 2:4, :], op=ALU.mult)
             dots = keep.tile([P, 2], F32)
             nc.vector.tensor_reduce(out=dots[:], in_=products[:], axis=AXIS.X, op=ALU.add)
             exps = keep.tile([P, 2], F32)
@@ -362,6 +374,7 @@ def tile_differentialattention_pa_kernel(
             nc.scalar.copy(out=out_rows[:], in_=out_sums[i][:])
             nc.sync.dma_start(out=out[b].rearrange("(p s) n -> s p n", p=P)[tile_in_batch], in_=out_rows[:])
 
+        spread_lambdas()
         kT[0] = keep_tokens("kT0", transpose_tokens(k_rows[0]))
         qT[0] = keep_tokens("qT0", transpose_tokens(q_rows[0]))
         compute_lam()

@@ -47,13 +47,14 @@ def tile_differentialattention_pa_kernel(
         keep = ctx.enter_context(tc.tile_pool(name="keep", bufs=1))
         work = ctx.enter_context(tc.tile_pool(name="work", bufs=3))
         stats = ctx.enter_context(tc.tile_pool(name="stats", bufs=4))
-        score_banks = ctx.enter_context(tc.psum_pool(name="score_banks", bufs=2 * KEY_BANKS))
-        spare_banks = ctx.enter_context(tc.psum_pool(name="spare_banks", bufs=4))
+        psum = ctx.enter_context(tc.psum_pool(name="psum_banks", bufs=8))
 
-        lambda_row = keep.tile([P, 4, HD], BF16)
-        nc.vector.memset(lambda_row[:], 0.0)
-        for n, vector in enumerate((lambda_q1, lambda_q2, lambda_k1, lambda_k2)):
-            nc.scalar.dma_start(out=lambda_row[0:1, n, :], in_=vector.unsqueeze(0))
+        lambda_q = keep.tile([P, 2, HD], BF16)
+        lambda_k = keep.tile([P, 2, HD], BF16)
+        nc.scalar.dma_start(out=lambda_q[:, 0, :], in_=lambda_q1.partition_broadcast(P))
+        nc.scalar.dma_start(out=lambda_k[:, 0, :], in_=lambda_k1.partition_broadcast(P))
+        nc.scalar.dma_start(out=lambda_q[:, 1, :], in_=lambda_q2.partition_broadcast(P))
+        nc.scalar.dma_start(out=lambda_k[:, 1, :], in_=lambda_k2.partition_broadcast(P))
 
         def load_tokens(name, tiled_source):
             rows = keep.tile([P, TILES_PER_BATCH, HD2], BF16, name=name)
@@ -94,7 +95,7 @@ def tile_differentialattention_pa_kernel(
         def transpose_tokens(rows):
             banks = []
             for half in range(2):
-                flipped = spare_banks.tile([P, TILES_PER_BATCH, P], BF16, tag="spare")
+                flipped = psum.tile([P, TILES_PER_BATCH, P], BF16, tag="bank")
                 for s in range(TILES_PER_BATCH):
                     nc.tensor.transpose(
                         flipped[:, s, :], rows[:, s, half * HD : (half + 1) * HD], ident_bf16[:]
@@ -112,24 +113,10 @@ def tile_differentialattention_pa_kernel(
         qT = [None] * B
 
         lam = keep.tile([P, 1], F32)
-        lambdas = keep.tile([P, 4, HD], F32)
-
-        def spread_lambdas():
-            ones = keep.tile([P, P], BF16)
-            nc.vector.memset(ones[:], 1.0)
-            spread = spare_banks.tile([P, 4, HD], F32, tag="spare")
-            nc.tensor.matmul(
-                spread[:].rearrange("p n h -> p (n h)"),
-                lhsT=ones[:],
-                rhs=lambda_row[:].rearrange("p n h -> p (n h)"),
-                start=True,
-                stop=True,
-            )
-            nc.scalar.copy(out=lambdas[:], in_=spread[:])
 
         def compute_lam():
             products = keep.tile([P, 2, HD], F32)
-            nc.vector.tensor_tensor(out=products[:], in0=lambdas[:, 0:2, :], in1=lambdas[:, 2:4, :], op=ALU.mult)
+            nc.vector.tensor_tensor(out=products[:], in0=lambda_q[:], in1=lambda_k[:], op=ALU.mult)
             dots = keep.tile([P, 2], F32)
             nc.vector.tensor_reduce(out=dots[:], in_=products[:], axis=AXIS.X, op=ALU.add)
             exps = keep.tile([P, 2], F32)
@@ -174,7 +161,7 @@ def tile_differentialattention_pa_kernel(
             words = x_rows[g][:].bitcast(F32)
             x_flipped[tile] = []
             for pair in range(D_PASSES // 2):
-                flipped = spare_banks.tile([P, 2, 2, P], F32, tag="spare")
+                flipped = psum.tile([P, 2, 2, P], F32, tag="bank")
                 for c in range(2):
                     for u in range(2):
                         first = t * (D // 2) + (2 * pair + c) * (K_PASS // 2) + u * P
@@ -203,7 +190,7 @@ def tile_differentialattention_pa_kernel(
         def project_chunk(g):
             v_sums[g] = []
             for half in range(2):
-                sums = spare_banks.tile([P, PACK, HD], F32, tag="spare")
+                sums = psum.tile([P, PACK, HD], F32, tag="bank")
                 for t in range(PACK):
                     for c in range(D_PASSES):
                         tokens = slice(c * P, (c + 1) * P)
@@ -253,7 +240,7 @@ def tile_differentialattention_pa_kernel(
             if half == 0:
                 scores[i] = []
             for c in range(KEY_BANKS):
-                bank = score_banks.tile([P, BANK], F32, tag="scores")
+                bank = psum.tile([P, BANK], F32, tag="bank")
                 nc.tensor.matmul(
                     bank[:],
                     lhsT=qT[b][:, half, queries],
@@ -263,23 +250,29 @@ def tile_differentialattention_pa_kernel(
                 )
                 scores[i].append(bank)
 
+        peaks = {}
+
+        def row_maximum(i, half, c):
+            if c == 0:
+                peaks[i, half] = stats.tile([P, KEY_BANKS], F32, name="peaks")
+            nc.vector.tensor_reduce(
+                out=peaks[i, half][:, c : c + 1], in_=scores[i][half * KEY_BANKS + c][:], axis=AXIS.X, op=ALU.max
+            )
+
         def exponentiate(i, half):
             if half == 0:
                 exponentials[i] = work.tile([P, 2, S], F32, name="expo", bufs=4)
                 exp_sums[i] = stats.tile([P, 2 * KEY_BANKS], F32, name="sums")
-            peaks = stats.tile([P, KEY_BANKS], F32)
             shift = stats.tile([P, 1], F32)
-            first = half * KEY_BANKS
-            for c in range(KEY_BANKS):
-                nc.vector.tensor_reduce(out=peaks[:, c : c + 1], in_=scores[i][first + c][:], axis=AXIS.X, op=ALU.max)
             nc.vector.tensor_scalar(
                 out=shift[:],
-                in0=peaks[:, 0:1],
-                scalar1=peaks[:, 1:2],
+                in0=peaks[i, half][:, 0:1],
+                scalar1=peaks[i, half][:, 1:2],
                 scalar2=-SCALE,
                 op0=ALU.max,
                 op1=ALU.mult,
             )
+            first = half * KEY_BANKS
             for c in range(KEY_BANKS):
                 nc.scalar.activation(
                     out=exponentials[i][:, half, c * BANK : (c + 1) * BANK],
@@ -292,18 +285,23 @@ def tile_differentialattention_pa_kernel(
 
         inverses = {}
 
-        def scale_second_half(i):
-            expo = exponentials[i]
-            totals = stats.tile([P, 2], F32)
+        totals = {}
+
+        def add_row_sums(i):
+            totals[i] = stats.tile([P, 2], F32, name="totals")
             nc.vector.tensor_reduce(
-                out=totals[:],
+                out=totals[i][:],
                 in_=exp_sums[i][:].rearrange("p (h c) -> p h c", c=KEY_BANKS),
                 axis=AXIS.X,
                 op=ALU.add,
             )
+
+        def scale_second_half(i):
+            expo = exponentials[i]
             inverse = stats.tile([P, 2], F32)
-            nc.vector.reciprocal(out=inverse[:], in_=totals[:])
-            nc.gpsimd.tensor_scalar(
+            nc.vector.reciprocal(out=inverse[:], in_=totals[i][:])
+            scaler = nc.gpsimd if i < QUERY_TILES - 2 else nc.vector
+            scaler.tensor_scalar(
                 out=expo[:, 1, :],
                 in0=expo[:, 1, :],
                 scalar1=inverse[:, 1:2],
@@ -329,7 +327,7 @@ def tile_differentialattention_pa_kernel(
 
         def transpose_attn(i):
             attn_words = attn_rows[i][:].bitcast(F32)
-            flipped = spare_banks.tile([P, CHUNKS_PER_BATCH, 2, P], F32, tag="spare")
+            flipped = psum.tile([P, CHUNKS_PER_BATCH, 2, P], F32, tag="bank")
             for g in range(CHUNKS_PER_BATCH):
                 for u in range(2):
                     first = (2 * g + u) * P
@@ -355,7 +353,7 @@ def tile_differentialattention_pa_kernel(
 
         def multiply_attn_v(i):
             b, tile_in_batch = divmod(i, TILES_PER_BATCH)
-            sums = spare_banks.tile([P, HD2], F32, tag="spare")
+            sums = psum.tile([P, HD2], F32, tag="bank")
             for g in range(CHUNKS_PER_BATCH):
                 nc.tensor.matmul_mx(
                     out=sums[:],
@@ -374,13 +372,13 @@ def tile_differentialattention_pa_kernel(
             nc.scalar.copy(out=out_rows[:], in_=out_sums[i][:])
             nc.sync.dma_start(out=out[b].rearrange("(p s) n -> s p n", p=P)[tile_in_batch], in_=out_rows[:])
 
-        spread_lambdas()
         kT[0] = keep_tokens("kT0", transpose_tokens(k_rows[0]))
         qT[0] = keep_tokens("qT0", transpose_tokens(q_rows[0]))
         compute_lam()
         group_wv()
         multiply_q_k(0, 0)
         multiply_q_k(0, 1)
+        units_multiplied = 2
         chunks_ready = 0
         finished = 0
         for step in range(QUERY_TILES + 3):
@@ -388,31 +386,38 @@ def tile_differentialattention_pa_kernel(
             new_x_tiles = [t for t in range(first_new, first_new + X_TILES_PER_STEP) if t < X_TILES]
             grouped_x_tiles = [t for t in range(first_new - X_TILES_PER_STEP, first_new) if 0 <= t < X_TILES]
             projected = [g for g in v_sums if g >= chunks_ready]
+            ahead = 2 if new_x_tiles or grouped_x_tiles or projected else 3
 
             for t in new_x_tiles[:1]:
                 transpose_x(t)
             if step < QUERY_TILES:
+                row_maximum(step, 0, 0)
+                row_maximum(step, 0, 1)
+                row_maximum(step, 1, 0)
                 exponentiate(step, 0)
-            if step + 1 < QUERY_TILES:
-                multiply_q_k(step + 1, 0)
+                row_maximum(step, 1, 1)
+            while units_multiplied <= min(2 * step + ahead, 2 * QUERY_TILES - 1):
+                multiply_q_k(units_multiplied // 2, units_multiplied % 2)
+                units_multiplied += 1
+            if 0 <= step - 2 < QUERY_TILES:
+                difference(step - 2)
+                transpose_attn(step - 2)
             if step < QUERY_TILES:
                 exponentiate(step, 1)
             if step == 0:
                 kT[1] = keep_tokens("kT1", transpose_tokens(k_rows[1]))
                 qT[1] = keep_tokens("qT1", transpose_tokens(q_rows[1]))
             if 0 <= step - 1 < QUERY_TILES:
-                scale_second_half(step - 1)
-            if 0 <= step - 2 < QUERY_TILES:
-                difference(step - 2)
-                transpose_attn(step - 2)
-            if step + 1 < QUERY_TILES:
-                multiply_q_k(step + 1, 1)
+                add_row_sums(step - 1)
+            if 0 <= step - 3 < QUERY_TILES:
+                quantise_attn(step - 3)
+            while units_multiplied <= min(2 * step + 1 + ahead, 2 * QUERY_TILES - 1):
+                multiply_q_k(units_multiplied // 2, units_multiplied % 2)
+                units_multiplied += 1
             for t in new_x_tiles[:1]:
                 group_x(t)
             if 0 <= step - 2 < QUERY_TILES:
                 group_attn(step - 2)
-            if 0 <= step - 3 < QUERY_TILES:
-                quantise_attn(step - 3)
             for turn in range(FINISHES_PER_STEP):
                 if finished <= step - 3 and chunks_ready >= (finished // TILES_PER_BATCH + 1) * CHUNKS_PER_BATCH:
                     multiply_attn_v(finished)
@@ -421,7 +426,7 @@ def tile_differentialattention_pa_kernel(
             for t in new_x_tiles[1:]:
                 transpose_x(t)
                 group_x(t)
-            if step == 1:
+            if step == 2:
                 quantise_wv()
             for t in grouped_x_tiles:
                 quantise_x(t)
@@ -429,6 +434,8 @@ def tile_differentialattention_pa_kernel(
                 group_v(g)
                 quantise_v(g)
                 chunks_ready += 1
+            if 0 <= step - 1 < QUERY_TILES:
+                scale_second_half(step - 1)
             for t in grouped_x_tiles:
                 if t % PACK == PACK - 1:
                     project_chunk(t // PACK)

@@ -32,8 +32,12 @@ X_TILES = CHUNKS * PACK
 D_PASSES = D // K_PASS
 KEY_BANKS = S // BANK
 
+SUMS_LAG = 1
+DIFFERENCE_LAG = 2
+QUANTISE_LAG = 3
 X_TILES_PER_STEP = 2
 FINISHES_PER_STEP = 2
+PSUM_BANKS = 8
 
 FLOPS = 2 * B * S * D * HD2 + 2 * (2 * B * S * S * HD) + 2 * B * S * S * HD2
 
@@ -47,7 +51,7 @@ def tile_differentialattention_pa_kernel(
         keep = ctx.enter_context(tc.tile_pool(name="keep", bufs=1))
         work = ctx.enter_context(tc.tile_pool(name="work", bufs=3))
         stats = ctx.enter_context(tc.tile_pool(name="stats", bufs=4))
-        psum = ctx.enter_context(tc.psum_pool(name="psum_banks", bufs=8))
+        psum = ctx.enter_context(tc.psum_pool(name="psum_banks", bufs=PSUM_BANKS))
 
         lambda_q = keep.tile([P, 2, HD], BF16)
         lambda_k = keep.tile([P, 2, HD], BF16)
@@ -62,10 +66,10 @@ def tile_differentialattention_pa_kernel(
             return rows
 
         def load_x(rows, g, u):
-            first = g * CHUNK + u * (CHUNK // 2)
+            first_token = g * CHUNK + u * (CHUNK // 2)
             nc.sync.dma_start(
                 out=rows[:, u * 2 * D : (u + 1) * 2 * D],
-                in_=x_flat[first : first + CHUNK // 2, :].rearrange("(p e) d -> p (e d)", e=2),
+                in_=x_flat[first_token : first_token + CHUNK // 2, :].rearrange("(p e) d -> p (e d)", e=2),
             )
 
         x_flat = x.flatten_outer_dims()
@@ -75,13 +79,13 @@ def tile_differentialattention_pa_kernel(
         q_rows = [None] * B
         k_rows[0] = load_tokens("k_rows0", k[0].rearrange("(s p) h -> p s h", p=P))
         q_rows[0] = load_tokens("q_rows0", q[0].rearrange("(p s) h -> p s h", p=P))
-        load_x(x_rows[0], 0, 0)
-        k_rows[1] = load_tokens("k_rows1", k[1].rearrange("(s p) h -> p s h", p=P))
-        q_rows[1] = load_tokens("q_rows1", q[1].rearrange("(p s) h -> p s h", p=P))
         nc.sync.dma_start(
             out=wv_rows[:].rearrange("p c (u e) n -> p (c u) (e n)", e=2),
             in_=WV.rearrange("(s p e) n -> p s (e n)", p=P, e=2),
         )
+        load_x(x_rows[0], 0, 0)
+        k_rows[1] = load_tokens("k_rows1", k[1].rearrange("(s p) h -> p s h", p=P))
+        q_rows[1] = load_tokens("q_rows1", q[1].rearrange("(p s) h -> p s h", p=P))
         load_x(x_rows[0], 0, 1)
         for g in range(1, CHUNKS):
             for u in range(2):
@@ -164,8 +168,10 @@ def tile_differentialattention_pa_kernel(
                 flipped = psum.tile([P, 2, 2, P], F32, tag="bank")
                 for c in range(2):
                     for u in range(2):
-                        first = t * (D // 2) + (2 * pair + c) * (K_PASS // 2) + u * P
-                        nc.tensor.transpose(flipped[:, c, u, :], words[:, first : first + P], ident_f32[:])
+                        first_word = t * (D // 2) + (2 * pair + c) * (K_PASS // 2) + u * P
+                        nc.tensor.transpose(
+                            flipped[:, c, u, :], words[:, first_word : first_word + P], ident_f32[:]
+                        )
                 x_flipped[tile].append(flipped)
 
         def group_x(tile):
@@ -239,12 +245,12 @@ def tile_differentialattention_pa_kernel(
             queries = slice(tile_in_batch * P, (tile_in_batch + 1) * P)
             if half == 0:
                 scores[i] = []
-            for c in range(KEY_BANKS):
+            for key_bank in range(KEY_BANKS):
                 bank = psum.tile([P, BANK], F32, tag="bank")
                 nc.tensor.matmul(
                     bank[:],
                     lhsT=qT[b][:, half, queries],
-                    rhs=kT[b][:, half, c * BANK : (c + 1) * BANK],
+                    rhs=kT[b][:, half, key_bank * BANK : (key_bank + 1) * BANK],
                     start=True,
                     stop=True,
                 )
@@ -252,16 +258,19 @@ def tile_differentialattention_pa_kernel(
 
         peaks = {}
 
-        def row_maximum(i, half, c):
-            if c == 0:
+        def row_maximum(i, half, key_bank):
+            if key_bank == 0:
                 peaks[i, half] = stats.tile([P, KEY_BANKS], F32, name="peaks")
             nc.vector.tensor_reduce(
-                out=peaks[i, half][:, c : c + 1], in_=scores[i][half * KEY_BANKS + c][:], axis=AXIS.X, op=ALU.max
+                out=peaks[i, half][:, key_bank : key_bank + 1],
+                in_=scores[i][half * KEY_BANKS + key_bank][:],
+                axis=AXIS.X,
+                op=ALU.max,
             )
 
         def exponentiate(i, half):
             if half == 0:
-                exponentials[i] = work.tile([P, 2, S], F32, name="expo", bufs=4)
+                exponentials[i] = work.tile([P, 2, S], F32, name="expo", bufs=DIFFERENCE_LAG + 2)
                 exp_sums[i] = stats.tile([P, 2 * KEY_BANKS], F32, name="sums")
             shift = stats.tile([P, 1], F32)
             nc.vector.tensor_scalar(
@@ -272,26 +281,25 @@ def tile_differentialattention_pa_kernel(
                 op0=ALU.max,
                 op1=ALU.mult,
             )
-            first = half * KEY_BANKS
-            for c in range(KEY_BANKS):
+            for key_bank in range(KEY_BANKS):
+                column = half * KEY_BANKS + key_bank
                 nc.scalar.activation(
-                    out=exponentials[i][:, half, c * BANK : (c + 1) * BANK],
-                    in_=scores[i][first + c][:],
+                    out=exponentials[i][:, half, key_bank * BANK : (key_bank + 1) * BANK],
+                    in_=scores[i][column][:],
                     func=ACT.Exp,
                     bias=shift[:],
                     scale=SCALE,
-                    accum_out=exp_sums[i][:, first + c : first + c + 1],
+                    accum_out=exp_sums[i][:, column : column + 1],
                 )
 
-        inverses = {}
-
         totals = {}
+        inverses = {}
 
         def add_row_sums(i):
             totals[i] = stats.tile([P, 2], F32, name="totals")
             nc.vector.tensor_reduce(
                 out=totals[i][:],
-                in_=exp_sums[i][:].rearrange("p (h c) -> p h c", c=KEY_BANKS),
+                in_=exp_sums[i][:].rearrange("p (h k) -> p h k", k=KEY_BANKS),
                 axis=AXIS.X,
                 op=ALU.add,
             )
@@ -300,7 +308,7 @@ def tile_differentialattention_pa_kernel(
             expo = exponentials[i]
             inverse = stats.tile([P, 2], F32)
             nc.vector.reciprocal(out=inverse[:], in_=totals[i][:])
-            scaler = nc.gpsimd if i < QUERY_TILES - 2 else nc.vector
+            scaler = nc.gpsimd if i < QUERY_TILES - DIFFERENCE_LAG else nc.vector
             scaler.tensor_scalar(
                 out=expo[:, 1, :],
                 in0=expo[:, 1, :],
@@ -328,17 +336,19 @@ def tile_differentialattention_pa_kernel(
         def transpose_attn(i):
             attn_words = attn_rows[i][:].bitcast(F32)
             flipped = psum.tile([P, CHUNKS_PER_BATCH, 2, P], F32, tag="bank")
-            for g in range(CHUNKS_PER_BATCH):
+            for key_pass in range(CHUNKS_PER_BATCH):
                 for u in range(2):
-                    first = (2 * g + u) * P
-                    nc.tensor.transpose(flipped[:, g, u, :], attn_words[:, first : first + P], ident_f32[:])
+                    first_word = (2 * key_pass + u) * P
+                    nc.tensor.transpose(
+                        flipped[:, key_pass, u, :], attn_words[:, first_word : first_word + P], ident_f32[:]
+                    )
             attn_flipped[i] = flipped
 
         def group_attn(i):
             grouped = work.tile([P, S], BF16, align_bytes=64, name="attn_grouped")
             nc.scalar.copy(
-                out=grouped[:].bitcast(F32).rearrange("p (g r u) -> p g r u", g=CHUNKS_PER_BATCH, u=2),
-                in_=attn_flipped[i][:].rearrange("p g u r -> p g r u"),
+                out=grouped[:].bitcast(F32).rearrange("p (k r u) -> p k r u", k=CHUNKS_PER_BATCH, u=2),
+                in_=attn_flipped[i][:].rearrange("p k u r -> p k r u"),
             )
             attn_grouped[i] = grouped
 
@@ -346,23 +356,24 @@ def tile_differentialattention_pa_kernel(
             attn_codes[i] = work.tile([P, CHUNKS_PER_BATCH, P], U32, align_bytes=64, bufs=6, name="attn_codes")
             attn_scales[i] = work.tile([P, CHUNKS_PER_BATCH, P], U8, align_bytes=64, bufs=6, name="attn_scales")
             nc.vector.quantize_mx(
-                out=attn_codes[i][:].rearrange("p g r -> p (g r)").bitcast(FP8X4),
-                scales=attn_scales[i][:].rearrange("p g r -> p (g r)"),
+                out=attn_codes[i][:].rearrange("p k r -> p (k r)").bitcast(FP8X4),
+                scales=attn_scales[i][:].rearrange("p k r -> p (k r)"),
                 in_=attn_grouped[i][:],
             )
 
         def multiply_attn_v(i):
-            b, tile_in_batch = divmod(i, TILES_PER_BATCH)
+            b = i // TILES_PER_BATCH
             sums = psum.tile([P, HD2], F32, tag="bank")
-            for g in range(CHUNKS_PER_BATCH):
+            for key_pass in range(CHUNKS_PER_BATCH):
+                g = b * CHUNKS_PER_BATCH + key_pass
                 nc.tensor.matmul_mx(
                     out=sums[:],
-                    lhsT=attn_codes[i][:, g, :].bitcast(FP8X4),
-                    lhsT_scale=attn_scales[i][:, g, :],
-                    rhs=v_codes[b * CHUNKS_PER_BATCH + g][:].bitcast(FP8X4),
-                    rhs_scale=v_scales[b * CHUNKS_PER_BATCH + g][:],
-                    start=(g == 0),
-                    stop=(g == CHUNKS_PER_BATCH - 1),
+                    lhsT=attn_codes[i][:, key_pass, :].bitcast(FP8X4),
+                    lhsT_scale=attn_scales[i][:, key_pass, :],
+                    rhs=v_codes[g][:].bitcast(FP8X4),
+                    rhs_scale=v_scales[g][:],
+                    start=(key_pass == 0),
+                    stop=(key_pass == CHUNKS_PER_BATCH - 1),
                 )
             out_sums[i] = sums
 
@@ -378,64 +389,66 @@ def tile_differentialattention_pa_kernel(
         group_wv()
         multiply_q_k(0, 0)
         multiply_q_k(0, 1)
+        units = 2 * QUERY_TILES
         units_multiplied = 2
         chunks_ready = 0
         finished = 0
-        for step in range(QUERY_TILES + 3):
+        for step in range(QUERY_TILES + QUANTISE_LAG):
             first_new = step * X_TILES_PER_STEP
-            new_x_tiles = [t for t in range(first_new, first_new + X_TILES_PER_STEP) if t < X_TILES]
-            grouped_x_tiles = [t for t in range(first_new - X_TILES_PER_STEP, first_new) if 0 <= t < X_TILES]
+            new_x_tiles = [tile for tile in range(first_new, first_new + X_TILES_PER_STEP) if tile < X_TILES]
+            grouped_x_tiles = [tile for tile in range(first_new - X_TILES_PER_STEP, first_new) if 0 <= tile < X_TILES]
             projected = [g for g in v_sums if g >= chunks_ready]
             ahead = 2 if new_x_tiles or grouped_x_tiles or projected else 3
 
-            for t in new_x_tiles[:1]:
-                transpose_x(t)
+            for tile in new_x_tiles[:1]:
+                transpose_x(tile)
             if step < QUERY_TILES:
                 row_maximum(step, 0, 0)
                 row_maximum(step, 0, 1)
                 row_maximum(step, 1, 0)
                 exponentiate(step, 0)
                 row_maximum(step, 1, 1)
-            while units_multiplied <= min(2 * step + ahead, 2 * QUERY_TILES - 1):
+            while units_multiplied <= min(2 * step + ahead, units - 1):
                 multiply_q_k(units_multiplied // 2, units_multiplied % 2)
                 units_multiplied += 1
-            if 0 <= step - 2 < QUERY_TILES:
-                difference(step - 2)
-                transpose_attn(step - 2)
+            if 0 <= step - DIFFERENCE_LAG < QUERY_TILES:
+                difference(step - DIFFERENCE_LAG)
+                transpose_attn(step - DIFFERENCE_LAG)
             if step < QUERY_TILES:
                 exponentiate(step, 1)
             if step == 0:
                 kT[1] = keep_tokens("kT1", transpose_tokens(k_rows[1]))
                 qT[1] = keep_tokens("qT1", transpose_tokens(q_rows[1]))
-            if 0 <= step - 1 < QUERY_TILES:
-                add_row_sums(step - 1)
-            if 0 <= step - 3 < QUERY_TILES:
-                quantise_attn(step - 3)
-            while units_multiplied <= min(2 * step + 1 + ahead, 2 * QUERY_TILES - 1):
+            if 0 <= step - SUMS_LAG < QUERY_TILES:
+                add_row_sums(step - SUMS_LAG)
+            if 0 <= step - QUANTISE_LAG < QUERY_TILES:
+                quantise_attn(step - QUANTISE_LAG)
+            while units_multiplied <= min(2 * step + 1 + ahead, units - 1):
                 multiply_q_k(units_multiplied // 2, units_multiplied % 2)
                 units_multiplied += 1
-            for t in new_x_tiles[:1]:
-                group_x(t)
-            if 0 <= step - 2 < QUERY_TILES:
-                group_attn(step - 2)
+            for tile in new_x_tiles[:1]:
+                group_x(tile)
+            if 0 <= step - DIFFERENCE_LAG < QUERY_TILES:
+                group_attn(step - DIFFERENCE_LAG)
             for turn in range(FINISHES_PER_STEP):
-                if finished <= step - 3 and chunks_ready >= (finished // TILES_PER_BATCH + 1) * CHUNKS_PER_BATCH:
+                chunks_needed = (finished // TILES_PER_BATCH + 1) * CHUNKS_PER_BATCH
+                if finished <= step - QUANTISE_LAG and chunks_ready >= chunks_needed:
                     multiply_attn_v(finished)
                     store_out(finished)
                     finished += 1
-            for t in new_x_tiles[1:]:
-                transpose_x(t)
-                group_x(t)
-            if step == 2:
+            for tile in new_x_tiles[1:]:
+                transpose_x(tile)
+                group_x(tile)
+            if grouped_x_tiles and grouped_x_tiles[-1] == PACK - 1:
                 quantise_wv()
-            for t in grouped_x_tiles:
-                quantise_x(t)
+            for tile in grouped_x_tiles:
+                quantise_x(tile)
             for g in projected:
                 group_v(g)
                 quantise_v(g)
                 chunks_ready += 1
-            if 0 <= step - 1 < QUERY_TILES:
-                scale_second_half(step - 1)
-            for t in grouped_x_tiles:
-                if t % PACK == PACK - 1:
-                    project_chunk(t // PACK)
+            if 0 <= step - SUMS_LAG < QUERY_TILES:
+                scale_second_half(step - SUMS_LAG)
+            for tile in grouped_x_tiles:
+                if tile % PACK == PACK - 1:
+                    project_chunk(tile // PACK)

@@ -60,16 +60,23 @@ def tile_differentialattention_pa_kernel(
         nc.scalar.dma_start(out=lambda_q[:, 1, :], in_=lambda_q2.partition_broadcast(P))
         nc.scalar.dma_start(out=lambda_k[:, 1, :], in_=lambda_k2.partition_broadcast(P))
 
-        def load_tokens(name, tiled_source):
-            rows = keep.tile([P, TILES_PER_BATCH, HD2], BF16, name=name)
-            nc.sync.dma_start(out=rows[:], in_=tiled_source)
+        def load_keys(b):
+            rows = keep.tile([P, TILES_PER_BATCH, HD2], BF16, name="k_rows%d" % b)
+            nc.sync.dma_start(
+                out=rows[:].rearrange("p (g t) h -> p g (t h)", t=PACK),
+                in_=k[b].rearrange("(g p t) h -> p g (t h)", p=P, t=PACK),
+            )
+            return rows
+
+        def load_queries(b):
+            rows = keep.tile([P, TILES_PER_BATCH, HD2], BF16, name="q_rows%d" % b)
+            nc.sync.dma_start(out=rows[:], in_=q[b].rearrange("(p s) h -> p s h", p=P))
             return rows
 
         def load_x(rows, g, u):
-            first_token = g * CHUNK + u * (CHUNK // 2)
+            chunk = x_flat[g * CHUNK : (g + 1) * CHUNK, :].rearrange("(p t) d -> p (t d)", t=PACK)
             nc.sync.dma_start(
-                out=rows[:, u * 2 * D : (u + 1) * 2 * D],
-                in_=x_flat[first_token : first_token + CHUNK // 2, :].rearrange("(p e) d -> p (e d)", e=2),
+                out=rows[:, u * 2 * D : (u + 1) * 2 * D], in_=chunk[:, u * 2 * D : (u + 1) * 2 * D]
             )
 
         x_flat = x.flatten_outer_dims()
@@ -77,15 +84,15 @@ def tile_differentialattention_pa_kernel(
         wv_rows = keep.tile([P, D_PASSES, PACK, HD2], BF16)
         k_rows = [None] * B
         q_rows = [None] * B
-        k_rows[0] = load_tokens("k_rows0", k[0].rearrange("(s p) h -> p s h", p=P))
-        q_rows[0] = load_tokens("q_rows0", q[0].rearrange("(p s) h -> p s h", p=P))
+        k_rows[0] = load_keys(0)
+        q_rows[0] = load_queries(0)
         nc.sync.dma_start(
             out=wv_rows[:].rearrange("p c (u e) n -> p (c u) (e n)", e=2),
             in_=WV.rearrange("(s p e) n -> p s (e n)", p=P, e=2),
         )
         load_x(x_rows[0], 0, 0)
-        k_rows[1] = load_tokens("k_rows1", k[1].rearrange("(s p) h -> p s h", p=P))
-        q_rows[1] = load_tokens("q_rows1", q[1].rearrange("(p s) h -> p s h", p=P))
+        k_rows[1] = load_keys(1)
+        q_rows[1] = load_queries(1)
         load_x(x_rows[0], 0, 1)
         for g in range(1, CHUNKS):
             for u in range(2):
@@ -116,7 +123,7 @@ def tile_differentialattention_pa_kernel(
         kT = [None] * B
         qT = [None] * B
 
-        lam = keep.tile([P, 1], F32)
+        minus_lam = keep.tile([P, 1], F32)
 
         def compute_lam():
             products = keep.tile([P, 2, HD], F32)
@@ -127,7 +134,7 @@ def tile_differentialattention_pa_kernel(
             exp_sum = keep.tile([P, 1], F32)
             nc.scalar.activation(out=exps[:], in_=dots[:], func=ACT.Exp, accum_out=exp_sum[:])
             nc.gpsimd.tensor_scalar(
-                out=lam[:], in0=exp_sum[:], scalar1=1.0, scalar2=LAMBDA_INIT, op0=ALU.mult, op1=ALU.add
+                out=minus_lam[:], in0=exp_sum[:], scalar1=-1.0, scalar2=-LAMBDA_INIT, op0=ALU.mult, op1=ALU.add
             )
 
         wv_codes = keep.tile([P, D_PASSES, HD2], U32, align_bytes=64)
@@ -193,35 +200,32 @@ def tile_differentialattention_pa_kernel(
                 out=x_codes[g][:, t, :].bitcast(FP8X4), scales=x_scales[g][:, t, :], in_=x_grouped[tile][:]
             )
 
-        def project_chunk(g):
-            v_sums[g] = []
-            for half in range(2):
-                sums = psum.tile([P, PACK, HD], F32, tag="bank")
-                for t in range(PACK):
-                    for c in range(D_PASSES):
-                        tokens = slice(c * P, (c + 1) * P)
-                        columns = slice(half * HD, (half + 1) * HD)
-                        nc.tensor.matmul_mx(
-                            out=sums[:, t, :],
-                            lhsT=x_codes[g][:, t, tokens].bitcast(FP8X4),
-                            lhsT_scale=x_scales[g][:, t, tokens],
-                            rhs=wv_codes[:, c, columns].bitcast(FP8X4),
-                            rhs_scale=wv_scales[:, c, columns],
-                            start=(c == 0),
-                            stop=(c == D_PASSES - 1),
-                        )
-                v_sums[g].append(sums)
+        def project_chunk(g, half):
+            sums = psum.tile([P, PACK, HD], F32, tag="bank")
+            for t in range(PACK):
+                for c in range(D_PASSES):
+                    tokens = slice(c * P, (c + 1) * P)
+                    columns = slice(half * HD, (half + 1) * HD)
+                    nc.tensor.matmul_mx(
+                        out=sums[:, t, :],
+                        lhsT=x_codes[g][:, t, tokens].bitcast(FP8X4),
+                        lhsT_scale=x_scales[g][:, t, tokens],
+                        rhs=wv_codes[:, c, columns].bitcast(FP8X4),
+                        rhs_scale=wv_scales[:, c, columns],
+                        start=(c == 0),
+                        stop=(c == D_PASSES - 1),
+                    )
+            v_sums[g, half] = sums
 
         v_grouped = {}
 
-        def group_v(g):
-            grouped = work.tile([P, HD2, PACK], BF16, align_bytes=64, name="v_grouped")
-            for half in range(2):
-                nc.vector.tensor_copy(
-                    out=grouped[:, half * HD : (half + 1) * HD, :],
-                    in_=v_sums[g][half][:].rearrange("p t n -> p n t"),
-                )
-            v_grouped[g] = grouped
+        def group_v(g, half):
+            if half == 0:
+                v_grouped[g] = work.tile([P, HD2, PACK], BF16, align_bytes=64, name="v_grouped")
+            nc.vector.tensor_copy(
+                out=v_grouped[g][:, half * HD : (half + 1) * HD, :],
+                in_=v_sums[g, half][:].rearrange("p t n -> p n t"),
+            )
 
         def quantise_v(g):
             nc.vector.quantize_mx(
@@ -233,7 +237,6 @@ def tile_differentialattention_pa_kernel(
         scores = {}
         exponentials = {}
         exp_sums = {}
-        attn_rows = {}
         attn_flipped = {}
         attn_grouped = {}
         out_sums = {}
@@ -270,9 +273,24 @@ def tile_differentialattention_pa_kernel(
 
         def exponentiate(i, half):
             if half == 0:
-                exponentials[i] = work.tile([P, 2, S], F32, name="expo", bufs=DIFFERENCE_LAG + 2)
+                exponentials[i] = work.tile([P, 2, S], F32, name="expo", bufs=5)
                 exp_sums[i] = stats.tile([P, 2 * KEY_BANKS], F32, name="sums")
+            for key_bank in range(KEY_BANKS):
+                column = half * KEY_BANKS + key_bank
+                nc.scalar.activation(
+                    out=exponentials[i][:, half, key_bank * BANK : (key_bank + 1) * BANK],
+                    in_=scores[i][column][:],
+                    func=ACT.Exp,
+                    bias=shifts[i, half][:],
+                    scale=SCALE,
+                    accum_out=exp_sums[i][:, column : column + 1],
+                )
+
+        shifts = {}
+
+        def find_shift(i, half):
             shift = stats.tile([P, 1], F32)
+            shifts[i, half] = shift
             nc.vector.tensor_scalar(
                 out=shift[:],
                 in0=peaks[i, half][:, 0:1],
@@ -281,19 +299,8 @@ def tile_differentialattention_pa_kernel(
                 op0=ALU.max,
                 op1=ALU.mult,
             )
-            for key_bank in range(KEY_BANKS):
-                column = half * KEY_BANKS + key_bank
-                nc.scalar.activation(
-                    out=exponentials[i][:, half, key_bank * BANK : (key_bank + 1) * BANK],
-                    in_=scores[i][column][:],
-                    func=ACT.Exp,
-                    bias=shift[:],
-                    scale=SCALE,
-                    accum_out=exp_sums[i][:, column : column + 1],
-                )
 
         totals = {}
-        inverses = {}
 
         def add_row_sums(i):
             totals[i] = stats.tile([P, 2], F32, name="totals")
@@ -304,61 +311,58 @@ def tile_differentialattention_pa_kernel(
                 op=ALU.add,
             )
 
-        def scale_second_half(i):
-            expo = exponentials[i]
-            inverse = stats.tile([P, 2], F32)
-            nc.vector.reciprocal(out=inverse[:], in_=totals[i][:])
-            scaler = nc.gpsimd if i < QUERY_TILES - DIFFERENCE_LAG else nc.vector
-            scaler.tensor_scalar(
-                out=expo[:, 1, :],
-                in0=expo[:, 1, :],
-                scalar1=inverse[:, 1:2],
-                scalar2=lam[:, 0:1],
-                op0=ALU.mult,
-                op1=ALU.mult,
-            )
-            inverses[i] = inverse
+        inverses = {}
 
-        def difference(i):
+        def invert_row_sums(i):
+            inverses[i] = stats.tile([P, 2], F32, name="inverse")
+            nc.vector.reciprocal(out=inverses[i][:], in_=totals[i][:])
+
+        def scale_halves(i):
             expo = exponentials[i]
             inverse = inverses[i]
-            attn = work.tile([P, S], BF16)
-            nc.vector.scalar_tensor_tensor(
-                out=attn[:],
-                in0=expo[:, 0, :],
-                scalar=inverse[:, 0:1],
-                in1=expo[:, 1, :],
-                op0=ALU.mult,
-                op1=ALU.subtract,
-            )
-            attn_rows[i] = attn
+            scaler = nc.gpsimd if i < QUERY_TILES - DIFFERENCE_LAG else nc.vector
+            for half, factor in ((0, 1.0), (1, minus_lam[:, 0:1])):
+                scaler.tensor_scalar(
+                    out=expo[:, half, :],
+                    in0=expo[:, half, :],
+                    scalar1=inverse[:, half : half + 1],
+                    scalar2=factor,
+                    op0=ALU.mult,
+                    op1=ALU.mult,
+                )
 
-        def transpose_attn(i):
-            attn_words = attn_rows[i][:].bitcast(F32)
-            flipped = psum.tile([P, CHUNKS_PER_BATCH, 2, P], F32, tag="bank")
-            for key_pass in range(CHUNKS_PER_BATCH):
-                for u in range(2):
-                    first_word = (2 * key_pass + u) * P
-                    nc.tensor.transpose(
-                        flipped[:, key_pass, u, :], attn_words[:, first_word : first_word + P], ident_f32[:]
+        def transpose_difference(i, key_pass):
+            expo = exponentials[i]
+            flipped = psum.tile([P, PACK, P], F32, tag="bank")
+            for t in range(PACK):
+                first_column = (key_pass * PACK + t) * P
+                for half in range(2):
+                    nc.tensor.matmul(
+                        flipped[:, t, :],
+                        lhsT=expo[:, half, first_column : first_column + P],
+                        rhs=ident_f32[:],
+                        start=(half == 0),
+                        stop=(half == 1),
+                        is_transpose=True,
                     )
-            attn_flipped[i] = flipped
+            attn_flipped[i, key_pass] = flipped
 
-        def group_attn(i):
-            grouped = work.tile([P, S], BF16, align_bytes=64, name="attn_grouped")
-            nc.scalar.copy(
-                out=grouped[:].bitcast(F32).rearrange("p (k r u) -> p k r u", k=CHUNKS_PER_BATCH, u=2),
-                in_=attn_flipped[i][:].rearrange("p k u r -> p k r u"),
+        def group_attn(i, key_pass):
+            if key_pass == 0:
+                attn_grouped[i] = work.tile([P, CHUNKS_PER_BATCH, P, PACK], BF16, align_bytes=64, name="attn_grouped")
+            copy = nc.vector.tensor_copy if key_pass == 0 else nc.scalar.copy
+            copy(
+                out=attn_grouped[i][:, key_pass, :, :],
+                in_=attn_flipped[i, key_pass][:].rearrange("p t r -> p r t"),
             )
-            attn_grouped[i] = grouped
 
         def quantise_attn(i):
-            attn_codes[i] = work.tile([P, CHUNKS_PER_BATCH, P], U32, align_bytes=64, bufs=6, name="attn_codes")
-            attn_scales[i] = work.tile([P, CHUNKS_PER_BATCH, P], U8, align_bytes=64, bufs=6, name="attn_scales")
+            attn_codes[i] = work.tile([P, CHUNKS_PER_BATCH, P], U32, align_bytes=64, bufs=10, name="attn_codes")
+            attn_scales[i] = work.tile([P, CHUNKS_PER_BATCH, P], U8, align_bytes=64, bufs=10, name="attn_scales")
             nc.vector.quantize_mx(
                 out=attn_codes[i][:].rearrange("p k r -> p (k r)").bitcast(FP8X4),
                 scales=attn_scales[i][:].rearrange("p k r -> p (k r)"),
-                in_=attn_grouped[i][:],
+                in_=attn_grouped[i][:].rearrange("p k r t -> p (k r t)"),
             )
 
         def multiply_attn_v(i):
@@ -379,76 +383,101 @@ def tile_differentialattention_pa_kernel(
 
         def store_out(i):
             b, tile_in_batch = divmod(i, TILES_PER_BATCH)
-            out_rows = work.tile([P, HD2], F32)
+            out_rows = work.tile([P, HD2], F32, bufs=6)
             nc.scalar.copy(out=out_rows[:], in_=out_sums[i][:])
             nc.sync.dma_start(out=out[b].rearrange("(p s) n -> s p n", p=P)[tile_in_batch], in_=out_rows[:])
 
         kT[0] = keep_tokens("kT0", transpose_tokens(k_rows[0]))
         qT[0] = keep_tokens("qT0", transpose_tokens(q_rows[0]))
-        compute_lam()
         group_wv()
         multiply_q_k(0, 0)
         multiply_q_k(0, 1)
-        units = 2 * QUERY_TILES
-        units_multiplied = 2
-        chunks_ready = 0
+        x_half_step = [0 + tile * 4 // 3 for tile in range(X_TILES)]
+        projections = {}
+        for g in range(CHUNKS):
+            u = (x_half_step[PACK * g + PACK - 1] // 2 + 1) * 2 + 1
+            projections[u] = (g, 0)
+            projections[u + 2] = (g, 1)
         finished = 0
-        for step in range(QUERY_TILES + QUANTISE_LAG):
-            first_new = step * X_TILES_PER_STEP
-            new_x_tiles = [tile for tile in range(first_new, first_new + X_TILES_PER_STEP) if tile < X_TILES]
-            grouped_x_tiles = [tile for tile in range(first_new - X_TILES_PER_STEP, first_new) if 0 <= tile < X_TILES]
-            projected = [g for g in v_sums if g >= chunks_ready]
-            ahead = 2 if new_x_tiles or grouped_x_tiles or projected else 3
-
-            for tile in new_x_tiles[:1]:
-                transpose_x(tile)
+        quantised = 0
+        chunks_ready = 0
+        sums_waiting = None
+        multiplied = []
+        row_maximum(0, 0, 0)
+        row_maximum(0, 0, 1)
+        find_shift(0, 0)
+        x_waiting = []
+        v_waiting = []
+        for step in range(QUERY_TILES + QUANTISE_LAG + 2):
+            new_x = [[tile for tile in range(X_TILES) if x_half_step[tile] == 2 * step + half] for half in range(2)]
+            if step + 1 < QUERY_TILES:
+                multiply_q_k(step + 1, 0)
             if step < QUERY_TILES:
-                row_maximum(step, 0, 0)
-                row_maximum(step, 0, 1)
                 row_maximum(step, 1, 0)
-                exponentiate(step, 0)
                 row_maximum(step, 1, 1)
-            while units_multiplied <= min(2 * step + ahead, units - 1):
-                multiply_q_k(units_multiplied // 2, units_multiplied % 2)
-                units_multiplied += 1
-            if 0 <= step - DIFFERENCE_LAG < QUERY_TILES:
-                difference(step - DIFFERENCE_LAG)
-                transpose_attn(step - DIFFERENCE_LAG)
-            if step < QUERY_TILES:
-                exponentiate(step, 1)
-            if step == 0:
-                kT[1] = keep_tokens("kT1", transpose_tokens(k_rows[1]))
-                qT[1] = keep_tokens("qT1", transpose_tokens(q_rows[1]))
             if 0 <= step - SUMS_LAG < QUERY_TILES:
                 add_row_sums(step - SUMS_LAG)
-            if 0 <= step - QUANTISE_LAG < QUERY_TILES:
-                quantise_attn(step - QUANTISE_LAG)
-            while units_multiplied <= min(2 * step + 1 + ahead, units - 1):
-                multiply_q_k(units_multiplied // 2, units_multiplied % 2)
-                units_multiplied += 1
-            for tile in new_x_tiles[:1]:
-                group_x(tile)
-            if 0 <= step - DIFFERENCE_LAG < QUERY_TILES:
-                group_attn(step - DIFFERENCE_LAG)
-            for turn in range(FINISHES_PER_STEP):
-                chunks_needed = (finished // TILES_PER_BATCH + 1) * CHUNKS_PER_BATCH
-                if finished <= step - QUANTISE_LAG and chunks_ready >= chunks_needed:
-                    multiply_attn_v(finished)
-                    store_out(finished)
-                    finished += 1
-            for tile in new_x_tiles[1:]:
+            if step < QUERY_TILES:
+                find_shift(step, 1)
+                exponentiate(step, 0)
+            for tile in new_x[0]:
                 transpose_x(tile)
-                group_x(tile)
-            if grouped_x_tiles and grouped_x_tiles[-1] == PACK - 1:
+            if 0 <= step - DIFFERENCE_LAG < QUERY_TILES:
+                transpose_difference(step - DIFFERENCE_LAG, 0)
+                transpose_difference(step - DIFFERENCE_LAG, 1)
+            if sums_waiting:
+                group_v(*sums_waiting)
+                if sums_waiting[1] == 1:
+                    v_waiting.append(sums_waiting[0])
+            sums_waiting = projections.get(2 * step)
+            if sums_waiting:
+                project_chunk(*sums_waiting)
+            if step == 2:
                 quantise_wv()
-            for tile in grouped_x_tiles:
+            for tile in x_waiting:
                 quantise_x(tile)
-            for g in projected:
-                group_v(g)
+            for g in v_waiting:
                 quantise_v(g)
                 chunks_ready += 1
+            v_waiting = []
+            if 0 <= step - QUANTISE_LAG < QUERY_TILES:
+                quantise_attn(step - QUANTISE_LAG)
+                quantised += 1
             if 0 <= step - SUMS_LAG < QUERY_TILES:
-                scale_second_half(step - SUMS_LAG)
-            for tile in grouped_x_tiles:
-                if tile % PACK == PACK - 1:
-                    project_chunk(tile // PACK)
+                invert_row_sums(step - SUMS_LAG)
+                scale_halves(step - SUMS_LAG)
+            for i in multiplied:
+                store_out(i)
+            multiplied = []
+            for tile in new_x[0]:
+                group_x(tile)
+            for turn in range(1 if step < 12 else 2):
+                chunks_needed = (finished // TILES_PER_BATCH + 1) * CHUNKS_PER_BATCH
+                if finished < quantised and chunks_ready >= chunks_needed:
+                    multiply_attn_v(finished)
+                    multiplied.append(finished)
+                    finished += 1
+            if step + 1 < QUERY_TILES:
+                multiply_q_k(step + 1, 1)
+            for tile in new_x[1]:
+                transpose_x(tile)
+            if step + 1 < QUERY_TILES:
+                row_maximum(step + 1, 0, 0)
+                row_maximum(step + 1, 0, 1)
+                find_shift(step + 1, 0)
+            if 0 <= step - DIFFERENCE_LAG < QUERY_TILES:
+                group_attn(step - DIFFERENCE_LAG, 0)
+            sums_waiting = projections.get(2 * step + 1)
+            if sums_waiting:
+                project_chunk(*sums_waiting)
+            if step < QUERY_TILES:
+                exponentiate(step, 1)
+            if 0 <= step - DIFFERENCE_LAG < QUERY_TILES:
+                group_attn(step - DIFFERENCE_LAG, 1)
+            for tile in new_x[1]:
+                group_x(tile)
+            x_waiting = new_x[0] + new_x[1]
+            if step == 0:
+                compute_lam()
+                kT[1] = keep_tokens("kT1", transpose_tokens(k_rows[1]))
+                qT[1] = keep_tokens("qT1", transpose_tokens(q_rows[1]))

@@ -124,6 +124,8 @@ def tile_differentialattention_pa_kernel(
         qT = [None] * B
 
         minus_lam = keep.tile([P, 1], F32)
+        one = keep.tile([P, 1], F32)
+        nc.gpsimd.memset(one[:], 1.0)
 
         def compute_lam():
             products = keep.tile([P, 2, HD], F32)
@@ -321,7 +323,7 @@ def tile_differentialattention_pa_kernel(
             expo = exponentials[i]
             inverse = inverses[i]
             scaler = nc.gpsimd if i < QUERY_TILES - DIFFERENCE_LAG else nc.vector
-            for half, factor in ((0, 1.0), (1, minus_lam[:, 0:1])):
+            for half, factor in ((0, one[:, 0:1]), (1, minus_lam[:, 0:1])):
                 scaler.tensor_scalar(
                     out=expo[:, half, :],
                     in0=expo[:, half, :],
@@ -331,21 +333,22 @@ def tile_differentialattention_pa_kernel(
                     op1=ALU.mult,
                 )
 
-        def transpose_difference(i, key_pass):
+        def transpose_difference(i):
             expo = exponentials[i]
-            flipped = psum.tile([P, PACK, P], F32, tag="bank")
+            for key_pass in range(CHUNKS_PER_BATCH):
+                attn_flipped[i, key_pass] = psum.tile([P, PACK, P], F32, tag="bank", name="attn_bank")
             for t in range(PACK):
-                first_column = (key_pass * PACK + t) * P
                 for half in range(2):
-                    nc.tensor.matmul(
-                        flipped[:, t, :],
-                        lhsT=expo[:, half, first_column : first_column + P],
-                        rhs=ident_f32[:],
-                        start=(half == 0),
-                        stop=(half == 1),
-                        is_transpose=True,
-                    )
-            attn_flipped[i, key_pass] = flipped
+                    for key_pass in range(CHUNKS_PER_BATCH):
+                        first_column = (key_pass * PACK + t) * P
+                        nc.tensor.matmul(
+                            attn_flipped[i, key_pass][:, t, :],
+                            lhsT=expo[:, half, first_column : first_column + P],
+                            rhs=ident_f32[:],
+                            start=(half == 0),
+                            stop=(half == 1),
+                            is_transpose=True,
+                        )
 
         def group_attn(i, key_pass):
             if key_pass == 0:
@@ -423,8 +426,7 @@ def tile_differentialattention_pa_kernel(
             for tile in new_x[0]:
                 transpose_x(tile)
             if 0 <= step - DIFFERENCE_LAG < QUERY_TILES:
-                transpose_difference(step - DIFFERENCE_LAG, 0)
-                transpose_difference(step - DIFFERENCE_LAG, 1)
+                transpose_difference(step - DIFFERENCE_LAG)
             if sums_waiting:
                 group_v(*sums_waiting)
                 if sums_waiting[1] == 1:

@@ -60,76 +60,70 @@ def tile_differentialattention_pa_kernel(
         nc.scalar.dma_start(out=lambda_q[:, 1, :], in_=lambda_q2.partition_broadcast(P))
         nc.scalar.dma_start(out=lambda_k[:, 1, :], in_=lambda_k2.partition_broadcast(P))
 
-        def load_keys(b):
-            rows = keep.tile([P, TILES_PER_BATCH, HD2], BF16, name="k_rows%d" % b)
+        def load_keys(b, g):
             nc.sync.dma_start(
-                out=rows[:].rearrange("p (g t) h -> p g (t h)", t=PACK),
-                in_=k[b].rearrange("(g p t) h -> p g (t h)", p=P, t=PACK),
+                out=k_rows[b][:, g * PACK : (g + 1) * PACK, :].rearrange("p t h -> p (t h)"),
+                in_=k[b, g * CHUNK : (g + 1) * CHUNK, :].rearrange("(p t) h -> p (t h)", t=PACK),
             )
-            return rows
 
-        def load_queries(b):
-            rows = keep.tile([P, TILES_PER_BATCH, HD2], BF16, name="q_rows%d" % b)
-            nc.sync.dma_start(out=rows[:], in_=q[b].rearrange("(p s) h -> p s h", p=P))
-            return rows
+        def load_queries(b, tiles):
+            nc.sync.dma_start(
+                out=q_rows[b][:, tiles, :], in_=q[b].rearrange("(p s) h -> p s h", p=P)[:, tiles, :]
+            )
 
-        def load_x(rows, g, u):
+        def load_x(g, tiles):
+            columns = slice(tiles.start * D, tiles.stop * D)
             chunk = x_flat[g * CHUNK : (g + 1) * CHUNK, :].rearrange("(p t) d -> p (t d)", t=PACK)
-            nc.sync.dma_start(
-                out=rows[:, u * 2 * D : (u + 1) * 2 * D], in_=chunk[:, u * 2 * D : (u + 1) * 2 * D]
-            )
+            nc.sync.dma_start(out=x_rows[g][:, columns], in_=chunk[:, columns])
 
         x_flat = x.flatten_outer_dims()
         x_rows = [keep.tile([P, PACK * D], BF16, name="x_rows%d" % g) for g in range(CHUNKS)]
         wv_rows = keep.tile([P, D_PASSES, PACK, HD2], BF16)
-        k_rows = [None] * B
-        q_rows = [None] * B
-        k_rows[0] = load_keys(0)
-        q_rows[0] = load_queries(0)
+        k_rows = [keep.tile([P, TILES_PER_BATCH, HD2], BF16, name="k_rows%d" % b) for b in range(B)]
+        q_rows = [keep.tile([P, TILES_PER_BATCH, HD2], BF16, name="q_rows%d" % b) for b in range(B)]
+        load_keys(0, 0)
+        load_queries(0, slice(0, 2))
+        load_keys(0, 1)
+        load_queries(0, slice(2, TILES_PER_BATCH))
+        load_x(0, slice(0, 1))
+        load_x(0, slice(1, 2))
         nc.sync.dma_start(
             out=wv_rows[:].rearrange("p c (u e) n -> p (c u) (e n)", e=2),
             in_=WV.rearrange("(s p e) n -> p s (e n)", p=P, e=2),
         )
-        load_x(x_rows[0], 0, 0)
-        k_rows[1] = load_keys(1)
-        q_rows[1] = load_queries(1)
-        load_x(x_rows[0], 0, 1)
+        load_x(0, slice(2, PACK))
+        for g in range(CHUNKS_PER_BATCH):
+            load_keys(1, g)
+        load_queries(1, slice(0, TILES_PER_BATCH))
         for g in range(1, CHUNKS):
-            for u in range(2):
-                load_x(x_rows[g], g, u)
+            for t in range(0, PACK, 2):
+                load_x(g, slice(t, t + 2))
 
         ident_bf16 = keep.tile([P, P], BF16)
         make_identity(nc, ident_bf16[:])
         ident_f32 = keep.tile([P, P], F32)
         make_identity(nc, ident_f32[:])
 
-        def transpose_tokens(rows):
-            banks = []
-            for half in range(2):
-                flipped = psum.tile([P, TILES_PER_BATCH, P], BF16, tag="bank")
-                for s in range(TILES_PER_BATCH):
-                    nc.tensor.transpose(
-                        flipped[:, s, :], rows[:, s, half * HD : (half + 1) * HD], ident_bf16[:]
-                    )
-                banks.append(flipped)
-            return banks
+        def flip_tokens(rows, flipped_sb, half, tiles, copy):
+            flipped = psum.tile([P, len(tiles), P], BF16, tag="bank")
+            for j, s in enumerate(tiles):
+                nc.tensor.transpose(flipped[:, j, :], rows[:, s, half * HD : (half + 1) * HD], ident_bf16[:])
+            copy(
+                out=flipped_sb[:, half, tiles.start * P : tiles.stop * P],
+                in_=flipped[:].rearrange("p s r -> p (s r)"),
+            )
 
-        def keep_tokens(name, banks):
-            flipped_sb = keep.tile([P, 2, S], BF16, name=name)
-            nc.vector.tensor_copy(out=flipped_sb[:, 0, :], in_=banks[0][:].rearrange("p s r -> p (s r)"))
-            nc.scalar.copy(out=flipped_sb[:, 1, :], in_=banks[1][:].rearrange("p s r -> p (s r)"))
-            return flipped_sb
-
-        kT = [None] * B
-        qT = [None] * B
+        kT = [keep.tile([P, 2, S], BF16, name="kT%d" % b) for b in range(B)]
+        qT = [keep.tile([P, 2, S], BF16, name="qT%d" % b) for b in range(B)]
 
         minus_lam = keep.tile([P, 1], F32)
-        one = keep.tile([P, 1], F32)
-        nc.gpsimd.memset(one[:], 1.0)
+
+        products = keep.tile([P, 2, HD], F32)
+
+        def multiply_lambdas():
+            nc.gpsimd.tensor_tensor(out=products[:], in0=lambda_q[:], in1=lambda_k[:], op=ALU.mult)
 
         def compute_lam():
-            products = keep.tile([P, 2, HD], F32)
-            nc.vector.tensor_tensor(out=products[:], in0=lambda_q[:], in1=lambda_k[:], op=ALU.mult)
             dots = keep.tile([P, 2], F32)
             nc.vector.tensor_reduce(out=dots[:], in_=products[:], axis=AXIS.X, op=ALU.add)
             exps = keep.tile([P, 2], F32)
@@ -323,7 +317,7 @@ def tile_differentialattention_pa_kernel(
             expo = exponentials[i]
             inverse = inverses[i]
             scaler = nc.gpsimd if i < QUERY_TILES - DIFFERENCE_LAG else nc.vector
-            for half, factor in ((0, one[:, 0:1]), (1, minus_lam[:, 0:1])):
+            for half, factor in ((0, 1.0), (1, minus_lam[:, 0:1])):
                 scaler.tensor_scalar(
                     out=expo[:, half, :],
                     in0=expo[:, half, :],
@@ -333,13 +327,13 @@ def tile_differentialattention_pa_kernel(
                     op1=ALU.mult,
                 )
 
-        def transpose_difference(i):
+        def transpose_difference(i, key_passes):
             expo = exponentials[i]
-            for key_pass in range(CHUNKS_PER_BATCH):
+            for key_pass in key_passes:
                 attn_flipped[i, key_pass] = psum.tile([P, PACK, P], F32, tag="bank", name="attn_bank")
             for t in range(PACK):
                 for half in range(2):
-                    for key_pass in range(CHUNKS_PER_BATCH):
+                    for key_pass in key_passes:
                         first_column = (key_pass * PACK + t) * P
                         nc.tensor.matmul(
                             attn_flipped[i, key_pass][:, t, :],
@@ -350,13 +344,47 @@ def tile_differentialattention_pa_kernel(
                             is_transpose=True,
                         )
 
-        def group_attn(i, key_pass):
-            if key_pass == 0:
+        def group_attn(i, key_pass, copy):
+            if i not in attn_grouped:
                 attn_grouped[i] = work.tile([P, CHUNKS_PER_BATCH, P, PACK], BF16, align_bytes=64, name="attn_grouped")
-            copy = nc.vector.tensor_copy if key_pass == 0 else nc.scalar.copy
             copy(
                 out=attn_grouped[i][:, key_pass, :, :],
                 in_=attn_flipped[i, key_pass][:].rearrange("p t r -> p r t"),
+            )
+
+        last_totals = {}
+        last_inverses = {}
+
+        def add_half_sum(i, half):
+            total = stats.tile([P, 1], F32, name="half_total")
+            nc.vector.tensor_reduce(
+                out=total[:], in_=exp_sums[i][:, half * KEY_BANKS : (half + 1) * KEY_BANKS], axis=AXIS.X, op=ALU.add
+            )
+            last_totals[half] = total
+
+        def invert_half_sum(i, half):
+            last_inverses[half] = stats.tile([P, 1], F32, name="half_inverse")
+            nc.vector.reciprocal(out=last_inverses[half][:], in_=last_totals[half][:])
+
+        def scale_half(i, half, columns):
+            factor = minus_lam[:, 0:1] if half else 1.0
+            nc.vector.tensor_scalar(
+                out=exponentials[i][:, half, columns],
+                in0=exponentials[i][:, half, columns],
+                scalar1=last_inverses[half][:],
+                scalar2=factor,
+                op0=ALU.mult,
+                op1=ALU.mult,
+            )
+
+        def quantise_key_pass(i, key_pass):
+            if key_pass == 0:
+                attn_codes[i] = work.tile([P, CHUNKS_PER_BATCH, P], U32, align_bytes=64, bufs=10, name="attn_codes")
+                attn_scales[i] = work.tile([P, CHUNKS_PER_BATCH, P], U8, align_bytes=64, bufs=10, name="attn_scales")
+            nc.vector.quantize_mx(
+                out=attn_codes[i][:, key_pass, :].bitcast(FP8X4),
+                scales=attn_scales[i][:, key_pass, :],
+                in_=attn_grouped[i][:, key_pass, :, :].rearrange("p r t -> p (r t)"),
             )
 
         def quantise_attn(i):
@@ -390,70 +418,87 @@ def tile_differentialattention_pa_kernel(
             nc.scalar.copy(out=out_rows[:], in_=out_sums[i][:])
             nc.sync.dma_start(out=out[b].rearrange("(p s) n -> s p n", p=P)[tile_in_batch], in_=out_rows[:])
 
-        kT[0] = keep_tokens("kT0", transpose_tokens(k_rows[0]))
-        qT[0] = keep_tokens("qT0", transpose_tokens(q_rows[0]))
-        group_wv()
+        first_chunk = range(PACK)
+        second_chunk = range(PACK, 2 * PACK)
+        all_tiles = range(TILES_PER_BATCH)
+        flip_tokens(k_rows[0], kT[0], 0, first_chunk, nc.vector.tensor_copy)
+        flip_tokens(q_rows[0], qT[0], 0, range(2), nc.scalar.copy)
+        flip_tokens(k_rows[0], kT[0], 0, second_chunk, nc.vector.tensor_copy)
+        flip_tokens(q_rows[0], qT[0], 1, range(2), nc.scalar.copy)
+        flip_tokens(k_rows[0], kT[0], 1, first_chunk, nc.scalar.copy)
         multiply_q_k(0, 0)
+        flip_tokens(k_rows[0], kT[0], 1, second_chunk, nc.scalar.copy)
         multiply_q_k(0, 1)
-        x_half_step = [0 + tile * 4 // 3 for tile in range(X_TILES)]
+        x_half_step = [0 + tile * 3 // 2 for tile in range(X_TILES)]
         projections = {}
         for g in range(CHUNKS):
-            u = (x_half_step[PACK * g + PACK - 1] // 2 + 1) * 2 + 1
-            projections[u] = (g, 0)
-            projections[u + 2] = (g, 1)
+            last_step = x_half_step[PACK * g + PACK - 1] // 2
+            projections[2 * (last_step + 1) + 1] = (g, 0)
+            projections[2 * (last_step + 2) + 1] = (g, 1)
         finished = 0
         quantised = 0
         chunks_ready = 0
-        sums_waiting = None
+        in_psum = None
         multiplied = []
-        row_maximum(0, 0, 0)
-        row_maximum(0, 0, 1)
-        find_shift(0, 0)
         x_waiting = []
         v_waiting = []
-        for step in range(QUERY_TILES + QUANTISE_LAG + 2):
+        row_maximum(0, 0, 0)
+        row_maximum(0, 0, 1)
+        row_maximum(0, 1, 0)
+        find_shift(0, 0)
+        row_maximum(0, 1, 1)
+        multiply_lambdas()
+        group_wv()
+        last = QUERY_TILES - 1
+        for step in range(QUERY_TILES):
             new_x = [[tile for tile in range(X_TILES) if x_half_step[tile] == 2 * step + half] for half in range(2)]
             if step + 1 < QUERY_TILES:
                 multiply_q_k(step + 1, 0)
-            if step < QUERY_TILES:
+            if 0 < step < QUERY_TILES:
                 row_maximum(step, 1, 0)
-                row_maximum(step, 1, 1)
             if 0 <= step - SUMS_LAG < QUERY_TILES:
                 add_row_sums(step - SUMS_LAG)
+            if 0 < step < QUERY_TILES:
+                row_maximum(step, 1, 1)
             if step < QUERY_TILES:
-                find_shift(step, 1)
                 exponentiate(step, 0)
             for tile in new_x[0]:
                 transpose_x(tile)
             if 0 <= step - DIFFERENCE_LAG < QUERY_TILES:
-                transpose_difference(step - DIFFERENCE_LAG)
-            if sums_waiting:
-                group_v(*sums_waiting)
-                if sums_waiting[1] == 1:
-                    v_waiting.append(sums_waiting[0])
-            sums_waiting = projections.get(2 * step)
-            if sums_waiting:
-                project_chunk(*sums_waiting)
+                transpose_difference(step - DIFFERENCE_LAG, range(CHUNKS_PER_BATCH))
             if step == 2:
                 quantise_wv()
-            for tile in x_waiting:
+            if x_waiting:
+                quantise_x(x_waiting[0])
+            elif 0 <= step - QUANTISE_LAG < QUERY_TILES:
+                quantise_attn(step - QUANTISE_LAG)
+                quantised += 1
+            if step < QUERY_TILES:
+                find_shift(step, 1)
+            for tile in x_waiting[1:]:
                 quantise_x(tile)
+            if x_waiting and 0 <= step - QUANTISE_LAG < QUERY_TILES:
+                quantise_attn(step - QUANTISE_LAG)
+                quantised += 1
             for g in v_waiting:
                 quantise_v(g)
                 chunks_ready += 1
             v_waiting = []
-            if 0 <= step - QUANTISE_LAG < QUERY_TILES:
-                quantise_attn(step - QUANTISE_LAG)
-                quantised += 1
             if 0 <= step - SUMS_LAG < QUERY_TILES:
                 invert_row_sums(step - SUMS_LAG)
                 scale_halves(step - SUMS_LAG)
+            if in_psum:
+                group_v(*in_psum)
+                if in_psum[1] == 1:
+                    v_waiting.append(in_psum[0])
             for i in multiplied:
                 store_out(i)
             multiplied = []
             for tile in new_x[0]:
                 group_x(tile)
-            for turn in range(1 if step < 12 else 2):
+            if step == last:
+                break
+            for turn in range(1 if step < last - 1 else FINISHES_PER_STEP):
                 chunks_needed = (finished // TILES_PER_BATCH + 1) * CHUNKS_PER_BATCH
                 if finished < quantised and chunks_ready >= chunks_needed:
                     multiply_attn_v(finished)
@@ -466,20 +511,58 @@ def tile_differentialattention_pa_kernel(
             if step + 1 < QUERY_TILES:
                 row_maximum(step + 1, 0, 0)
                 row_maximum(step + 1, 0, 1)
-                find_shift(step + 1, 0)
             if 0 <= step - DIFFERENCE_LAG < QUERY_TILES:
-                group_attn(step - DIFFERENCE_LAG, 0)
-            sums_waiting = projections.get(2 * step + 1)
-            if sums_waiting:
-                project_chunk(*sums_waiting)
+                group_attn(step - DIFFERENCE_LAG, 0, nc.vector.tensor_copy)
+            if step + 1 < QUERY_TILES:
+                find_shift(step + 1, 0)
+            in_psum = projections.get(2 * step + 1)
+            if in_psum:
+                project_chunk(*in_psum)
             if step < QUERY_TILES:
                 exponentiate(step, 1)
             if 0 <= step - DIFFERENCE_LAG < QUERY_TILES:
-                group_attn(step - DIFFERENCE_LAG, 1)
+                group_attn(step - DIFFERENCE_LAG, 1, nc.scalar.copy)
             for tile in new_x[1]:
                 group_x(tile)
             x_waiting = new_x[0] + new_x[1]
             if step == 0:
                 compute_lam()
-                kT[1] = keep_tokens("kT1", transpose_tokens(k_rows[1]))
-                qT[1] = keep_tokens("qT1", transpose_tokens(q_rows[1]))
+            if step == 0:
+                flip_tokens(q_rows[0], qT[0], 0, range(2, TILES_PER_BATCH), nc.vector.tensor_copy)
+                flip_tokens(q_rows[0], qT[0], 1, range(2, TILES_PER_BATCH), nc.scalar.copy)
+            if step == 1:
+                flip_tokens(k_rows[1], kT[1], 0, all_tiles, nc.vector.tensor_copy)
+                flip_tokens(k_rows[1], kT[1], 1, all_tiles, nc.scalar.copy)
+            if step == 2:
+                flip_tokens(q_rows[1], qT[1], 0, all_tiles, nc.vector.tensor_copy)
+                flip_tokens(q_rows[1], qT[1], 1, all_tiles, nc.scalar.copy)
+        for i in range(finished, last - 2):
+            multiply_attn_v(i)
+        exponentiate(last, 1)
+        add_half_sum(last, 0)
+        group_attn(last - 2, 0, nc.vector.tensor_copy)
+        invert_half_sum(last, 0)
+        transpose_difference(last - 1, range(CHUNKS_PER_BATCH))
+        group_attn(last - 2, 1, nc.scalar.copy)
+        for i in range(finished, last - 2):
+            store_out(i)
+        add_half_sum(last, 1)
+        scale_half(last, 0, slice(0, S))
+        invert_half_sum(last, 1)
+        quantise_attn(last - 2)
+        multiply_attn_v(last - 2)
+        for key_pass in range(CHUNKS_PER_BATCH):
+            scale_half(last, 1, slice(key_pass * CHUNK, (key_pass + 1) * CHUNK))
+            transpose_difference(last, range(key_pass, key_pass + 1))
+        group_attn(last - 1, 1, nc.scalar.copy)
+        group_attn(last - 1, 0, nc.vector.tensor_copy)
+        store_out(last - 2)
+        quantise_attn(last - 1)
+        multiply_attn_v(last - 1)
+        group_attn(last, 0, nc.scalar.copy)
+        group_attn(last, 1, nc.scalar.copy)
+        for key_pass in range(CHUNKS_PER_BATCH):
+            quantise_key_pass(last, key_pass)
+        multiply_attn_v(last)
+        store_out(last - 1)
+        store_out(last)

@@ -163,29 +163,26 @@ def tile_differentialattention_pa_kernel(
         v_codes = [keep.tile([P, HD2], U32, name="v_codes%d" % g, align_bytes=64) for g in range(CHUNKS)]
         v_scales = [keep.tile([P, HD2], U8, name="v_scales%d" % g, align_bytes=64) for g in range(CHUNKS)]
 
-        def transpose_x(tile):
+        def transpose_x(tile, pair):
             g, t = divmod(tile, PACK)
             words = x_rows[g][:].bitcast(F32)
-            x_flipped[tile] = []
-            for pair in range(D_PASSES // 2):
-                flipped = psum.tile([P, 2, 2, P], F32, tag="bank")
-                for c in range(2):
-                    for u in range(2):
-                        first_word = t * (D // 2) + (2 * pair + c) * (K_PASS // 2) + u * P
-                        nc.tensor.transpose(
-                            flipped[:, c, u, :], words[:, first_word : first_word + P], ident_f32[:]
-                        )
-                x_flipped[tile].append(flipped)
+            flipped = psum.tile([P, 2, 2, P], F32, tag="bank", name="x_bank")
+            for c in range(2):
+                for u in range(2):
+                    first_word = t * (D // 2) + (2 * pair + c) * (K_PASS // 2) + u * P
+                    nc.tensor.transpose(
+                        flipped[:, c, u, :], words[:, first_word : first_word + P], ident_f32[:]
+                    )
+            x_flipped[tile, pair] = flipped
 
-        def group_x(tile):
-            grouped = work.tile([P, D_PASSES * P * PACK], BF16, align_bytes=64, name="x_grouped")
-            grouped_words = grouped[:].bitcast(F32).rearrange("p (c r u) -> p c r u", c=D_PASSES, u=2)
-            for pair in range(D_PASSES // 2):
-                nc.scalar.copy(
-                    out=grouped_words[:, 2 * pair : 2 * pair + 2, :, :],
-                    in_=x_flipped[tile][pair][:].rearrange("p c u r -> p c r u"),
-                )
-            x_grouped[tile] = grouped
+        def group_x(tile, pair):
+            if pair == 0:
+                x_grouped[tile] = work.tile([P, D_PASSES * P * PACK], BF16, align_bytes=64, name="x_grouped")
+            grouped_words = x_grouped[tile][:].bitcast(F32).rearrange("p (c r u) -> p c r u", c=D_PASSES, u=2)
+            nc.scalar.copy(
+                out=grouped_words[:, 2 * pair : 2 * pair + 2, :, :],
+                in_=x_flipped[tile, pair][:].rearrange("p c u r -> p c r u"),
+            )
 
         def quantise_x(tile):
             g, t = divmod(tile, PACK)
@@ -196,14 +193,15 @@ def tile_differentialattention_pa_kernel(
                 out=x_codes[g][:, t, :].bitcast(FP8X4), scales=x_scales[g][:, t, :], in_=x_grouped[tile][:]
             )
 
-        def project_chunk(g, half):
-            sums = psum.tile([P, PACK, HD], F32, tag="bank")
-            for t in range(PACK):
+        def project_tokens(g, half, tiles):
+            if tiles.start == 0:
+                v_sums[g, half] = psum.tile([P, PACK, HD], F32, tag="bank", name="v_bank")
+            for t in tiles:
                 for c in range(D_PASSES):
                     tokens = slice(c * P, (c + 1) * P)
                     columns = slice(half * HD, (half + 1) * HD)
                     nc.tensor.matmul_mx(
-                        out=sums[:, t, :],
+                        out=v_sums[g, half][:, t, :],
                         lhsT=x_codes[g][:, t, tokens].bitcast(FP8X4),
                         lhsT_scale=x_scales[g][:, t, tokens],
                         rhs=wv_codes[:, c, columns].bitcast(FP8X4),
@@ -211,7 +209,6 @@ def tile_differentialattention_pa_kernel(
                         start=(c == 0),
                         stop=(c == D_PASSES - 1),
                     )
-            v_sums[g, half] = sums
 
         v_grouped = {}
 
@@ -239,21 +236,18 @@ def tile_differentialattention_pa_kernel(
         attn_codes = {}
         attn_scales = {}
 
-        def multiply_q_k(i, half):
+        def multiply_q_k(i, half, key_bank):
             b, tile_in_batch = divmod(i, TILES_PER_BATCH)
             queries = slice(tile_in_batch * P, (tile_in_batch + 1) * P)
-            if half == 0:
-                scores[i] = []
-            for key_bank in range(KEY_BANKS):
-                bank = psum.tile([P, BANK], F32, tag="bank")
-                nc.tensor.matmul(
-                    bank[:],
-                    lhsT=qT[b][:, half, queries],
-                    rhs=kT[b][:, half, key_bank * BANK : (key_bank + 1) * BANK],
-                    start=True,
-                    stop=True,
-                )
-                scores[i].append(bank)
+            bank = psum.tile([P, BANK], F32, tag="bank", name="scores_bank")
+            nc.tensor.matmul(
+                bank[:],
+                lhsT=qT[b][:, half, queries],
+                rhs=kT[b][:, half, key_bank * BANK : (key_bank + 1) * BANK],
+                start=True,
+                stop=True,
+            )
+            scores[i, half, key_bank] = bank
 
         peaks = {}
 
@@ -262,7 +256,7 @@ def tile_differentialattention_pa_kernel(
                 peaks[i, half] = stats.tile([P, KEY_BANKS], F32, name="peaks")
             nc.vector.tensor_reduce(
                 out=peaks[i, half][:, key_bank : key_bank + 1],
-                in_=scores[i][half * KEY_BANKS + key_bank][:],
+                in_=scores[i, half, key_bank][:],
                 axis=AXIS.X,
                 op=ALU.max,
             )
@@ -275,7 +269,7 @@ def tile_differentialattention_pa_kernel(
                 column = half * KEY_BANKS + key_bank
                 nc.scalar.activation(
                     out=exponentials[i][:, half, key_bank * BANK : (key_bank + 1) * BANK],
-                    in_=scores[i][column][:],
+                    in_=scores[i, half, key_bank][:],
                     func=ACT.Exp,
                     bias=shifts[i, half][:],
                     scale=SCALE,
@@ -426,21 +420,24 @@ def tile_differentialattention_pa_kernel(
         flip_tokens(k_rows[0], kT[0], 0, second_chunk, nc.vector.tensor_copy)
         flip_tokens(q_rows[0], qT[0], 1, range(2), nc.scalar.copy)
         flip_tokens(k_rows[0], kT[0], 1, first_chunk, nc.scalar.copy)
-        multiply_q_k(0, 0)
+        multiply_q_k(0, 0, 0)
+        multiply_q_k(0, 0, 1)
         flip_tokens(k_rows[0], kT[0], 1, second_chunk, nc.scalar.copy)
-        multiply_q_k(0, 1)
-        x_half_step = [0 + tile * 3 // 2 for tile in range(X_TILES)]
+        multiply_q_k(0, 1, 0)
+        multiply_q_k(0, 1, 1)
+        x_half_step = [0 + tile * 4 // 3 for tile in range(X_TILES)]
         projections = {}
         for g in range(CHUNKS):
-            last_step = x_half_step[PACK * g + PACK - 1] // 2
-            projections[2 * (last_step + 1) + 1] = (g, 0)
-            projections[2 * (last_step + 2) + 1] = (g, 1)
+            quantised_in = (x_half_step[PACK * g + PACK - 1] + 1) // 2 + 1
+            projections[2 * quantised_in + 1] = (g, 0)
+            projections[2 * quantised_in + 3] = (g, 1)
         finished = 0
         quantised = 0
         chunks_ready = 0
         in_psum = None
         multiplied = []
         x_waiting = []
+        x_late = []
         v_waiting = []
         row_maximum(0, 0, 0)
         row_maximum(0, 0, 1)
@@ -452,8 +449,20 @@ def tile_differentialattention_pa_kernel(
         last = QUERY_TILES - 1
         for step in range(QUERY_TILES):
             new_x = [[tile for tile in range(X_TILES) if x_half_step[tile] == 2 * step + half] for half in range(2)]
-            if step + 1 < QUERY_TILES:
-                multiply_q_k(step + 1, 0)
+            for tile in new_x[0]:
+                transpose_x(tile, 0)
+            for tile in new_x[0]:
+                transpose_x(tile, 1)
+            if step < last:
+                multiply_q_k(step + 1, 0, 0)
+            if step < last:
+                multiply_q_k(step + 1, 0, 1)
+            if 0 <= step - DIFFERENCE_LAG:
+                transpose_difference(step - DIFFERENCE_LAG, range(0, 1))
+            if step < last:
+                multiply_q_k(step + 1, 1, 0)
+            if 0 <= step - DIFFERENCE_LAG:
+                transpose_difference(step - DIFFERENCE_LAG, range(1, 2))
             if 0 < step < QUERY_TILES:
                 row_maximum(step, 1, 0)
             if 0 <= step - SUMS_LAG < QUERY_TILES:
@@ -462,10 +471,6 @@ def tile_differentialattention_pa_kernel(
                 row_maximum(step, 1, 1)
             if step < QUERY_TILES:
                 exponentiate(step, 0)
-            for tile in new_x[0]:
-                transpose_x(tile)
-            if 0 <= step - DIFFERENCE_LAG < QUERY_TILES:
-                transpose_difference(step - DIFFERENCE_LAG, range(CHUNKS_PER_BATCH))
             if step == 2:
                 quantise_wv()
             if x_waiting:
@@ -495,19 +500,27 @@ def tile_differentialattention_pa_kernel(
                 store_out(i)
             multiplied = []
             for tile in new_x[0]:
-                group_x(tile)
+                group_x(tile, 0)
+                group_x(tile, 1)
             if step == last:
                 break
+            in_psum = projections.get(2 * step + 1)
+            if step < last:
+                multiply_q_k(step + 1, 1, 1)
+            for tile in new_x[1]:
+                transpose_x(tile, 0)
+            for tile in new_x[1]:
+                transpose_x(tile, 1)
             for turn in range(1 if step < last - 1 else FINISHES_PER_STEP):
                 chunks_needed = (finished // TILES_PER_BATCH + 1) * CHUNKS_PER_BATCH
                 if finished < quantised and chunks_ready >= chunks_needed:
                     multiply_attn_v(finished)
                     multiplied.append(finished)
                     finished += 1
-            if step + 1 < QUERY_TILES:
-                multiply_q_k(step + 1, 1)
-            for tile in new_x[1]:
-                transpose_x(tile)
+            if in_psum:
+                project_tokens(*in_psum, range(0, 2))
+            if in_psum:
+                project_tokens(*in_psum, range(2, 4))
             if step + 1 < QUERY_TILES:
                 row_maximum(step + 1, 0, 0)
                 row_maximum(step + 1, 0, 1)
@@ -515,16 +528,15 @@ def tile_differentialattention_pa_kernel(
                 group_attn(step - DIFFERENCE_LAG, 0, nc.vector.tensor_copy)
             if step + 1 < QUERY_TILES:
                 find_shift(step + 1, 0)
-            in_psum = projections.get(2 * step + 1)
-            if in_psum:
-                project_chunk(*in_psum)
             if step < QUERY_TILES:
                 exponentiate(step, 1)
             if 0 <= step - DIFFERENCE_LAG < QUERY_TILES:
                 group_attn(step - DIFFERENCE_LAG, 1, nc.scalar.copy)
             for tile in new_x[1]:
-                group_x(tile)
-            x_waiting = new_x[0] + new_x[1]
+                group_x(tile, 0)
+                group_x(tile, 1)
+            x_waiting = x_late + new_x[0]
+            x_late = new_x[1]
             if step == 0:
                 compute_lam()
             if step == 0:

@@ -85,12 +85,12 @@ def tile_differentialattention_pa_kernel(
         load_queries(0, slice(0, 2))
         load_keys(0, 1)
         load_queries(0, slice(2, TILES_PER_BATCH))
-        load_x(0, slice(0, 1))
-        load_x(0, slice(1, 2))
         nc.sync.dma_start(
             out=wv_rows[:].rearrange("p c (u e) n -> p (c u) (e n)", e=2),
             in_=WV.rearrange("(s p e) n -> p s (e n)", p=P, e=2),
         )
+        load_x(0, slice(0, 1))
+        load_x(0, slice(1, 2))
         load_x(0, slice(2, PACK))
         for g in range(CHUNKS_PER_BATCH):
             load_keys(1, g)
@@ -307,19 +307,28 @@ def tile_differentialattention_pa_kernel(
             inverses[i] = stats.tile([P, 2], F32, name="inverse")
             nc.vector.reciprocal(out=inverses[i][:], in_=totals[i][:])
 
-        def scale_halves(i):
+        def scale_halves(i, share=0):
             expo = exponentials[i]
             inverse = inverses[i]
             scaler = nc.gpsimd if i < QUERY_TILES - DIFFERENCE_LAG else nc.vector
-            for half, factor in ((0, 1.0), (1, minus_lam[:, 0:1])):
+            for half, factor in ((1, minus_lam[:, 0:1]), (0, 1.0)):
+                first = share if half == 0 else 0
                 scaler.tensor_scalar(
-                    out=expo[:, half, :],
-                    in0=expo[:, half, :],
+                    out=expo[:, half, first:],
+                    in0=expo[:, half, first:],
                     scalar1=inverse[:, half : half + 1],
                     scalar2=factor,
                     op0=ALU.mult,
                     op1=ALU.mult,
                 )
+
+        def scale_share(i, share):
+            nc.scalar.activation(
+                out=exponentials[i][:, 0, 0:share],
+                in_=exponentials[i][:, 0, 0:share],
+                func=ACT.Copy,
+                scale=inverses[i][:, 0:1],
+            )
 
         def transpose_difference(i, key_passes):
             expo = exponentials[i]
@@ -444,8 +453,8 @@ def tile_differentialattention_pa_kernel(
         row_maximum(0, 1, 0)
         find_shift(0, 0)
         row_maximum(0, 1, 1)
-        multiply_lambdas()
         group_wv()
+        multiply_lambdas()
         last = QUERY_TILES - 1
         for step in range(QUERY_TILES):
             new_x = [[tile for tile in range(X_TILES) if x_half_step[tile] == 2 * step + half] for half in range(2)]
@@ -473,6 +482,8 @@ def tile_differentialattention_pa_kernel(
                 exponentiate(step, 0)
             if step == 2:
                 quantise_wv()
+            if step == 1:
+                compute_lam()
             if x_waiting:
                 quantise_x(x_waiting[0])
             elif 0 <= step - QUANTISE_LAG < QUERY_TILES:
@@ -491,7 +502,7 @@ def tile_differentialattention_pa_kernel(
             v_waiting = []
             if 0 <= step - SUMS_LAG < QUERY_TILES:
                 invert_row_sums(step - SUMS_LAG)
-                scale_halves(step - SUMS_LAG)
+                scale_halves(step - SUMS_LAG, 256 if step - SUMS_LAG < last - 1 else 0)
             if in_psum:
                 group_v(*in_psum)
                 if in_psum[1] == 1:
@@ -532,13 +543,13 @@ def tile_differentialattention_pa_kernel(
                 exponentiate(step, 1)
             if 0 <= step - DIFFERENCE_LAG < QUERY_TILES:
                 group_attn(step - DIFFERENCE_LAG, 1, nc.scalar.copy)
+            if 0 <= step - SUMS_LAG < last - 1 and 0 <= step - SUMS_LAG:
+                scale_share(step - SUMS_LAG, 256)
             for tile in new_x[1]:
                 group_x(tile, 0)
                 group_x(tile, 1)
             x_waiting = x_late + new_x[0]
             x_late = new_x[1]
-            if step == 0:
-                compute_lam()
             if step == 0:
                 flip_tokens(q_rows[0], qT[0], 0, range(2, TILES_PER_BATCH), nc.vector.tensor_copy)
                 flip_tokens(q_rows[0], qT[0], 1, range(2, TILES_PER_BATCH), nc.scalar.copy)

@@ -104,10 +104,13 @@ def tile_differentialattention_pa_kernel(
         ident_f32 = keep.tile([P, P], F32)
         make_identity(nc, ident_f32[:])
 
-        def flip_tokens(rows, flipped_sb, half, tiles, copy):
-            flipped = psum.tile([P, len(tiles), P], BF16, tag="bank")
+        def flip_tokens(rows, half, tiles):
+            flipped = psum.tile([P, len(tiles), P], BF16, tag="bank", name="flip_bank")
             for j, s in enumerate(tiles):
                 nc.tensor.transpose(flipped[:, j, :], rows[:, s, half * HD : (half + 1) * HD], ident_bf16[:])
+            return flipped
+
+        def keep_tokens(flipped_sb, half, tiles, flipped, copy):
             copy(
                 out=flipped_sb[:, half, tiles.start * P : tiles.stop * P],
                 in_=flipped[:].rearrange("p s r -> p (s r)"),
@@ -175,11 +178,11 @@ def tile_differentialattention_pa_kernel(
                     )
             x_flipped[tile, pair] = flipped
 
-        def group_x(tile, pair):
+        def group_x(tile, pair, copy=nc.scalar.copy):
             if pair == 0:
                 x_grouped[tile] = work.tile([P, D_PASSES * P * PACK], BF16, align_bytes=64, name="x_grouped")
             grouped_words = x_grouped[tile][:].bitcast(F32).rearrange("p (c r u) -> p c r u", c=D_PASSES, u=2)
-            nc.scalar.copy(
+            copy(
                 out=grouped_words[:, 2 * pair : 2 * pair + 2, :, :],
                 in_=x_flipped[tile, pair][:].rearrange("p c u r -> p c r u"),
             )
@@ -415,23 +418,23 @@ def tile_differentialattention_pa_kernel(
                 )
             out_sums[i] = sums
 
-        def store_out(i):
+        def store_out(i, copy=nc.scalar.copy):
             b, tile_in_batch = divmod(i, TILES_PER_BATCH)
             out_rows = work.tile([P, HD2], F32, bufs=6)
-            nc.scalar.copy(out=out_rows[:], in_=out_sums[i][:])
+            copy(out=out_rows[:], in_=out_sums[i][:])
             nc.sync.dma_start(out=out[b].rearrange("(p s) n -> s p n", p=P)[tile_in_batch], in_=out_rows[:])
 
         first_chunk = range(PACK)
         second_chunk = range(PACK, 2 * PACK)
         all_tiles = range(TILES_PER_BATCH)
-        flip_tokens(k_rows[0], kT[0], 0, first_chunk, nc.vector.tensor_copy)
-        flip_tokens(q_rows[0], qT[0], 0, range(2), nc.scalar.copy)
-        flip_tokens(k_rows[0], kT[0], 0, second_chunk, nc.vector.tensor_copy)
-        flip_tokens(q_rows[0], qT[0], 1, range(2), nc.scalar.copy)
-        flip_tokens(k_rows[0], kT[0], 1, first_chunk, nc.scalar.copy)
+        keep_tokens(kT[0], 0, first_chunk, flip_tokens(k_rows[0], 0, first_chunk), nc.vector.tensor_copy)
+        keep_tokens(qT[0], 0, range(2), flip_tokens(q_rows[0], 0, range(2)), nc.scalar.copy)
+        keep_tokens(kT[0], 0, second_chunk, flip_tokens(k_rows[0], 0, second_chunk), nc.vector.tensor_copy)
+        keep_tokens(qT[0], 1, range(2), flip_tokens(q_rows[0], 1, range(2)), nc.scalar.copy)
+        keep_tokens(kT[0], 1, first_chunk, flip_tokens(k_rows[0], 1, first_chunk), nc.scalar.copy)
         multiply_q_k(0, 0, 0)
         multiply_q_k(0, 0, 1)
-        flip_tokens(k_rows[0], kT[0], 1, second_chunk, nc.scalar.copy)
+        keep_tokens(kT[0], 1, second_chunk, flip_tokens(k_rows[0], 1, second_chunk), nc.scalar.copy)
         multiply_q_k(0, 1, 0)
         multiply_q_k(0, 1, 1)
         x_half_step = [0 + tile * 4 // 3 for tile in range(X_TILES)]
@@ -446,6 +449,12 @@ def tile_differentialattention_pa_kernel(
         in_psum = None
         multiplied = []
         x_waiting = []
+        later_tiles = {
+            0: (q_rows[0], qT[0], range(2, TILES_PER_BATCH)),
+            1: (k_rows[1], kT[1], all_tiles),
+            2: (q_rows[1], qT[1], all_tiles),
+        }
+        flipped = []
         x_late = []
         v_waiting = []
         row_maximum(0, 0, 0)
@@ -468,8 +477,6 @@ def tile_differentialattention_pa_kernel(
                 multiply_q_k(step + 1, 0, 1)
             if 0 <= step - DIFFERENCE_LAG:
                 transpose_difference(step - DIFFERENCE_LAG, range(0, 1))
-            if step < last:
-                multiply_q_k(step + 1, 1, 0)
             if 0 <= step - DIFFERENCE_LAG:
                 transpose_difference(step - DIFFERENCE_LAG, range(1, 2))
             if 0 < step < QUERY_TILES:
@@ -480,15 +487,15 @@ def tile_differentialattention_pa_kernel(
                 row_maximum(step, 1, 1)
             if step < QUERY_TILES:
                 exponentiate(step, 0)
-            if step == 2:
+            if step == 3:
                 quantise_wv()
-            if step == 1:
-                compute_lam()
             if x_waiting:
                 quantise_x(x_waiting[0])
             elif 0 <= step - QUANTISE_LAG < QUERY_TILES:
                 quantise_attn(step - QUANTISE_LAG)
                 quantised += 1
+            if step == 1:
+                compute_lam()
             if step < QUERY_TILES:
                 find_shift(step, 1)
             for tile in x_waiting[1:]:
@@ -500,7 +507,7 @@ def tile_differentialattention_pa_kernel(
                 quantise_v(g)
                 chunks_ready += 1
             v_waiting = []
-            if 0 <= step - SUMS_LAG < QUERY_TILES:
+            if 0 <= step - SUMS_LAG < last - 1:
                 invert_row_sums(step - SUMS_LAG)
                 scale_halves(step - SUMS_LAG, 256 if step - SUMS_LAG < last - 1 else 0)
             if in_psum:
@@ -512,16 +519,22 @@ def tile_differentialattention_pa_kernel(
             multiplied = []
             for tile in new_x[0]:
                 group_x(tile, 0)
-                group_x(tile, 1)
+                group_x(tile, 1, nc.vector.tensor_copy if step < 2 else nc.scalar.copy)
             if step == last:
                 break
+            flipped = []
+            if step in later_tiles:
+                rows, flipped_sb, tiles = later_tiles[step]
+                flipped = [flip_tokens(rows, half, tiles) for half in range(2)]
             in_psum = projections.get(2 * step + 1)
             if step < last:
-                multiply_q_k(step + 1, 1, 1)
+                multiply_q_k(step + 1, 1, 0)
             for tile in new_x[1]:
                 transpose_x(tile, 0)
             for tile in new_x[1]:
                 transpose_x(tile, 1)
+            if step < last:
+                multiply_q_k(step + 1, 1, 1)
             for turn in range(1 if step < last - 1 else FINISHES_PER_STEP):
                 chunks_needed = (finished // TILES_PER_BATCH + 1) * CHUNKS_PER_BATCH
                 if finished < quantised and chunks_ready >= chunks_needed:
@@ -537,12 +550,16 @@ def tile_differentialattention_pa_kernel(
                 row_maximum(step + 1, 0, 1)
             if 0 <= step - DIFFERENCE_LAG < QUERY_TILES:
                 group_attn(step - DIFFERENCE_LAG, 0, nc.vector.tensor_copy)
+            if flipped:
+                keep_tokens(flipped_sb, 0, tiles, flipped[0], nc.vector.tensor_copy)
             if step + 1 < QUERY_TILES:
                 find_shift(step + 1, 0)
             if step < QUERY_TILES:
                 exponentiate(step, 1)
             if 0 <= step - DIFFERENCE_LAG < QUERY_TILES:
                 group_attn(step - DIFFERENCE_LAG, 1, nc.scalar.copy)
+            if flipped:
+                keep_tokens(flipped_sb, 1, tiles, flipped[1], nc.vector.tensor_copy if step < 2 else nc.scalar.copy)
             if 0 <= step - SUMS_LAG < last - 1 and 0 <= step - SUMS_LAG:
                 scale_share(step - SUMS_LAG, 256)
             for tile in new_x[1]:
@@ -550,42 +567,44 @@ def tile_differentialattention_pa_kernel(
                 group_x(tile, 1)
             x_waiting = x_late + new_x[0]
             x_late = new_x[1]
-            if step == 0:
-                flip_tokens(q_rows[0], qT[0], 0, range(2, TILES_PER_BATCH), nc.vector.tensor_copy)
-                flip_tokens(q_rows[0], qT[0], 1, range(2, TILES_PER_BATCH), nc.scalar.copy)
-            if step == 1:
-                flip_tokens(k_rows[1], kT[1], 0, all_tiles, nc.vector.tensor_copy)
-                flip_tokens(k_rows[1], kT[1], 1, all_tiles, nc.scalar.copy)
-            if step == 2:
-                flip_tokens(q_rows[1], qT[1], 0, all_tiles, nc.vector.tensor_copy)
-                flip_tokens(q_rows[1], qT[1], 1, all_tiles, nc.scalar.copy)
-        for i in range(finished, last - 2):
-            multiply_attn_v(i)
+        backlog = list(range(finished, last - 2))
+        invert_row_sums(last - 1)
         exponentiate(last, 1)
         add_half_sum(last, 0)
-        group_attn(last - 2, 0, nc.vector.tensor_copy)
+        scale_halves(last - 1)
+        for i in backlog[:2]:
+            multiply_attn_v(i)
         invert_half_sum(last, 0)
         transpose_difference(last - 1, range(CHUNKS_PER_BATCH))
-        group_attn(last - 2, 1, nc.scalar.copy)
-        for i in range(finished, last - 2):
-            store_out(i)
         add_half_sum(last, 1)
         scale_half(last, 0, slice(0, S))
         invert_half_sum(last, 1)
-        quantise_attn(last - 2)
-        multiply_attn_v(last - 2)
+        group_attn(last - 2, 1, nc.scalar.copy)
+        group_attn(last - 2, 0, nc.vector.tensor_copy)
+        for i in backlog[:2]:
+            store_out(i)
+        for i in backlog[2:3]:
+            multiply_attn_v(i)
+        for i in backlog[2:3]:
+            store_out(i)
         for key_pass in range(CHUNKS_PER_BATCH):
             scale_half(last, 1, slice(key_pass * CHUNK, (key_pass + 1) * CHUNK))
             transpose_difference(last, range(key_pass, key_pass + 1))
+        quantise_attn(last - 2)
         group_attn(last - 1, 1, nc.scalar.copy)
         group_attn(last - 1, 0, nc.vector.tensor_copy)
-        store_out(last - 2)
+        for i in backlog[3:]:
+            multiply_attn_v(i)
+        multiply_attn_v(last - 2)
         quantise_attn(last - 1)
-        multiply_attn_v(last - 1)
         group_attn(last, 0, nc.scalar.copy)
-        group_attn(last, 1, nc.scalar.copy)
-        for key_pass in range(CHUNKS_PER_BATCH):
-            quantise_key_pass(last, key_pass)
+        group_attn(last, 1, nc.vector.tensor_copy)
+        for i in backlog[3:]:
+            store_out(i)
+        multiply_attn_v(last - 1)
+        quantise_key_pass(last, 0)
+        quantise_key_pass(last, 1)
         multiply_attn_v(last)
-        store_out(last - 1)
+        store_out(last - 2, nc.vector.tensor_copy)
+        store_out(last - 1, nc.vector.tensor_copy)
         store_out(last)

@@ -53,12 +53,9 @@ def tile_differentialattention_pa_kernel(
         stats = ctx.enter_context(tc.tile_pool(name="stats", bufs=4))
         psum = ctx.enter_context(tc.psum_pool(name="psum_banks", bufs=PSUM_BANKS))
 
-        lambda_q = keep.tile([P, 2, HD], BF16)
-        lambda_k = keep.tile([P, 2, HD], BF16)
-        nc.scalar.dma_start(out=lambda_q[:, 0, :], in_=lambda_q1.partition_broadcast(P))
-        nc.scalar.dma_start(out=lambda_k[:, 0, :], in_=lambda_k1.partition_broadcast(P))
-        nc.scalar.dma_start(out=lambda_q[:, 1, :], in_=lambda_q2.partition_broadcast(P))
-        nc.scalar.dma_start(out=lambda_k[:, 1, :], in_=lambda_k2.partition_broadcast(P))
+        lambdas = keep.tile([P, 2 * B, HD], BF16)
+        for j, vector in enumerate((lambda_q1, lambda_q2, lambda_k1, lambda_k2)):
+            nc.scalar.dma_start(out=lambdas[0:1, j, :], in_=vector.unsqueeze(0))
 
         def load_keys(b, g):
             nc.sync.dma_start(
@@ -122,18 +119,42 @@ def tile_differentialattention_pa_kernel(
         minus_lam = keep.tile([P, 1], F32)
 
         products = keep.tile([P, 2, HD], F32)
+        dots = keep.tile([P, 2], F32)
+        exps = keep.tile([P, 2], F32)
+        exp_sum = keep.tile([P, 1], F32)
+        lam_row = keep.tile([P, P], F32)
+        nc.gpsimd.memset(lam_row[:], 0.0)
 
         def multiply_lambdas():
-            nc.gpsimd.tensor_tensor(out=products[:], in0=lambda_q[:], in1=lambda_k[:], op=ALU.mult)
+            nc.vector.tensor_tensor(
+                out=products[0:1, :, :], in0=lambdas[0:1, 0:2, :], in1=lambdas[0:1, 2:4, :], op=ALU.mult
+            )
 
-        def compute_lam():
-            dots = keep.tile([P, 2], F32)
-            nc.vector.tensor_reduce(out=dots[:], in_=products[:], axis=AXIS.X, op=ALU.add)
-            exps = keep.tile([P, 2], F32)
-            exp_sum = keep.tile([P, 1], F32)
-            nc.scalar.activation(out=exps[:], in_=dots[:], func=ACT.Exp, accum_out=exp_sum[:])
-            nc.gpsimd.tensor_scalar(
-                out=minus_lam[:], in0=exp_sum[:], scalar1=-1.0, scalar2=-LAMBDA_INIT, op0=ALU.mult, op1=ALU.add
+        def add_products():
+            nc.vector.tensor_reduce(out=dots[0:1, :], in_=products[0:1, :, :], axis=AXIS.X, op=ALU.add)
+
+        def exponentiate_dots():
+            nc.scalar.activation(out=exps[0:1, :], in_=dots[0:1, :], func=ACT.Exp, accum_out=exp_sum[0:1, :])
+
+        def fill_lam_row():
+            nc.scalar.activation(
+                out=lam_row[0:1, :], in_=lam_row[0:1, :], func=ACT.Identity, bias=exp_sum[0:1, :], scale=1.0
+            )
+
+        lam_spread = {}
+
+        def spread_lam():
+            lam_spread[0] = psum.tile([P, P], F32, tag="bank", name="lam_bank")
+            nc.tensor.transpose(lam_spread[0][:], lam_row[:], ident_f32[:])
+
+        def finish_lam():
+            nc.vector.tensor_scalar(
+                out=minus_lam[:],
+                in0=lam_spread[0][:, 0:1],
+                scalar1=-1.0,
+                scalar2=-LAMBDA_INIT,
+                op0=ALU.mult,
+                op1=ALU.add,
             )
 
         wv_codes = keep.tile([P, D_PASSES, HD2], U32, align_bytes=64)
@@ -215,10 +236,10 @@ def tile_differentialattention_pa_kernel(
 
         v_grouped = {}
 
-        def group_v(g, half):
+        def group_v(g, half, copy=nc.vector.tensor_copy):
             if half == 0:
                 v_grouped[g] = work.tile([P, HD2, PACK], BF16, align_bytes=64, name="v_grouped")
-            nc.vector.tensor_copy(
+            copy(
                 out=v_grouped[g][:, half * HD : (half + 1) * HD, :],
                 in_=v_sums[g, half][:].rearrange("p t n -> p n t"),
             )
@@ -314,11 +335,14 @@ def tile_differentialattention_pa_kernel(
             expo = exponentials[i]
             inverse = inverses[i]
             scaler = nc.gpsimd if i < QUERY_TILES - DIFFERENCE_LAG else nc.vector
-            for half, factor in ((1, minus_lam[:, 0:1]), (0, 1.0)):
-                first = share if half == 0 else 0
+            for half, factor, columns in (
+                (1, minus_lam[:, 0:1], slice(0, CHUNK)),
+                (0, 1.0, slice(share, S)),
+                (1, minus_lam[:, 0:1], slice(CHUNK, S)),
+            ):
                 scaler.tensor_scalar(
-                    out=expo[:, half, first:],
-                    in0=expo[:, half, first:],
+                    out=expo[:, half, columns],
+                    in0=expo[:, half, columns],
                     scalar1=inverse[:, half : half + 1],
                     scalar2=factor,
                     op0=ALU.mult,
@@ -428,13 +452,17 @@ def tile_differentialattention_pa_kernel(
         second_chunk = range(PACK, 2 * PACK)
         all_tiles = range(TILES_PER_BATCH)
         keep_tokens(kT[0], 0, first_chunk, flip_tokens(k_rows[0], 0, first_chunk), nc.vector.tensor_copy)
+        multiply_lambdas()
         keep_tokens(qT[0], 0, range(2), flip_tokens(q_rows[0], 0, range(2)), nc.scalar.copy)
         keep_tokens(kT[0], 0, second_chunk, flip_tokens(k_rows[0], 0, second_chunk), nc.vector.tensor_copy)
+        add_products()
         keep_tokens(qT[0], 1, range(2), flip_tokens(q_rows[0], 1, range(2)), nc.scalar.copy)
         keep_tokens(kT[0], 1, first_chunk, flip_tokens(k_rows[0], 1, first_chunk), nc.scalar.copy)
+        exponentiate_dots()
         multiply_q_k(0, 0, 0)
         multiply_q_k(0, 0, 1)
         keep_tokens(kT[0], 1, second_chunk, flip_tokens(k_rows[0], 1, second_chunk), nc.scalar.copy)
+        fill_lam_row()
         multiply_q_k(0, 1, 0)
         multiply_q_k(0, 1, 1)
         x_half_step = [0 + tile * 4 // 3 for tile in range(X_TILES)]
@@ -463,7 +491,6 @@ def tile_differentialattention_pa_kernel(
         find_shift(0, 0)
         row_maximum(0, 1, 1)
         group_wv()
-        multiply_lambdas()
         last = QUERY_TILES - 1
         for step in range(QUERY_TILES):
             new_x = [[tile for tile in range(X_TILES) if x_half_step[tile] == 2 * step + half] for half in range(2)]
@@ -495,7 +522,7 @@ def tile_differentialattention_pa_kernel(
                 quantise_attn(step - QUANTISE_LAG)
                 quantised += 1
             if step == 1:
-                compute_lam()
+                finish_lam()
             if step < QUERY_TILES:
                 find_shift(step, 1)
             for tile in x_waiting[1:]:
@@ -509,7 +536,7 @@ def tile_differentialattention_pa_kernel(
             v_waiting = []
             if 0 <= step - SUMS_LAG < last - 1:
                 invert_row_sums(step - SUMS_LAG)
-                scale_halves(step - SUMS_LAG, 256 if step - SUMS_LAG < last - 1 else 0)
+                scale_halves(step - SUMS_LAG, (256 if step < 14 else 384))
             if in_psum:
                 group_v(*in_psum)
                 if in_psum[1] == 1:
@@ -560,11 +587,13 @@ def tile_differentialattention_pa_kernel(
                 group_attn(step - DIFFERENCE_LAG, 1, nc.scalar.copy)
             if flipped:
                 keep_tokens(flipped_sb, 1, tiles, flipped[1], nc.vector.tensor_copy if step < 2 else nc.scalar.copy)
-            if 0 <= step - SUMS_LAG < last - 1 and 0 <= step - SUMS_LAG:
-                scale_share(step - SUMS_LAG, 256)
+            if 0 <= step - SUMS_LAG < last - 1 and (256 if step < 14 else 384):
+                scale_share(step - SUMS_LAG, (256 if step < 14 else 384))
             for tile in new_x[1]:
                 group_x(tile, 0)
                 group_x(tile, 1)
+            if step == 0:
+                spread_lam()
             x_waiting = x_late + new_x[0]
             x_late = new_x[1]
         backlog = list(range(finished, last - 2))

@@ -81,12 +81,12 @@ def tile_differentialattention_pa_kernel(
         load_keys(0, 0)
         load_queries(0, slice(0, 2))
         load_keys(0, 1)
-        load_queries(0, slice(2, TILES_PER_BATCH))
         nc.sync.dma_start(
             out=wv_rows[:].rearrange("p c (u e) n -> p (c u) (e n)", e=2),
             in_=WV.rearrange("(s p e) n -> p s (e n)", p=P, e=2),
         )
         load_x(0, slice(0, 1))
+        load_queries(0, slice(2, TILES_PER_BATCH))
         load_x(0, slice(1, 2))
         load_x(0, slice(2, PACK))
         for g in range(CHUNKS_PER_BATCH):
@@ -114,6 +114,14 @@ def tile_differentialattention_pa_kernel(
             )
 
         kT = [keep.tile([P, 2, S], BF16, name="kT%d" % b) for b in range(B)]
+        zeros = keep.tile([P, BANK], BF16)
+        nc.vector.memset(zeros[:], 0.0)
+
+        def warm_up(passes):
+            idle = psum.tile([P, BANK], F32, tag="bank", name="idle_bank")
+            for spare in range(passes):
+                nc.tensor.matmul(idle[:], lhsT=zeros[:, 0:P], rhs=zeros[:], start=True, stop=True)
+
         qT = [keep.tile([P, 2, S], BF16, name="qT%d" % b) for b in range(B)]
 
         minus_lam = keep.tile([P, 1], F32)
@@ -451,6 +459,7 @@ def tile_differentialattention_pa_kernel(
         first_chunk = range(PACK)
         second_chunk = range(PACK, 2 * PACK)
         all_tiles = range(TILES_PER_BATCH)
+        warm_up(4)
         keep_tokens(kT[0], 0, first_chunk, flip_tokens(k_rows[0], 0, first_chunk), nc.vector.tensor_copy)
         multiply_lambdas()
         keep_tokens(qT[0], 0, range(2), flip_tokens(q_rows[0], 0, range(2)), nc.scalar.copy)

@@ -114,13 +114,13 @@ def tile_differentialattention_pa_kernel(
             )
 
         kT = [keep.tile([P, 2, S], BF16, name="kT%d" % b) for b in range(B)]
-        zeros = keep.tile([P, BANK], BF16)
+        zeros = keep.tile([P, P], BF16)
         nc.vector.memset(zeros[:], 0.0)
 
         def warm_up(passes):
-            idle = psum.tile([P, BANK], F32, tag="bank", name="idle_bank")
+            idle = psum.tile([P, P], F32, tag="bank", name="idle_bank")
             for spare in range(passes):
-                nc.tensor.matmul(idle[:], lhsT=zeros[:, 0:P], rhs=zeros[:], start=True, stop=True)
+                nc.tensor.matmul(idle[:], lhsT=zeros[:], rhs=zeros[:], start=True, stop=True)
 
         qT = [keep.tile([P, 2, S], BF16, name="qT%d" % b) for b in range(B)]
 
@@ -134,7 +134,7 @@ def tile_differentialattention_pa_kernel(
         nc.gpsimd.memset(lam_row[:], 0.0)
 
         def multiply_lambdas():
-            nc.vector.tensor_tensor(
+            nc.gpsimd.tensor_tensor(
                 out=products[0:1, :, :], in0=lambdas[0:1, 0:2, :], in1=lambdas[0:1, 2:4, :], op=ALU.mult
             )
 
@@ -459,19 +459,15 @@ def tile_differentialattention_pa_kernel(
         first_chunk = range(PACK)
         second_chunk = range(PACK, 2 * PACK)
         all_tiles = range(TILES_PER_BATCH)
-        warm_up(4)
+        warm_up(12)
         keep_tokens(kT[0], 0, first_chunk, flip_tokens(k_rows[0], 0, first_chunk), nc.vector.tensor_copy)
-        multiply_lambdas()
         keep_tokens(qT[0], 0, range(2), flip_tokens(q_rows[0], 0, range(2)), nc.scalar.copy)
         keep_tokens(kT[0], 0, second_chunk, flip_tokens(k_rows[0], 0, second_chunk), nc.vector.tensor_copy)
-        add_products()
         keep_tokens(qT[0], 1, range(2), flip_tokens(q_rows[0], 1, range(2)), nc.scalar.copy)
         keep_tokens(kT[0], 1, first_chunk, flip_tokens(k_rows[0], 1, first_chunk), nc.scalar.copy)
-        exponentiate_dots()
         multiply_q_k(0, 0, 0)
         multiply_q_k(0, 0, 1)
         keep_tokens(kT[0], 1, second_chunk, flip_tokens(k_rows[0], 1, second_chunk), nc.scalar.copy)
-        fill_lam_row()
         multiply_q_k(0, 1, 0)
         multiply_q_k(0, 1, 1)
         x_half_step = [0 + tile * 4 // 3 for tile in range(X_TILES)]
@@ -494,12 +490,14 @@ def tile_differentialattention_pa_kernel(
         flipped = []
         x_late = []
         v_waiting = []
+        multiply_lambdas()
+        group_wv()
         row_maximum(0, 0, 0)
         row_maximum(0, 0, 1)
         row_maximum(0, 1, 0)
         find_shift(0, 0)
         row_maximum(0, 1, 1)
-        group_wv()
+        add_products()
         last = QUERY_TILES - 1
         for step in range(QUERY_TILES):
             new_x = [[tile for tile in range(X_TILES) if x_half_step[tile] == 2 * step + half] for half in range(2)]
@@ -547,9 +545,12 @@ def tile_differentialattention_pa_kernel(
                 invert_row_sums(step - SUMS_LAG)
                 scale_halves(step - SUMS_LAG, (256 if step < 14 else 384))
             if in_psum:
-                group_v(*in_psum)
+                group_v(*in_psum, nc.scalar.copy if in_psum[0] == 3 else nc.vector.tensor_copy)
                 if in_psum[1] == 1:
                     v_waiting.append(in_psum[0])
+            if step == 0:
+                exponentiate_dots()
+                fill_lam_row()
             for i in multiplied:
                 store_out(i)
             multiplied = []
@@ -621,9 +622,9 @@ def tile_differentialattention_pa_kernel(
         group_attn(last - 2, 0, nc.vector.tensor_copy)
         for i in backlog[:2]:
             store_out(i)
-        for i in backlog[2:3]:
+        for i in backlog[2:4]:
             multiply_attn_v(i)
-        for i in backlog[2:3]:
+        for i in backlog[2:4]:
             store_out(i)
         for key_pass in range(CHUNKS_PER_BATCH):
             scale_half(last, 1, slice(key_pass * CHUNK, (key_pass + 1) * CHUNK))
@@ -631,13 +632,13 @@ def tile_differentialattention_pa_kernel(
         quantise_attn(last - 2)
         group_attn(last - 1, 1, nc.scalar.copy)
         group_attn(last - 1, 0, nc.vector.tensor_copy)
-        for i in backlog[3:]:
+        for i in backlog[4:]:
             multiply_attn_v(i)
         multiply_attn_v(last - 2)
         quantise_attn(last - 1)
         group_attn(last, 0, nc.scalar.copy)
         group_attn(last, 1, nc.vector.tensor_copy)
-        for i in backlog[3:]:
+        for i in backlog[4:]:
             store_out(i)
         multiply_attn_v(last - 1)
         quantise_key_pass(last, 0)

@@ -552,7 +552,7 @@ def tile_differentialattention_pa_kernel(
                 exponentiate_dots()
                 fill_lam_row()
             for i in multiplied:
-                store_out(i)
+                store_out(i, nc.vector.tensor_copy if step in (12, 13) else nc.scalar.copy)
             multiplied = []
             for tile in new_x[0]:
                 group_x(tile, 0)

import math
from contextlib import ExitStack

import concourse.mybir as mybir
from concourse.masks import make_identity

F32 = mybir.dt.float32
BF16 = mybir.dt.bfloat16
U32 = mybir.dt.uint32
U8 = mybir.dt.uint8
FP8X4 = mybir.dt.float8_e4m3fn_x4
ALU = mybir.AluOpType
ACT = mybir.ActivationFunctionType
AXIS = mybir.AxisListType

B, S, D, HD = 2, 1024, 2048, 128
HD2 = 2 * HD
DEPTH = 12
LAMBDA_INIT = 0.8 - 0.6 * math.exp(-0.3 * DEPTH)
SCALE = HD**-0.5

P = 128
PACK = 4
K_PASS = P * PACK
BANK = 512
CHUNK = K_PASS
CHUNKS_PER_BATCH = S // CHUNK
CHUNKS = B * CHUNKS_PER_BATCH
TILES_PER_BATCH = S // P
QUERY_TILES = B * TILES_PER_BATCH
X_TILES = CHUNKS * PACK
D_PASSES = D // K_PASS
KEY_BANKS = S // BANK

SUMS_LAG = 1
DIFFERENCE_LAG = 2
QUANTISE_LAG = 3
X_TILES_PER_STEP = 2
FINISHES_PER_STEP = 2
PSUM_BANKS = 8

FLOPS = 2 * B * S * D * HD2 + 2 * (2 * B * S * S * HD) + 2 * B * S * S * HD2


def tile_differentialattention_pa_kernel(
    tc, x, q, k, WV, lambda_q1, lambda_q2, lambda_k1, lambda_k2, out
):
    nc = tc.nc
    with ExitStack() as ctx:
        ctx.enter_context(tc.manual_schedule())
        keep = ctx.enter_context(tc.tile_pool(name="keep", bufs=1))
        work = ctx.enter_context(tc.tile_pool(name="work", bufs=3))
        stats = ctx.enter_context(tc.tile_pool(name="stats", bufs=4))
        psum = ctx.enter_context(tc.psum_pool(name="psum_banks", bufs=PSUM_BANKS))

        lambdas = keep.tile([P, 2 * B, HD], BF16)
        for j, vector in enumerate((lambda_q1, lambda_q2, lambda_k1, lambda_k2)):
            nc.scalar.dma_start(out=lambdas[0:1, j, :], in_=vector.unsqueeze(0))

        def load_keys(b, g):
            nc.sync.dma_start(
                out=k_rows[b][:, g * PACK : (g + 1) * PACK, :].rearrange("p t h -> p (t h)"),
                in_=k[b, g * CHUNK : (g + 1) * CHUNK, :].rearrange("(p t) h -> p (t h)", t=PACK),
            )

        def load_queries(b, tiles):
            nc.sync.dma_start(
                out=q_rows[b][:, tiles, :], in_=q[b].rearrange("(p s) h -> p s h", p=P)[:, tiles, :]
            )

        def load_x(g, tiles):
            columns = slice(tiles.start * D, tiles.stop * D)
            chunk = x_flat[g * CHUNK : (g + 1) * CHUNK, :].rearrange("(p t) d -> p (t d)", t=PACK)
            nc.sync.dma_start(out=x_rows[g][:, columns], in_=chunk[:, columns])

        x_flat = x.flatten_outer_dims()
        x_rows = [keep.tile([P, PACK * D], BF16, name="x_rows%d" % g) for g in range(CHUNKS)]
        wv_rows = keep.tile([P, D_PASSES, PACK, HD2], BF16)
        k_rows = [keep.tile([P, TILES_PER_BATCH, HD2], BF16, name="k_rows%d" % b) for b in range(B)]
        q_rows = [keep.tile([P, TILES_PER_BATCH, HD2], BF16, name="q_rows%d" % b) for b in range(B)]
        load_keys(0, 0)
        load_queries(0, slice(0, 2))
        load_keys(0, 1)
        nc.sync.dma_start(
            out=wv_rows[:].rearrange("p c (u e) n -> p (c u) (e n)", e=2),
            in_=WV.rearrange("(s p e) n -> p s (e n)", p=P, e=2),
        )
        load_x(0, slice(0, 1))
        load_queries(0, slice(2, TILES_PER_BATCH))
        load_x(0, slice(1, 2))
        load_x(0, slice(2, PACK))
        for g in range(CHUNKS_PER_BATCH):
            load_keys(1, g)
        load_queries(1, slice(0, TILES_PER_BATCH))
        for g in range(1, CHUNKS):
            for t in range(0, PACK, 2):
                load_x(g, slice(t, t + 2))

        ident_bf16 = keep.tile([P, P], BF16)
        make_identity(nc, ident_bf16[:])
        ident_f32 = keep.tile([P, P], F32)
        make_identity(nc, ident_f32[:])

        def flip_tokens(rows, half, tiles):
            flipped = psum.tile([P, len(tiles), P], BF16, tag="bank", name="flip_bank")
            for j, s in enumerate(tiles):
                nc.tensor.transpose(flipped[:, j, :], rows[:, s, half * HD : (half + 1) * HD], ident_bf16[:])
            return flipped

        def keep_tokens(flipped_sb, half, tiles, flipped, copy):
            copy(
                out=flipped_sb[:, half, tiles.start * P : tiles.stop * P],
                in_=flipped[:].rearrange("p s r -> p (s r)"),
            )

        kT = [keep.tile([P, 2, S], BF16, name="kT%d" % b) for b in range(B)]
        zeros = keep.tile([P, P], BF16)
        nc.vector.memset(zeros[:], 0.0)

        def warm_up(passes):
            idle = psum.tile([P, P], F32, tag="bank", name="idle_bank")
            for spare in range(passes):
                nc.tensor.matmul(idle[:], lhsT=zeros[:], rhs=zeros[:], start=True, stop=True)

        qT = [keep.tile([P, 2, S], BF16, name="qT%d" % b) for b in range(B)]

        minus_lam = keep.tile([P, 1], F32)

        products = keep.tile([P, 2, HD], F32)
        dots = keep.tile([P, 2], F32)
        exps = keep.tile([P, 2], F32)
        exp_sum = keep.tile([P, 1], F32)
        lam_row = keep.tile([P, P], F32)
        nc.gpsimd.memset(lam_row[:], 0.0)

        def multiply_lambdas():
            nc.gpsimd.tensor_tensor(
                out=products[0:1, :, :], in0=lambdas[0:1, 0:2, :], in1=lambdas[0:1, 2:4, :], op=ALU.mult
            )

        def add_products():
            nc.vector.tensor_reduce(out=dots[0:1, :], in_=products[0:1, :, :], axis=AXIS.X, op=ALU.add)

        def exponentiate_dots():
            nc.scalar.activation(out=exps[0:1, :], in_=dots[0:1, :], func=ACT.Exp, accum_out=exp_sum[0:1, :])

        def fill_lam_row():
            nc.scalar.activation(
                out=lam_row[0:1, :], in_=lam_row[0:1, :], func=ACT.Identity, bias=exp_sum[0:1, :], scale=1.0
            )

        lam_spread = {}

        def spread_lam():
            lam_spread[0] = psum.tile([P, P], F32, tag="bank", name="lam_bank")
            nc.tensor.transpose(lam_spread[0][:], lam_row[:], ident_f32[:])

        def finish_lam():
            nc.vector.tensor_scalar(
                out=minus_lam[:],
                in0=lam_spread[0][:, 0:1],
                scalar1=-1.0,
                scalar2=-LAMBDA_INIT,
                op0=ALU.mult,
                op1=ALU.add,
            )

        wv_codes = keep.tile([P, D_PASSES, HD2], U32, align_bytes=64)
        wv_scales = keep.tile([P, D_PASSES, HD2], U8, align_bytes=64)

        wv_grouped = keep.tile([P, D_PASSES, HD2, PACK], BF16, align_bytes=64)

        def group_wv():
            nc.gpsimd.tensor_scalar(
                out=wv_grouped[:],
                in0=wv_rows[:].rearrange("p c t n -> p c n t"),
                scalar1=1.0,
                scalar2=0.0,
                op0=ALU.mult,
                op1=ALU.add,
            )

        def quantise_wv():
            nc.vector.quantize_mx(
                out=wv_codes[:].rearrange("p c n -> p (c n)").bitcast(FP8X4),
                scales=wv_scales[:].rearrange("p c n -> p (c n)"),
                in_=wv_grouped[:].rearrange("p c n t -> p (c n t)"),
            )

        x_flipped = {}
        x_grouped = {}
        x_codes = {}
        x_scales = {}
        v_sums = {}
        v_codes = [keep.tile([P, HD2], U32, name="v_codes%d" % g, align_bytes=64) for g in range(CHUNKS)]
        v_scales = [keep.tile([P, HD2], U8, name="v_scales%d" % g, align_bytes=64) for g in range(CHUNKS)]

        def transpose_x(tile, pair):
            g, t = divmod(tile, PACK)
            words = x_rows[g][:].bitcast(F32)
            flipped = psum.tile([P, 2, 2, P], F32, tag="bank", name="x_bank")
            for c in range(2):
                for u in range(2):
                    first_word = t * (D // 2) + (2 * pair + c) * (K_PASS // 2) + u * P
                    nc.tensor.transpose(
                        flipped[:, c, u, :], words[:, first_word : first_word + P], ident_f32[:]
                    )
            x_flipped[tile, pair] = flipped

        def group_x(tile, pair, copy=nc.scalar.copy):
            if pair == 0:
                x_grouped[tile] = work.tile([P, D_PASSES * P * PACK], BF16, align_bytes=64, name="x_grouped")
            grouped_words = x_grouped[tile][:].bitcast(F32).rearrange("p (c r u) -> p c r u", c=D_PASSES, u=2)
            copy(
                out=grouped_words[:, 2 * pair : 2 * pair + 2, :, :],
                in_=x_flipped[tile, pair][:].rearrange("p c u r -> p c r u"),
            )

        def quantise_x(tile):
            g, t = divmod(tile, PACK)
            if t == 0:
                x_codes[g] = work.tile([P, PACK, D_PASSES * P], U32, align_bytes=64, bufs=2, name="x_codes")
                x_scales[g] = work.tile([P, PACK, D_PASSES * P], U8, align_bytes=64, bufs=2, name="x_scales")
            nc.vector.quantize_mx(
                out=x_codes[g][:, t, :].bitcast(FP8X4), scales=x_scales[g][:, t, :], in_=x_grouped[tile][:]
            )

        def project_tokens(g, half, tiles):
            if tiles.start == 0:
                v_sums[g, half] = psum.tile([P, PACK, HD], F32, tag="bank", name="v_bank")
            for t in tiles:
                for c in range(D_PASSES):
                    tokens = slice(c * P, (c + 1) * P)
                    columns = slice(half * HD, (half + 1) * HD)
                    nc.tensor.matmul_mx(
                        out=v_sums[g, half][:, t, :],
                        lhsT=x_codes[g][:, t, tokens].bitcast(FP8X4),
                        lhsT_scale=x_scales[g][:, t, tokens],
                        rhs=wv_codes[:, c, columns].bitcast(FP8X4),
                        rhs_scale=wv_scales[:, c, columns],
                        start=(c == 0),
                        stop=(c == D_PASSES - 1),
                    )

        v_grouped = {}

        def group_v(g, half, copy=nc.vector.tensor_copy):
            if half == 0:
                v_grouped[g] = work.tile([P, HD2, PACK], BF16, align_bytes=64, name="v_grouped")
            copy(
                out=v_grouped[g][:, half * HD : (half + 1) * HD, :],
                in_=v_sums[g, half][:].rearrange("p t n -> p n t"),
            )

        def quantise_v(g):
            nc.vector.quantize_mx(
                out=v_codes[g][:].bitcast(FP8X4),
                scales=v_scales[g][:],
                in_=v_grouped[g][:].rearrange("p n t -> p (n t)"),
            )

        scores = {}
        exponentials = {}
        exp_sums = {}
        attn_flipped = {}
        attn_grouped = {}
        out_sums = {}
        attn_codes = {}
        attn_scales = {}

        def multiply_q_k(i, half, key_bank):
            b, tile_in_batch = divmod(i, TILES_PER_BATCH)
            queries = slice(tile_in_batch * P, (tile_in_batch + 1) * P)
            bank = psum.tile([P, BANK], F32, tag="bank", name="scores_bank")
            nc.tensor.matmul(
                bank[:],
                lhsT=qT[b][:, half, queries],
                rhs=kT[b][:, half, key_bank * BANK : (key_bank + 1) * BANK],
                start=True,
                stop=True,
            )
            scores[i, half, key_bank] = bank

        peaks = {}

        def row_maximum(i, half, key_bank):
            if key_bank == 0:
                peaks[i, half] = stats.tile([P, KEY_BANKS], F32, name="peaks")
            nc.vector.tensor_reduce(
                out=peaks[i, half][:, key_bank : key_bank + 1],
                in_=scores[i, half, key_bank][:],
                axis=AXIS.X,
                op=ALU.max,
            )

        def exponentiate(i, half):
            if half == 0:
                exponentials[i] = work.tile([P, 2, S], F32, name="expo", bufs=5)
                exp_sums[i] = stats.tile([P, 2 * KEY_BANKS], F32, name="sums")
            for key_bank in range(KEY_BANKS):
                column = half * KEY_BANKS + key_bank
                nc.scalar.activation(
                    out=exponentials[i][:, half, key_bank * BANK : (key_bank + 1) * BANK],
                    in_=scores[i, half, key_bank][:],
                    func=ACT.Exp,
                    bias=shifts[i, half][:],
                    scale=SCALE,
                    accum_out=exp_sums[i][:, column : column + 1],
                )

        shifts = {}

        def find_shift(i, half):
            shift = stats.tile([P, 1], F32)
            shifts[i, half] = shift
            nc.vector.tensor_scalar(
                out=shift[:],
                in0=peaks[i, half][:, 0:1],
                scalar1=peaks[i, half][:, 1:2],
                scalar2=-SCALE,
                op0=ALU.max,
                op1=ALU.mult,
            )

        totals = {}

        def add_row_sums(i):
            totals[i] = stats.tile([P, 2], F32, name="totals")
            nc.vector.tensor_reduce(
                out=totals[i][:],
                in_=exp_sums[i][:].rearrange("p (h k) -> p h k", k=KEY_BANKS),
                axis=AXIS.X,
                op=ALU.add,
            )

        inverses = {}

        def invert_row_sums(i):
            inverses[i] = stats.tile([P, 2], F32, name="inverse")
            nc.vector.reciprocal(out=inverses[i][:], in_=totals[i][:])

        def scale_halves(i, share=0):
            expo = exponentials[i]
            inverse = inverses[i]
            scaler = nc.gpsimd if i < QUERY_TILES - DIFFERENCE_LAG else nc.vector
            for half, factor, columns in (
                (1, minus_lam[:, 0:1], slice(0, CHUNK)),
                (0, 1.0, slice(share, S)),
                (1, minus_lam[:, 0:1], slice(CHUNK, S)),
            ):
                scaler.tensor_scalar(
                    out=expo[:, half, columns],
                    in0=expo[:, half, columns],
                    scalar1=inverse[:, half : half + 1],
                    scalar2=factor,
                    op0=ALU.mult,
                    op1=ALU.mult,
                )

        def scale_share(i, share):
            nc.scalar.activation(
                out=exponentials[i][:, 0, 0:share],
                in_=exponentials[i][:, 0, 0:share],
                func=ACT.Copy,
                scale=inverses[i][:, 0:1],
            )

        def transpose_difference(i, key_passes):
            expo = exponentials[i]
            for key_pass in key_passes:
                attn_flipped[i, key_pass] = psum.tile([P, PACK, P], F32, tag="bank", name="attn_bank")
            for t in range(PACK):
                for half in range(2):
                    for key_pass in key_passes:
                        first_column = (key_pass * PACK + t) * P
                        nc.tensor.matmul(
                            attn_flipped[i, key_pass][:, t, :],
                            lhsT=expo[:, half, first_column : first_column + P],
                            rhs=ident_f32[:],
                            start=(half == 0),
                            stop=(half == 1),
                            is_transpose=True,
                        )

        def group_attn(i, key_pass, copy):
            if i not in attn_grouped:
                attn_grouped[i] = work.tile([P, CHUNKS_PER_BATCH, P, PACK], BF16, align_bytes=64, name="attn_grouped")
            copy(
                out=attn_grouped[i][:, key_pass, :, :],
                in_=attn_flipped[i, key_pass][:].rearrange("p t r -> p r t"),
            )

        last_totals = {}
        last_inverses = {}

        def add_half_sum(i, half):
            total = stats.tile([P, 1], F32, name="half_total")
            nc.vector.tensor_reduce(
                out=total[:], in_=exp_sums[i][:, half * KEY_BANKS : (half + 1) * KEY_BANKS], axis=AXIS.X, op=ALU.add
            )
            last_totals[half] = total

        def invert_half_sum(i, half):
            last_inverses[half] = stats.tile([P, 1], F32, name="half_inverse")
            nc.vector.reciprocal(out=last_inverses[half][:], in_=last_totals[half][:])

        def scale_half(i, half, columns):
            factor = minus_lam[:, 0:1] if half else 1.0
            nc.vector.tensor_scalar(
                out=exponentials[i][:, half, columns],
                in0=exponentials[i][:, half, columns],
                scalar1=last_inverses[half][:],
                scalar2=factor,
                op0=ALU.mult,
                op1=ALU.mult,
            )

        def quantise_key_pass(i, key_pass):
            if key_pass == 0:
                attn_codes[i] = work.tile([P, CHUNKS_PER_BATCH, P], U32, align_bytes=64, bufs=10, name="attn_codes")
                attn_scales[i] = work.tile([P, CHUNKS_PER_BATCH, P], U8, align_bytes=64, bufs=10, name="attn_scales")
            nc.vector.quantize_mx(
                out=attn_codes[i][:, key_pass, :].bitcast(FP8X4),
                scales=attn_scales[i][:, key_pass, :],
                in_=attn_grouped[i][:, key_pass, :, :].rearrange("p r t -> p (r t)"),
            )

        def quantise_attn(i):
            attn_codes[i] = work.tile([P, CHUNKS_PER_BATCH, P], U32, align_bytes=64, bufs=10, name="attn_codes")
            attn_scales[i] = work.tile([P, CHUNKS_PER_BATCH, P], U8, align_bytes=64, bufs=10, name="attn_scales")
            nc.vector.quantize_mx(
                out=attn_codes[i][:].rearrange("p k r -> p (k r)").bitcast(FP8X4),
                scales=attn_scales[i][:].rearrange("p k r -> p (k r)"),
                in_=attn_grouped[i][:].rearrange("p k r t -> p (k r t)"),
            )

        def multiply_attn_v(i):
            b = i // TILES_PER_BATCH
            sums = psum.tile([P, HD2], F32, tag="bank")
            for key_pass in range(CHUNKS_PER_BATCH):
                g = b * CHUNKS_PER_BATCH + key_pass
                nc.tensor.matmul_mx(
                    out=sums[:],
                    lhsT=attn_codes[i][:, key_pass, :].bitcast(FP8X4),
                    lhsT_scale=attn_scales[i][:, key_pass, :],
                    rhs=v_codes[g][:].bitcast(FP8X4),
                    rhs_scale=v_scales[g][:],
                    start=(key_pass == 0),
                    stop=(key_pass == CHUNKS_PER_BATCH - 1),
                )
            out_sums[i] = sums

        def store_out(i, copy=nc.scalar.copy):
            b, tile_in_batch = divmod(i, TILES_PER_BATCH)
            out_rows = work.tile([P, HD2], F32, bufs=6)
            copy(out=out_rows[:], in_=out_sums[i][:])
            nc.sync.dma_start(out=out[b].rearrange("(p s) n -> s p n", p=P)[tile_in_batch], in_=out_rows[:])

        first_chunk = range(PACK)
        second_chunk = range(PACK, 2 * PACK)
        all_tiles = range(TILES_PER_BATCH)
        warm_up(12)
        keep_tokens(kT[0], 0, first_chunk, flip_tokens(k_rows[0], 0, first_chunk), nc.vector.tensor_copy)
        keep_tokens(qT[0], 0, range(2), flip_tokens(q_rows[0], 0, range(2)), nc.scalar.copy)
        keep_tokens(kT[0], 0, second_chunk, flip_tokens(k_rows[0], 0, second_chunk), nc.vector.tensor_copy)
        keep_tokens(qT[0], 1, range(2), flip_tokens(q_rows[0], 1, range(2)), nc.scalar.copy)
        keep_tokens(kT[0], 1, first_chunk, flip_tokens(k_rows[0], 1, first_chunk), nc.scalar.copy)
        multiply_q_k(0, 0, 0)
        multiply_q_k(0, 0, 1)
        keep_tokens(kT[0], 1, second_chunk, flip_tokens(k_rows[0], 1, second_chunk), nc.scalar.copy)
        multiply_q_k(0, 1, 0)
        multiply_q_k(0, 1, 1)
        x_half_step = [0 + tile * 4 // 3 for tile in range(X_TILES)]
        projections = {}
        for g in range(CHUNKS):
            quantised_in = (x_half_step[PACK * g + PACK - 1] + 1) // 2 + 1
            projections[2 * quantised_in + 1] = (g, 0)
            projections[2 * quantised_in + 3] = (g, 1)
        finished = 0
        quantised = 0
        chunks_ready = 0
        in_psum = None
        multiplied = []
        x_waiting = []
        later_tiles = {
            0: (q_rows[0], qT[0], range(2, TILES_PER_BATCH)),
            1: (k_rows[1], kT[1], all_tiles),
            2: (q_rows[1], qT[1], all_tiles),
        }
        flipped = []
        x_late = []
        v_waiting = []
        multiply_lambdas()
        group_wv()
        row_maximum(0, 0, 0)
        row_maximum(0, 0, 1)
        row_maximum(0, 1, 0)
        find_shift(0, 0)
        row_maximum(0, 1, 1)
        add_products()
        last = QUERY_TILES - 1
        for step in range(QUERY_TILES):
            new_x = [[tile for tile in range(X_TILES) if x_half_step[tile] == 2 * step + half] for half in range(2)]
            for tile in new_x[0]:
                transpose_x(tile, 0)
            for tile in new_x[0]:
                transpose_x(tile, 1)
            if step < last:
                multiply_q_k(step + 1, 0, 0)
            if step < last:
                multiply_q_k(step + 1, 0, 1)
            if 0 <= step - DIFFERENCE_LAG:
                transpose_difference(step - DIFFERENCE_LAG, range(0, 1))
            if 0 <= step - DIFFERENCE_LAG:
                transpose_difference(step - DIFFERENCE_LAG, range(1, 2))
            if 0 < step < QUERY_TILES:
                row_maximum(step, 1, 0)
            if 0 <= step - SUMS_LAG < QUERY_TILES:
                add_row_sums(step - SUMS_LAG)
            if 0 < step < QUERY_TILES:
                row_maximum(step, 1, 1)
            if step < QUERY_TILES:
                exponentiate(step, 0)
            if step == 3:
                quantise_wv()
            if x_waiting:
                quantise_x(x_waiting[0])
            elif 0 <= step - QUANTISE_LAG < QUERY_TILES:
                quantise_attn(step - QUANTISE_LAG)
                quantised += 1
            if step == 1:
                finish_lam()
            if step < QUERY_TILES:
                find_shift(step, 1)
            for tile in x_waiting[1:]:
                quantise_x(tile)
            if x_waiting and 0 <= step - QUANTISE_LAG < QUERY_TILES:
                quantise_attn(step - QUANTISE_LAG)
                quantised += 1
            for g in v_waiting:
                quantise_v(g)
                chunks_ready += 1
            v_waiting = []
            if 0 <= step - SUMS_LAG < last - 1:
                invert_row_sums(step - SUMS_LAG)
                scale_halves(step - SUMS_LAG, (256 if step < 14 else 384))
            if in_psum:
                group_v(*in_psum, nc.scalar.copy if in_psum[0] == 3 else nc.vector.tensor_copy)
                if in_psum[1] == 1:
                    v_waiting.append(in_psum[0])
            if step == 0:
                exponentiate_dots()
                fill_lam_row()
            for i in multiplied:
                store_out(i, nc.vector.tensor_copy if step in (12, 13) else nc.scalar.copy)
            multiplied = []
            for tile in new_x[0]:
                group_x(tile, 0)
                group_x(tile, 1, nc.vector.tensor_copy if step < 2 else nc.scalar.copy)
            if step == last:
                break
            flipped = []
            if step in later_tiles:
                rows, flipped_sb, tiles = later_tiles[step]
                flipped = [flip_tokens(rows, half, tiles) for half in range(2)]
            in_psum = projections.get(2 * step + 1)
            if step < last:
                multiply_q_k(step + 1, 1, 0)
            for tile in new_x[1]:
                transpose_x(tile, 0)
            for tile in new_x[1]:
                transpose_x(tile, 1)
            if step < last:
                multiply_q_k(step + 1, 1, 1)
            for turn in range(1 if step < last - 1 else FINISHES_PER_STEP):
                chunks_needed = (finished // TILES_PER_BATCH + 1) * CHUNKS_PER_BATCH
                if finished < quantised and chunks_ready >= chunks_needed:
                    multiply_attn_v(finished)
                    multiplied.append(finished)
                    finished += 1
            if in_psum:
                project_tokens(*in_psum, range(0, 2))
            if in_psum:
                project_tokens(*in_psum, range(2, 4))
            if step + 1 < QUERY_TILES:
                row_maximum(step + 1, 0, 0)
                row_maximum(step + 1, 0, 1)
            if 0 <= step - DIFFERENCE_LAG < QUERY_TILES:
                group_attn(step - DIFFERENCE_LAG, 0, nc.vector.tensor_copy)
            if flipped:
                keep_tokens(flipped_sb, 0, tiles, flipped[0], nc.vector.tensor_copy)
            if step + 1 < QUERY_TILES:
                find_shift(step + 1, 0)
            if step < QUERY_TILES:
                exponentiate(step, 1)
            if 0 <= step - DIFFERENCE_LAG < QUERY_TILES:
                group_attn(step - DIFFERENCE_LAG, 1, nc.scalar.copy)
            if flipped:
                keep_tokens(flipped_sb, 1, tiles, flipped[1], nc.vector.tensor_copy if step < 2 else nc.scalar.copy)
            if 0 <= step - SUMS_LAG < last - 1 and (256 if step < 14 else 384):
                scale_share(step - SUMS_LAG, (256 if step < 14 else 384))
            for tile in new_x[1]:
                group_x(tile, 0)
                group_x(tile, 1)
            if step == 0:
                spread_lam()
            x_waiting = x_late + new_x[0]
            x_late = new_x[1]
        backlog = list(range(finished, last - 2))
        invert_row_sums(last - 1)
        exponentiate(last, 1)
        add_half_sum(last, 0)
        scale_halves(last - 1)
        for i in backlog[:2]:
            multiply_attn_v(i)
        invert_half_sum(last, 0)
        transpose_difference(last - 1, range(CHUNKS_PER_BATCH))
        add_half_sum(last, 1)
        scale_half(last, 0, slice(0, S))
        invert_half_sum(last, 1)
        group_attn(last - 2, 1, nc.scalar.copy)
        group_attn(last - 2, 0, nc.vector.tensor_copy)
        for i in backlog[:2]:
            store_out(i)
        for i in backlog[2:4]:
            multiply_attn_v(i)
        for i in backlog[2:4]:
            store_out(i)
        for key_pass in range(CHUNKS_PER_BATCH):
            scale_half(last, 1, slice(key_pass * CHUNK, (key_pass + 1) * CHUNK))
            transpose_difference(last, range(key_pass, key_pass + 1))
        quantise_attn(last - 2)
        group_attn(last - 1, 1, nc.scalar.copy)
        group_attn(last - 1, 0, nc.vector.tensor_copy)
        for i in backlog[4:]:
            multiply_attn_v(i)
        multiply_attn_v(last - 2)
        quantise_attn(last - 1)
        group_attn(last, 0, nc.scalar.copy)
        group_attn(last, 1, nc.vector.tensor_copy)
        for i in backlog[4:]:
            store_out(i)
        multiply_attn_v(last - 1)
        quantise_key_pass(last, 0)
        quantise_key_pass(last, 1)
        multiply_attn_v(last)
        store_out(last - 2, nc.vector.tensor_copy)
        store_out(last - 1, nc.vector.tensor_copy)
        store_out(last)
